import numpy as np
import ml_dtypes


def mxq(x, axis, fmt="e4m3"):
    dtype, down = {"e4m3": (ml_dtypes.float8_e4m3fn, 7), "e5m2": (ml_dtypes.float8_e5m2, 14)}[fmt]
    v = np.moveaxis(np.asarray(x, np.float32).astype(ml_dtypes.bfloat16).astype(np.float64), axis, -1)
    blocks = v.reshape(v.shape[:-1] + (-1, 32))
    amax = np.abs(blocks).max(-1, keepdims=True)
    byte = np.maximum(np.where(amax > 0, np.frexp(amax)[1] - 1 + 127, 0) - down, 1)
    scale = np.exp2(byte - 127.0)
    codes = (blocks / scale).astype(np.float32).astype(dtype).astype(np.float64)
    return np.moveaxis((codes * scale).reshape(v.shape), -1, axis)


WIDE = False


def mx_kscale(k):
    if not WIDE:
        return np.ones(k)
    levels = np.array([10, -10, 5, -5, 0])
    if k % 512:
        return np.exp2(np.random.permutation(np.resize(levels, k // 32))).repeat(32)
    a = np.empty((k // 512, 16))
    for p in range(k // 512):
        a[p, :8] = np.random.permutation(np.resize(levels, 8))
        for g in range(8):
            far = levels[np.abs(levels - a[p, g]) >= 10]
            a[p, g + 8] = far[np.random.randint(len(far))]
    return np.exp2(a.ravel()).repeat(32)


BF16 = ml_dtypes.bfloat16


def bf(x):
    return np.asarray(x, np.float32).astype(BF16)


def f64(x):
    return np.asarray(x).astype(np.float64)


E2M1 = np.array([0.0, 0.5, 1.0, 1.5, 2.0, 3.0, 4.0, 6.0, -0.0, -0.5, -1.0, -1.5, -2.0, -3.0, -4.0, -6.0])


def pack_weight(w, fmt):
    k, n = w.shape
    w = f64(bf(w)).reshape(k // 32, 32, n)
    amax = np.abs(w).max(1)
    if fmt == "e4m3":
        byte = np.frexp(amax)[1] - 1 + 127 - 7
    else:
        mant, ex = np.frexp(amax / 6.0)
        byte = np.where(mant > 0.5, ex, ex - 1) + 127
    byte = np.clip(np.where(amax > 0, byte, 1), 1, 254)
    scaled = (w * np.exp2(127.0 - byte)[:, None, :]).reshape(k, n).astype(np.float32)
    by_word = np.ascontiguousarray(scaled.reshape(k // 512, 128, 4, n).transpose(0, 1, 3, 2))
    if fmt == "e4m3":
        words = by_word.astype(ml_dtypes.float8_e4m3fn).view(np.uint8)
    else:
        c = by_word.astype(ml_dtypes.float4_e2m1fn).view(np.uint8) & 0xF
        words = c[..., 0::2] | (c[..., 1::2] << 4)
    return np.ascontiguousarray(words), np.ascontiguousarray(byte.astype(np.uint8).reshape(k // 512, 16, n))


def unpack_weight(words, scales, fmt):
    g, p, n, _ = words.shape
    if fmt == "e4m3":
        vals = np.ascontiguousarray(words).view(ml_dtypes.float8_e4m3fn).astype(np.float64)
    else:
        nib = np.empty((g, p, n, 4), np.uint8)
        nib[..., 0::2] = words & 0xF
        nib[..., 1::2] = words >> 4
        vals = E2M1[nib]
    vals = vals * np.repeat(np.exp2(scales.astype(np.float64) - 127.0), 8, axis=1)[..., None]
    return vals.transpose(0, 1, 3, 2).reshape(g * 512, n)
def pack4(w):
    words, scales = pack_weight(w, "e2m1")
    return words.reshape(words.shape[0], 128, -1), scales


def unpack4(words, scales):
    return unpack_weight(words.reshape(words.shape[0], 128, -1, 2), scales, "e2m1")


B, S, NS, DS, H = 4, 1024, 4, 128, 512
D = NS * DS


def draw0():
    t, u = mx_kscale(H), mx_kscale(D)
    hid = bf(0.6 * np.random.standard_normal((B, S, NS, H)) * t)
    Wd = bf(1.5 * np.random.standard_normal((NS, H, DS)) / np.sqrt(H) / t[None, :, None] * u.reshape(NS, 1, DS))
    words, scales = pack4(np.random.standard_normal((D, D)) / np.sqrt(D) / u[:, None])
    return {"hid": hid,
            "Wd": Wd,
            "Wo_words": words,
            "Wo_scales": scales,
            "x": bf(np.random.standard_normal((B, S, D)))}


def core(hid, Wd, Wo_words, Wo_scales, x):
    hq = mxq(f64(hid).transpose(0, 2, 1, 3), 3, "e4m3")
    down = hq @ mxq(f64(Wd), 1, "e4m3")
    joined = down.transpose(0, 2, 1, 3).reshape(B, S, D)
    return (mxq(joined, 2, "e4m3") @ unpack4(Wo_words, Wo_scales)) + f64(x)


def e4m3fn_bytes(y):
    return np.clip(np.asarray(y, np.float64), -448.0, 448.0).astype(np.float32).astype(ml_dtypes.float8_e4m3fn).view(np.uint8)


def e4m3fn_values(b):
    return np.asarray(b, np.uint8).view(ml_dtypes.float8_e4m3fn).astype(np.float64)


def setup_inputs():
    d = draw0()
    x0 = np.asarray(d['hid']).astype(np.float64)
    s = (np.max(np.abs(x0), axis=(0, 1, 2), keepdims=True) / 448.0).astype(np.float32)
    out = {}
    for k, v in d.items():
        if k == 'hid':
            out['hid_bytes'] = e4m3fn_bytes(x0 / s.astype(np.float64))
            out['hid_scale'] = s
        else:
            out[k] = v
    return out


def reference(hid_bytes, hid_scale, Wd, Wo_words, Wo_scales, x):
    return core(e4m3fn_values(hid_bytes) * hid_scale.astype(np.float64), Wd, Wo_words, Wo_scales, x)

@@ -1,0 +1,241 @@
+import concourse.mybir as mybir
+from concourse.masks import make_identity
+from contextlib import ExitStack
+
+F32 = mybir.dt.float32
+BF16 = mybir.dt.bfloat16
+U32 = mybir.dt.uint32
+I32 = mybir.dt.int32
+U8 = mybir.dt.uint8
+F8 = mybir.dt.float8_e4m3fn
+F8X4 = mybir.dt.float8_e4m3fn_x4
+F4X4 = mybir.dt.float4_e2m1fn_x4
+MULT = mybir.AluOpType.mult
+ADD = mybir.AluOpType.add
+
+P = 128
+TOKENS = 4096
+NS = 4
+H = 512
+DS = 128
+D = NS * DS
+TILES = TOKENS // P
+PAIRS = TILES // 2
+FLOPS = 2 * TOKENS * NS * H * DS + 2 * TOKENS * D * D
+
+
+def tile_mopn_layer_pb_t_w4_kernel(tc, hid_bytes, hid_scale, Wd, Wo_words, Wo_scales, x, out):
+    nc = tc.nc
+    hid = hid_bytes.rearrange("b s n k -> (b s) (n k)").rearrange("(j p i) c -> j p (i c)", p=P, i=2)
+    xin = x.rearrange("b s d -> (b s) d").rearrange("(j p i) c -> j p (i c)", p=P, i=2)
+    oview = out.rearrange("b s d -> (b s) d").rearrange("(j p i) c -> j p (i c)", p=P, i=2)
+    srow = hid_scale.rearrange("a b c k -> (a b c k)")
+
+    with ExitStack() as ctx:
+        keep = ctx.enter_context(tc.tile_pool(name="keep", bufs=1))
+        loads = ctx.enter_context(tc.tile_pool(name="loads", bufs=8))
+        sb = ctx.enter_context(tc.tile_pool(name="sb", bufs=4))
+        pst = ctx.enter_context(tc.psum_pool(name="pst", bufs=2))
+
+        ctx.enter_context(tc.manual_schedule())
+
+        scale = keep.tile([P, NS * H], F32, align_bytes=64)
+        scale_p = keep.tile([P, 4], F32, align_bytes=64)
+        ident = keep.tile([P, P], F32, align_bytes=64)
+        ident_b = keep.tile([P, P], BF16, align_bytes=64)
+        w_raw = keep.tile([P, NS, 4, DS], BF16, align_bytes=64)
+        w_grp = keep.tile([P, 4, NS, 32, 4], BF16, align_bytes=64)
+        w_codes = keep.tile([P, 4, NS, 32], U32, align_bytes=64)
+        w_scales = keep.tile([P, 4 * P], U8, align_bytes=64)
+        wz_codes = keep.tile([P, 4, 640], U32, align_bytes=64)
+        wo_words = keep.tile([P, 2 * D], U8, align_bytes=64)
+        wo_scales = keep.tile([P, D], U8, align_bytes=64)
+
+        hbs = {}
+        xts = {}
+
+        def load_hid(j, halves=1):
+            hb = loads.tile([P, 4096], U8, align_bytes=64)
+            w = 4096 // halves
+            for h in range(halves):
+                nc.sync.dma_start(out=hb[:, h * w : (h + 1) * w], in_=hid[j][:, h * w : (h + 1) * w])
+            hbs[j] = hb
+
+        def load_x(j):
+            xt = loads.tile([P, 2 * D], BF16, align_bytes=64)
+            nc.sync.dma_start(out=xt[:], in_=xin[j])
+            xts[j] = xt
+
+        nc.sync.dma_start(out=scale_p[:], in_=srow.rearrange("(p t) -> p t", t=4))
+        load_hid(0, 2)
+        nc.sync.dma_start(out=w_raw[:].rearrange("p n j d -> p n (j d)"), in_=Wd.rearrange("n (p j) d -> p n (j d)", j=4))
+        nc.gpsimd.memset(wo_scales[:].bitcast(I32), 0)
+        make_identity(nc, ident[:])
+        make_identity(nc, ident_b[:])
+        nc.gpsimd.memset(wz_codes[:].rearrange("p t z -> p (t z)").bitcast(I32), 0)
+        load_hid(1)
+        nc.sync.dma_start(out=wo_words[:], in_=Wo_words[0])
+        wos = Wo_scales[0].bitcast(I32)
+        for q in range(4):
+            nc.sync.dma_start(out=wo_scales[32 * q : 32 * q + 4, :].bitcast(I32), in_=wos[4 * q : 4 * q + 4, :])
+        load_x(0)
+        for j in range(2, 5):
+            load_hid(j)
+            load_x(j - 1)
+
+        spread = pst.tile([P, 4, P], F32, name="po")
+        for t in range(4):
+            nc.tensor.transpose(spread[:, t, :], scale_p[:, t : t + 1].to_broadcast([P, P]), ident[:])
+        nc.vector.tensor_copy(out=scale[:, 0:H].rearrange("p (m t) -> p m t", t=4), in_=spread[:].rearrange("p t m -> p m t"))
+        for n in range(1, NS):
+            nc.scalar.copy(out=scale[:, n * H : (n + 1) * H], in_=scale[:, 0:H])
+        for n in range(NS):
+            nc.scalar.copy(out=w_grp[:, :, n], in_=w_raw[:, n].rearrange("p j (m t) -> p t m j", t=4))
+
+        def prepare_w():
+            nc.vector.quantize_mx(
+                out=w_codes[:].rearrange("p t n m -> p (t n m)").bitcast(F8X4),
+                scales=w_scales[:],
+                in_=w_grp[:].rearrange("p t n m j -> p (t n m j)"),
+            )
+            nc.vector.tensor_copy(
+                out=wz_codes[:].rearrange("p t (n z) -> p t n z", z=160)[:, :, :, 0:32].bitcast(I32), in_=w_codes[:].bitcast(I32)
+            )
+
+        xs_t, xt_t, g_t, c_t, s_t, jp_t, jg_t, jc_t, js_t, po_t, o_t = ({} for z in range(11))
+
+        ws_t = {}
+
+        def on_scalar(i):
+            return 2 <= i < TILES - 2 and i % 3 != 1
+
+        def widen_s(i):
+            if not on_scalar(i):
+                return
+            ws = sb.tile([P, H], BF16, align_bytes=64)
+            base = (i % 2) * NS * H + 3 * H
+            nc.scalar.copy(out=ws[:], in_=hbs[i // 2][:, base : base + H].bitcast(F8))
+            ws_t[i] = ws
+
+        def widen(i):
+            xs = sb.tile([P, NS * H], BF16, align_bytes=64)
+            base = (i % 2) * NS * H
+            hb = hbs[i // 2]
+            w = 512 if i == 0 else 1024 if i == TILES - 1 else 1536 if on_scalar(i) else 2048
+            for c in range(0, 3 * H if on_scalar(i) else 4 * H, w):
+                nc.vector.tensor_tensor(
+                    out=xs[:, c : c + w],
+                    in0=hb[:, base + c : base + c + w].bitcast(F8),
+                    in1=scale[:, 0:w],
+                    op=MULT,
+                )
+            xs_t[i] = xs
+
+        def turn(i):
+            words = xs_t[i][:].bitcast(F32)
+            banks = []
+            for h in range(2):
+                xt = pst.tile([P, 2, 2, P], F32, name="xt%d" % h)
+                for a in range(2):
+                    n = 2 * h + a
+                    if n == 3 and on_scalar(i):
+                        planes = xt[:, a].rearrange("p u r -> p (u r)").bitcast(BF16)
+                        for t in range(4):
+                            nc.tensor.transpose(planes[:, P * t : P * (t + 1)], ws_t[i][:, t::4], ident_b[:])
+                        continue
+                    for u in range(2):
+                        nc.tensor.transpose(xt[:, a, u, :], words[:, 256 * n + u : 256 * (n + 1) : 2], ident[:])
+                banks.append(xt)
+            xt_t[i] = banks
+
+        def empty(i):
+            g = sb.tile([P, 2048], BF16, align_bytes=64)
+            for h in range(2):
+                if h == 1 and on_scalar(i):
+                    nc.scalar.copy(
+                        out=g[:, 1024:1536].bitcast(F32).rearrange("p (r u) -> p r u", u=2),
+                        in_=xt_t[i][1][:, 0].rearrange("p u r -> p r u"),
+                    )
+                    planes = xt_t[i][1][:, 1].rearrange("p u r -> p (u r)").bitcast(BF16)
+                    dst = g[:, 1536:2048].rearrange("p (r t) -> p r t", t=4)
+                    for t in range(4):
+                        nc.scalar.activation(
+                            out=dst[:, :, t],
+                            in_=planes[:, P * t : P * (t + 1)],
+                            func=mybir.ActivationFunctionType.Copy,
+                            scale=scale_p[:, t : t + 1],
+                        )
+                    continue
+                nc.scalar.copy(
+                    out=g[:, 1024 * h : 1024 * (h + 1)].bitcast(F32).rearrange("p (a r u) -> p a r u", a=2, u=2),
+                    in_=xt_t[i][h][:].rearrange("p a u r -> p a r u"),
+                )
+            g_t[i] = g
+
+        def quant(i):
+            c = sb.tile([P, 512], U32, name="codes", align_bytes=64)
+            s = sb.tile([P, 512], U8, name="scales", align_bytes=64)
+            nc.vector.quantize_mx(out=c[:].bitcast(F8X4), scales=s[:], in_=g_t[i][:])
+            c_t[i], s_t[i] = c, s
+
+        def mm1(i):
+            jp = pst.tile([P, 4, P], F32, name="jp")
+            for t in range(4):
+                for n in range(NS):
+                    nc.tensor.matmul_mx(
+                        out=jp[:, t, :],
+                        lhsT=wz_codes[:, t, P * n : P * (n + 1)].bitcast(F8X4),
+                        lhsT_scale=w_scales[:, P * t : P * (t + 1)],
+                        rhs=c_t[i][:, P * n : P * (n + 1)].bitcast(F8X4),
+                        rhs_scale=s_t[i][:, P * n : P * (n + 1)],
+                        start=(n == 0),
+                        stop=(n == NS - 1),
+                    )
+            jp_t[i] = jp
+
+        def empty_j(i):
+            jg = sb.tile([P, P, 4], BF16, name="jg", align_bytes=64)
+            nc.scalar.copy(out=jg[:], in_=jp_t[i][:].rearrange("p t r -> p r t"))
+            jg_t[i] = jg
+
+        def quant_j(i):
+            c = sb.tile([P, P], U32, name="jcodes", align_bytes=64)
+            s = sb.tile([P, P], U8, name="jscales", align_bytes=64)
+            nc.vector.quantize_mx(out=c[:].bitcast(F8X4), scales=s[:], in_=jg_t[i][:].rearrange("p r t -> p (r t)"))
+            jc_t[i], js_t[i] = c, s
+
+        def mm2(i):
+            po = pst.tile([P, D], F32, name="po")
+            nc.tensor.matmul_mx(
+                out=po[:],
+                lhsT=jc_t[i][:].bitcast(F8X4),
+                lhsT_scale=js_t[i][:],
+                rhs=wo_words[:].bitcast(F4X4),
+                rhs_scale=wo_scales[:],
+                start=True,
+                stop=True,
+            )
+            po_t[i] = po
+
+        def add(i):
+            if i % 2 == 0:
+                o_t[i // 2] = sb.tile([P, 2 * D], F32, name="o", align_bytes=64)
+            o = o_t[i // 2]
+            cols = slice((i % 2) * D, (i % 2 + 1) * D)
+            nc.vector.tensor_tensor(out=o[:, cols], in0=po_t[i][:], in1=xts[i // 2][:, cols], op=ADD)
+            if i >= TILES - 2:
+                nc.sync.dma_start(out=oview[i // 2][:, cols], in_=o[:, cols])
+            elif i % 2 == 1:
+                nc.sync.dma_start(out=oview[i // 2], in_=o[:])
+
+        STAGES = [(empty_j, 3), (widen_s, -1), (widen, 0), (add, 6), (quant, 2), (quant_j, 4), (turn, 0), (empty, 0), (mm1, 2), (mm2, 4)]
+        for i in range(-1, TILES + 6):
+            if i % 2 == 0 and i // 2 + 5 < PAIRS and i >= 0:
+                load_hid(i // 2 + 5)
+            if i % 2 == 0 and i // 2 + 4 < PAIRS and i >= 0:
+                load_x(i // 2 + 4)
+            for stage, lag in STAGES:
+                if 0 <= i - lag < TILES:
+                    stage(i - lag)
+            if i == 1:
+                prepare_w()

@@ -12,6 +12,7 @@ F8X4 = mybir.dt.float8_e4m3fn_x4
 F4X4 = mybir.dt.float4_e2m1fn_x4
 MULT = mybir.AluOpType.mult
 ADD = mybir.AluOpType.add
+COPY = mybir.ActivationFunctionType.Copy
 
 P = 128
 TOKENS = 4096
@@ -19,6 +20,7 @@ NS = 4
 H = 512
 DS = 128
 D = NS * DS
+HALF = 2 * H
 TILES = TOKENS // P
 PAIRS = TILES // 2
 FLOPS = 2 * TOKENS * NS * H * DS + 2 * TOKENS * D * D
@@ -34,15 +36,14 @@ def tile_mopn_layer_pb_t_w4_kernel(tc, hid_bytes, hid_scale, Wd, Wo_words, Wo_sc
     with ExitStack() as ctx:
         keep = ctx.enter_context(tc.tile_pool(name="keep", bufs=1))
         loads = ctx.enter_context(tc.tile_pool(name="loads", bufs=8))
-        sb = ctx.enter_context(tc.tile_pool(name="sb", bufs=4))
+        sb = ctx.enter_context(tc.tile_pool(name="sb", bufs=5))
         pst = ctx.enter_context(tc.psum_pool(name="pst", bufs=2))
 
         ctx.enter_context(tc.manual_schedule())
 
-        scale = keep.tile([P, NS * H], F32, align_bytes=64)
+        scale = keep.tile([P, HALF], F32, align_bytes=64)
         scale_p = keep.tile([P, 4], F32, align_bytes=64)
         ident = keep.tile([P, P], F32, align_bytes=64)
-        ident_b = keep.tile([P, P], BF16, align_bytes=64)
         w_raw = keep.tile([P, NS, 4, DS], BF16, align_bytes=64)
         w_grp = keep.tile([P, 4, NS, 32, 4], BF16, align_bytes=64)
         w_codes = keep.tile([P, 4, NS, 32], U32, align_bytes=64)
@@ -69,9 +70,8 @@ def tile_mopn_layer_pb_t_w4_kernel(tc, hid_bytes, hid_scale, Wd, Wo_words, Wo_sc
         nc.sync.dma_start(out=scale_p[:], in_=srow.rearrange("(p t) -> p t", t=4))
         load_hid(0, 2)
         nc.sync.dma_start(out=w_raw[:].rearrange("p n j d -> p n (j d)"), in_=Wd.rearrange("n (p j) d -> p n (j d)", j=4))
-        nc.gpsimd.memset(wo_scales[:].bitcast(I32), 0)
         make_identity(nc, ident[:])
-        make_identity(nc, ident_b[:])
+        nc.gpsimd.memset(wo_scales[:].bitcast(I32), 0)
         nc.gpsimd.memset(wz_codes[:].rearrange("p t z -> p (t z)").bitcast(I32), 0)
         load_hid(1)
         nc.sync.dma_start(out=wo_words[:], in_=Wo_words[0])
@@ -87,8 +87,7 @@ def tile_mopn_layer_pb_t_w4_kernel(tc, hid_bytes, hid_scale, Wd, Wo_words, Wo_sc
         for t in range(4):
             nc.tensor.transpose(spread[:, t, :], scale_p[:, t : t + 1].to_broadcast([P, P]), ident[:])
         nc.vector.tensor_copy(out=scale[:, 0:H].rearrange("p (m t) -> p m t", t=4), in_=spread[:].rearrange("p t m -> p m t"))
-        for n in range(1, NS):
-            nc.scalar.copy(out=scale[:, n * H : (n + 1) * H], in_=scale[:, 0:H])
+        nc.scalar.copy(out=scale[:, H:HALF], in_=scale[:, 0:H])
         for n in range(NS):
             nc.scalar.copy(out=w_grp[:, :, n], in_=w_raw[:, n].rearrange("p j (m t) -> p t m j", t=4))
 
@@ -102,75 +101,78 @@ def tile_mopn_layer_pb_t_w4_kernel(tc, hid_bytes, hid_scale, Wd, Wo_words, Wo_sc
                 out=wz_codes[:].rearrange("p t (n z) -> p t n z", z=160)[:, :, :, 0:32].bitcast(I32), in_=w_codes[:].bitcast(I32)
             )
 
-        xs_t, xt_t, g_t, c_t, s_t, jp_t, jg_t, jc_t, js_t, po_t, o_t = ({} for z in range(11))
-
-        ws_t = {}
+        xs_t, xt_t, g_t, c_t, s_t, jp_t, jg_t, jc_t, js_t, po_t, o_t, ws_t, pw_t = ({} for z in range(13))
 
         def on_scalar(i):
-            return 2 <= i < TILES - 2 and i % 3 != 1
+            return 1 <= i < TILES - 1 and (i + 1) * 3 // 5 > i * 3 // 5
 
         def widen_s(i):
             if not on_scalar(i):
                 return
-            ws = sb.tile([P, H], BF16, align_bytes=64)
-            base = (i % 2) * NS * H + 3 * H
-            nc.scalar.copy(out=ws[:], in_=hbs[i // 2][:, base : base + H].bitcast(F8))
+            ws = sb.tile([P, HALF], BF16, align_bytes=64)
+            base = (i % 2) * NS * H + HALF
+            nc.scalar.copy(out=ws[:], in_=hbs[i // 2][:, base : base + HALF].bitcast(F8))
             ws_t[i] = ws
 
         def widen(i):
-            xs = sb.tile([P, NS * H], BF16, align_bytes=64)
             base = (i % 2) * NS * H
             hb = hbs[i // 2]
-            w = 512 if i == 0 else 1024 if i == TILES - 1 else 1536 if on_scalar(i) else 2048
-            for c in range(0, 3 * H if on_scalar(i) else 4 * H, w):
-                nc.vector.tensor_tensor(
-                    out=xs[:, c : c + w],
-                    in0=hb[:, base + c : base + c + w].bitcast(F8),
-                    in1=scale[:, 0:w],
-                    op=MULT,
-                )
-            xs_t[i] = xs
+            w = H if i == 0 else HALF
+            halves = []
+            for h in range(1 if on_scalar(i) else 2):
+                xs = sb.tile([P, HALF], BF16, name="xs%d" % h, align_bytes=64)
+                for c in range(0, HALF, w):
+                    nc.vector.tensor_tensor(
+                        out=xs[:, c : c + w],
+                        in0=hb[:, base + h * HALF + c : base + h * HALF + c + w].bitcast(F8),
+                        in1=scale[:, 0:w],
+                        op=MULT,
+                    )
+                halves.append(xs)
+            if on_scalar(i):
+                halves.append(ws_t[i])
+            xs_t[i] = halves
 
         def turn(i):
-            words = xs_t[i][:].bitcast(F32)
             banks = []
             for h in range(2):
+                words = xs_t[i][h][:].bitcast(F32)
                 xt = pst.tile([P, 2, 2, P], F32, name="xt%d" % h)
                 for a in range(2):
-                    n = 2 * h + a
-                    if n == 3 and on_scalar(i):
-                        planes = xt[:, a].rearrange("p u r -> p (u r)").bitcast(BF16)
-                        for t in range(4):
-                            nc.tensor.transpose(planes[:, P * t : P * (t + 1)], ws_t[i][:, t::4], ident_b[:])
-                        continue
                     for u in range(2):
-                        nc.tensor.transpose(xt[:, a, u, :], words[:, 256 * n + u : 256 * (n + 1) : 2], ident[:])
+                        nc.tensor.transpose(xt[:, a, u, :], words[:, 256 * a + u : 256 * (a + 1) : 2], ident[:])
                 banks.append(xt)
             xt_t[i] = banks
 
         def empty(i):
-            g = sb.tile([P, 2048], BF16, align_bytes=64)
+            g = sb.tile([P, 2 * HALF], BF16, align_bytes=64)
             for h in range(2):
                 if h == 1 and on_scalar(i):
-                    nc.scalar.copy(
-                        out=g[:, 1024:1536].bitcast(F32).rearrange("p (r u) -> p r u", u=2),
-                        in_=xt_t[i][1][:, 0].rearrange("p u r -> p r u"),
-                    )
-                    planes = xt_t[i][1][:, 1].rearrange("p u r -> p (u r)").bitcast(BF16)
-                    dst = g[:, 1536:2048].rearrange("p (r t) -> p r t", t=4)
-                    for t in range(4):
-                        nc.scalar.activation(
-                            out=dst[:, :, t],
-                            in_=planes[:, P * t : P * (t + 1)],
-                            func=mybir.ActivationFunctionType.Copy,
-                            scale=scale_p[:, t : t + 1],
-                        )
+                    pw = sb.tile([P, 2, 2, P, 2], BF16, align_bytes=64)
+                    src = xt_t[i][1][:].rearrange("p a u r -> p (a u r)").bitcast(BF16).rearrange("p (a u r e) -> p a u r e", a=2, u=2, e=2)
+                    for e in range(2):
+                        for u in range(2):
+                            nc.scalar.activation(
+                                out=pw[:, u, :, :, e],
+                                in_=src[:, :, u, :, e],
+                                func=COPY,
+                                scale=scale_p[:, 2 * u + e : 2 * u + e + 1],
+                            )
+                    pw_t[i] = pw
                     continue
                 nc.scalar.copy(
-                    out=g[:, 1024 * h : 1024 * (h + 1)].bitcast(F32).rearrange("p (a r u) -> p a r u", a=2, u=2),
+                    out=g[:, HALF * h : HALF * (h + 1)].bitcast(F32).rearrange("p (a r u) -> p a r u", a=2, u=2),
                     in_=xt_t[i][h][:].rearrange("p a u r -> p a r u"),
                 )
             g_t[i] = g
+
+        def weave(i):
+            if not on_scalar(i):
+                return
+            nc.vector.tensor_copy(
+                out=g_t[i][:, HALF : 2 * HALF].bitcast(F32).rearrange("p (m u) -> p m u", u=2),
+                in_=pw_t[i][:].rearrange("p u a r e -> p (u a r e)").bitcast(F32).rearrange("p (u m) -> p m u", u=2),
+            )
 
         def quant(i):
             c = sb.tile([P, 512], U32, name="codes", align_bytes=64)
@@ -228,8 +230,8 @@ def tile_mopn_layer_pb_t_w4_kernel(tc, hid_bytes, hid_scale, Wd, Wo_words, Wo_sc
             elif i % 2 == 1:
                 nc.sync.dma_start(out=oview[i // 2], in_=o[:])
 
-        STAGES = [(empty_j, 3), (widen_s, -1), (widen, 0), (add, 6), (quant, 2), (quant_j, 4), (turn, 0), (empty, 0), (mm1, 2), (mm2, 4)]
-        for i in range(-1, TILES + 6):
+        STAGES = [(empty_j, 4), (widen_s, -1), (widen, 0), (add, 7), (weave, 2), (quant, 3), (quant_j, 5), (turn, 0), (empty, 0), (mm1, 3), (mm2, 5)]
+        for i in range(-1, TILES + 7):
             if i % 2 == 0 and i // 2 + 5 < PAIRS and i >= 0:
                 load_hid(i // 2 + 5)
             if i % 2 == 0 and i // 2 + 4 < PAIRS and i >= 0:

@@ -37,11 +37,11 @@ def tile_mopn_layer_pb_t_w4_kernel(tc, hid_bytes, hid_scale, Wd, Wo_words, Wo_sc
         keep = ctx.enter_context(tc.tile_pool(name="keep", bufs=1))
         loads = ctx.enter_context(tc.tile_pool(name="loads", bufs=8))
         sb = ctx.enter_context(tc.tile_pool(name="sb", bufs=5))
+        ring = ctx.enter_context(tc.tile_pool(name="ring", bufs=5))
         pst = ctx.enter_context(tc.psum_pool(name="pst", bufs=2))
 
         ctx.enter_context(tc.manual_schedule())
 
-        scale = keep.tile([P, HALF], F32, align_bytes=64)
         scale_p = keep.tile([P, 4], F32, align_bytes=64)
         ident = keep.tile([P, P], F32, align_bytes=64)
         w_raw = keep.tile([P, NS, 4, DS], BF16, align_bytes=64)
@@ -83,13 +83,9 @@ def tile_mopn_layer_pb_t_w4_kernel(tc, hid_bytes, hid_scale, Wd, Wo_words, Wo_sc
             load_hid(j)
             load_x(j - 1)
 
-        spread = pst.tile([P, 4, P], F32, name="po")
-        for t in range(4):
-            nc.tensor.transpose(spread[:, t, :], scale_p[:, t : t + 1].to_broadcast([P, P]), ident[:])
-        nc.vector.tensor_copy(out=scale[:, 0:H].rearrange("p (m t) -> p m t", t=4), in_=spread[:].rearrange("p t m -> p m t"))
-        nc.scalar.copy(out=scale[:, H:HALF], in_=scale[:, 0:H])
-        for n in range(NS):
-            nc.scalar.copy(out=w_grp[:, :, n], in_=w_raw[:, n].rearrange("p j (m t) -> p t m j", t=4))
+        def group_w():
+            for n in range(NS):
+                nc.vector.tensor_copy(out=w_grp[:, :, n], in_=w_raw[:, n].rearrange("p j (m t) -> p t m j", t=4))
 
         def prepare_w():
             nc.vector.quantize_mx(
@@ -104,65 +100,54 @@ def tile_mopn_layer_pb_t_w4_kernel(tc, hid_bytes, hid_scale, Wd, Wo_words, Wo_sc
         xs_t, xt_t, g_t, c_t, s_t, jp_t, jg_t, jc_t, js_t, po_t, o_t, ws_t, pw_t = ({} for z in range(13))
 
         def on_scalar(i):
-            return 1 <= i < TILES - 1 and (i + 1) * 3 // 5 > i * 3 // 5
+            return i < TILES - 1 and (i + 1) * 3 // 4 > i * 3 // 4
 
         def widen_s(i):
-            if not on_scalar(i):
-                return
             ws = sb.tile([P, HALF], BF16, align_bytes=64)
             base = (i % 2) * NS * H + HALF
             nc.scalar.copy(out=ws[:], in_=hbs[i // 2][:, base : base + HALF].bitcast(F8))
             ws_t[i] = ws
 
-        def widen(i):
+        def widen_g(i):
+            xs = ring.tile([P, 2 * HALF], BF16, name="ring", align_bytes=64)
             base = (i % 2) * NS * H
-            hb = hbs[i // 2]
-            w = H if i == 0 else HALF
-            halves = []
-            for h in range(1 if on_scalar(i) else 2):
-                xs = sb.tile([P, HALF], BF16, name="xs%d" % h, align_bytes=64)
-                for c in range(0, HALF, w):
-                    nc.vector.tensor_tensor(
-                        out=xs[:, c : c + w],
-                        in0=hb[:, base + h * HALF + c : base + h * HALF + c + w].bitcast(F8),
-                        in1=scale[:, 0:w],
-                        op=MULT,
-                    )
-                halves.append(xs)
-            if on_scalar(i):
-                halves.append(ws_t[i])
-            xs_t[i] = halves
+            eng = nc.vector if i < 2 else nc.gpsimd
+            eng.tensor_copy(out=xs[:, 0:HALF], in_=hbs[i // 2][:, base : base + HALF].bitcast(F8))
+            xs_t[i] = xs
 
         def turn(i):
             banks = []
             for h in range(2):
-                words = xs_t[i][h][:].bitcast(F32)
+                words = (xs_t[i][:, 0:HALF] if h == 0 else ws_t[i][:]).bitcast(F32)
                 xt = pst.tile([P, 2, 2, P], F32, name="xt%d" % h)
                 for a in range(2):
                     for u in range(2):
-                        nc.tensor.transpose(xt[:, a, u, :], words[:, 256 * a + u : 256 * (a + 1) : 2], ident[:])
+                        nc.tensor.transpose(xt[:, u, a, :], words[:, 256 * a + u : 256 * (a + 1) : 2], ident[:])
                 banks.append(xt)
             xt_t[i] = banks
 
-        def empty(i):
-            g = sb.tile([P, 2 * HALF], BF16, align_bytes=64)
-            for h in range(2):
-                if h == 1 and on_scalar(i):
-                    pw = sb.tile([P, 2, 2, P, 2], BF16, align_bytes=64)
-                    src = xt_t[i][1][:].rearrange("p a u r -> p (a u r)").bitcast(BF16).rearrange("p (a u r e) -> p a u r e", a=2, u=2, e=2)
-                    for e in range(2):
-                        for u in range(2):
-                            nc.scalar.activation(
-                                out=pw[:, u, :, :, e],
-                                in_=src[:, :, u, :, e],
-                                func=COPY,
-                                scale=scale_p[:, 2 * u + e : 2 * u + e + 1],
-                            )
-                    pw_t[i] = pw
-                    continue
-                nc.scalar.copy(
-                    out=g[:, HALF * h : HALF * (h + 1)].bitcast(F32).rearrange("p (a r u) -> p a r u", a=2, u=2),
-                    in_=xt_t[i][h][:].rearrange("p a u r -> p a r u"),
+        def bank_view(i, h):
+            return xt_t[i][h][:].rearrange("p u a r -> p (u a r)").bitcast(BF16).rearrange("p (u m e) -> p u m e", u=2, e=2)
+
+        def empty_s(i):
+            if not on_scalar(i):
+                return
+            pw = sb.tile([P, 2, 2 * P, 2], BF16, align_bytes=64)
+            src = bank_view(i, 1)
+            for e in range(2):
+                for u in range(2):
+                    nc.scalar.activation(out=pw[:, u, :, e], in_=src[:, u, :, e], func=COPY, scale=scale_p[:, 2 * u + e : 2 * u + e + 1])
+            pw_t[i] = pw
+
+        def empty_v(i):
+            g = ring.tile([P, 2 * HALF], BF16, name="ring", align_bytes=64)
+            factors = scale_p[:].rearrange("p (u e) -> p u e", u=2).unsqueeze(1).to_broadcast([P, 2 * P, 2, 2])
+            for h in range(1 if on_scalar(i) else 2):
+                nc.vector.tensor_tensor(
+                    out=g[:, HALF * h : HALF * (h + 1)].rearrange("p (m u e) -> p m u e", u=2, e=2),
+                    in0=bank_view(i, h).rearrange("p u m e -> p m u e"),
+                    in1=factors,
+                    op=MULT,
                 )
             g_t[i] = g
 
@@ -171,7 +156,7 @@ def tile_mopn_layer_pb_t_w4_kernel(tc, hid_bytes, hid_scale, Wd, Wo_words, Wo_sc
                 return
             nc.vector.tensor_copy(
                 out=g_t[i][:, HALF : 2 * HALF].bitcast(F32).rearrange("p (m u) -> p m u", u=2),
-                in_=pw_t[i][:].rearrange("p u a r e -> p (u a r e)").bitcast(F32).rearrange("p (u m) -> p m u", u=2),
+                in_=pw_t[i][:].rearrange("p u m e -> p (u m e)").bitcast(F32).rearrange("p (u m) -> p m u", u=2),
             )
 
         def quant(i):
@@ -230,7 +215,20 @@ def tile_mopn_layer_pb_t_w4_kernel(tc, hid_bytes, hid_scale, Wd, Wo_words, Wo_sc
             elif i % 2 == 1:
                 nc.sync.dma_start(out=oview[i // 2], in_=o[:])
 
-        STAGES = [(empty_j, 4), (widen_s, -1), (widen, 0), (add, 7), (weave, 2), (quant, 3), (quant_j, 5), (turn, 0), (empty, 0), (mm1, 3), (mm2, 5)]
+        STAGES = [
+            (empty_j, 5),
+            (quant_j, 6),
+            (weave, 2),
+            (quant, 3),
+            (widen_g, -1),
+            (widen_s, -1),
+            (empty_v, 1),
+            (empty_s, 1),
+            (add, 7),
+            (mm1, 4),
+            (mm2, 6),
+            (turn, 0),
+        ]
         for i in range(-1, TILES + 7):
             if i % 2 == 0 and i // 2 + 5 < PAIRS and i >= 0:
                 load_hid(i // 2 + 5)
@@ -239,5 +237,7 @@ def tile_mopn_layer_pb_t_w4_kernel(tc, hid_bytes, hid_scale, Wd, Wo_words, Wo_sc
             for stage, lag in STAGES:
                 if 0 <= i - lag < TILES:
                     stage(i - lag)
+            if i == 0:
+                group_w()
             if i == 1:
                 prepare_w()

@@ -23,6 +23,17 @@ D = NS * DS
 HALF = 2 * H
 TILES = TOKENS // P
 PAIRS = TILES // 2
+LAG_W = 2
+LAG_Q = 3
+LAG_J = 2
+LAG_A = 1
+LAG_M = 3
+V_TILES = LAG_M + LAG_J + 1
+M_S = 208
+G_COLS = 1280
+E_COLS = 1024
+W_STEP = 0
+M_V = 2 * P - M_S
 FLOPS = 2 * TOKENS * NS * H * DS + 2 * TOKENS * D * D
 
 
@@ -36,8 +47,8 @@ def tile_mopn_layer_pb_t_w4_kernel(tc, hid_bytes, hid_scale, Wd, Wo_words, Wo_sc
     with ExitStack() as ctx:
         keep = ctx.enter_context(tc.tile_pool(name="keep", bufs=1))
         loads = ctx.enter_context(tc.tile_pool(name="loads", bufs=8))
-        sb = ctx.enter_context(tc.tile_pool(name="sb", bufs=5))
-        ring = ctx.enter_context(tc.tile_pool(name="ring", bufs=5))
+        sb = ctx.enter_context(tc.tile_pool(name="sb", bufs=6))
+        ring = ctx.enter_context(tc.tile_pool(name="ring", bufs=2 * LAG_J - 1))
         pst = ctx.enter_context(tc.psum_pool(name="pst", bufs=2))
 
         ctx.enter_context(tc.manual_schedule())
@@ -71,8 +82,8 @@ def tile_mopn_layer_pb_t_w4_kernel(tc, hid_bytes, hid_scale, Wd, Wo_words, Wo_sc
         load_hid(0, 2)
         nc.sync.dma_start(out=w_raw[:].rearrange("p n j d -> p n (j d)"), in_=Wd.rearrange("n (p j) d -> p n (j d)", j=4))
         make_identity(nc, ident[:])
-        nc.gpsimd.memset(wo_scales[:].bitcast(I32), 0)
-        nc.gpsimd.memset(wz_codes[:].rearrange("p t z -> p (t z)").bitcast(I32), 0)
+        nc.vector.memset(wo_scales[:].bitcast(I32), 0)
+        nc.vector.memset(wz_codes[:].rearrange("p t z -> p (t z)").bitcast(I32), 0)
         load_hid(1)
         nc.sync.dma_start(out=wo_words[:], in_=Wo_words[0])
         wos = Wo_scales[0].bitcast(I32)
@@ -87,42 +98,45 @@ def tile_mopn_layer_pb_t_w4_kernel(tc, hid_bytes, hid_scale, Wd, Wo_words, Wo_sc
             for n in range(NS):
                 nc.vector.tensor_copy(out=w_grp[:, :, n], in_=w_raw[:, n].rearrange("p j (m t) -> p t m j", t=4))
 
-        def prepare_w():
+        def quant_w():
             nc.vector.quantize_mx(
                 out=w_codes[:].rearrange("p t n m -> p (t n m)").bitcast(F8X4),
                 scales=w_scales[:],
                 in_=w_grp[:].rearrange("p t n m j -> p (t n m j)"),
             )
+
+        def pad_w():
             nc.vector.tensor_copy(
                 out=wz_codes[:].rearrange("p t (n z) -> p t n z", z=160)[:, :, :, 0:32].bitcast(I32), in_=w_codes[:].bitcast(I32)
             )
 
-        xs_t, xt_t, g_t, c_t, s_t, jp_t, jg_t, jc_t, js_t, po_t, o_t, ws_t, pw_t = ({} for z in range(13))
+        xs_t, xt_t, g_t, c_t, s_t, jp_t, jg_t, jc_t, js_t, po_t, o_t, pw_t = ({} for z in range(12))
 
-        def on_scalar(i):
-            return i < TILES - 1 and (i + 1) * 3 // 4 > i * 3 // 4
-
-        def widen_s(i):
-            ws = sb.tile([P, HALF], BF16, align_bytes=64)
-            base = (i % 2) * NS * H + HALF
-            nc.scalar.copy(out=ws[:], in_=hbs[i // 2][:, base : base + HALF].bitcast(F8))
-            ws_t[i] = ws
+        def split(i):
+            return E_COLS if i < V_TILES else G_COLS
 
         def widen_g(i):
             xs = ring.tile([P, 2 * HALF], BF16, name="ring", align_bytes=64)
             base = (i % 2) * NS * H
-            eng = nc.vector if i < 2 else nc.gpsimd
-            eng.tensor_copy(out=xs[:, 0:HALF], in_=hbs[i // 2][:, base : base + HALF].bitcast(F8))
+            eng = nc.vector if i < V_TILES else nc.gpsimd
+            cut = split(i)
+            eng.tensor_copy(out=xs[:, 0:cut], in_=hbs[i // 2][:, base : base + cut].bitcast(F8))
             xs_t[i] = xs
+
+        def widen_s(i):
+            base = (i % 2) * NS * H
+            cut = split(i)
+            nc.scalar.copy(out=xs_t[i][:, cut:], in_=hbs[i // 2][:, base + cut : base + 2 * HALF].bitcast(F8))
 
         def turn(i):
             banks = []
+            words = xs_t[i][:].bitcast(F32)
             for h in range(2):
-                words = (xs_t[i][:, 0:HALF] if h == 0 else ws_t[i][:]).bitcast(F32)
                 xt = pst.tile([P, 2, 2, P], F32, name="xt%d" % h)
                 for a in range(2):
+                    n = 2 * h + a
                     for u in range(2):
-                        nc.tensor.transpose(xt[:, u, a, :], words[:, 256 * a + u : 256 * (a + 1) : 2], ident[:])
+                        nc.tensor.transpose(xt[:, u, a, :], words[:, 256 * n + u : 256 * (n + 1) : 2], ident[:])
                 banks.append(xt)
             xt_t[i] = banks
 
@@ -130,32 +144,27 @@ def tile_mopn_layer_pb_t_w4_kernel(tc, hid_bytes, hid_scale, Wd, Wo_words, Wo_sc
             return xt_t[i][h][:].rearrange("p u a r -> p (u a r)").bitcast(BF16).rearrange("p (u m e) -> p u m e", u=2, e=2)
 
         def empty_s(i):
-            if not on_scalar(i):
-                return
-            pw = sb.tile([P, 2, 2 * P, 2], BF16, align_bytes=64)
+            pw = sb.tile([P, 2, M_S, 2], BF16, align_bytes=64)
             src = bank_view(i, 1)
             for e in range(2):
                 for u in range(2):
-                    nc.scalar.activation(out=pw[:, u, :, e], in_=src[:, u, :, e], func=COPY, scale=scale_p[:, 2 * u + e : 2 * u + e + 1])
+                    nc.scalar.activation(out=pw[:, u, :, e], in_=src[:, u, M_V:, e], func=COPY, scale=scale_p[:, 2 * u + e : 2 * u + e + 1])
             pw_t[i] = pw
 
         def empty_v(i):
-            g = ring.tile([P, 2 * HALF], BF16, name="ring", align_bytes=64)
-            factors = scale_p[:].rearrange("p (u e) -> p u e", u=2).unsqueeze(1).to_broadcast([P, 2 * P, 2, 2])
-            for h in range(1 if on_scalar(i) else 2):
+            g = sb.tile([P, 2 * HALF], BF16, name="g", align_bytes=64)
+            for h, m in ((0, 2 * P), (1, M_V)):
                 nc.vector.tensor_tensor(
-                    out=g[:, HALF * h : HALF * (h + 1)].rearrange("p (m u e) -> p m u e", u=2, e=2),
-                    in0=bank_view(i, h).rearrange("p u m e -> p m u e"),
-                    in1=factors,
+                    out=g[:, HALF * h : HALF * h + 4 * m].rearrange("p (m u e) -> p m u e", u=2, e=2),
+                    in0=bank_view(i, h)[:, :, 0:m, :].rearrange("p u m e -> p m u e"),
+                    in1=scale_p[:].rearrange("p (u e) -> p u e", u=2).unsqueeze(1).to_broadcast([P, m, 2, 2]),
                     op=MULT,
                 )
             g_t[i] = g
 
         def weave(i):
-            if not on_scalar(i):
-                return
             nc.vector.tensor_copy(
-                out=g_t[i][:, HALF : 2 * HALF].bitcast(F32).rearrange("p (m u) -> p m u", u=2),
+                out=g_t[i][:, HALF + 4 * M_V :].bitcast(F32).rearrange("p (m u) -> p m u", u=2),
                 in_=pw_t[i][:].rearrange("p u m e -> p (u m e)").bitcast(F32).rearrange("p (u m) -> p m u", u=2),
             )
 
@@ -167,6 +176,7 @@ def tile_mopn_layer_pb_t_w4_kernel(tc, hid_bytes, hid_scale, Wd, Wo_words, Wo_sc
 
         def mm1(i):
             jp = pst.tile([P, 4, P], F32, name="jp")
+            jp_t[i] = jp
             for t in range(4):
                 for n in range(NS):
                     nc.tensor.matmul_mx(
@@ -178,12 +188,11 @@ def tile_mopn_layer_pb_t_w4_kernel(tc, hid_bytes, hid_scale, Wd, Wo_words, Wo_sc
                         start=(n == 0),
                         stop=(n == NS - 1),
                     )
-            jp_t[i] = jp
 
         def empty_j(i):
-            jg = sb.tile([P, P, 4], BF16, name="jg", align_bytes=64)
-            nc.scalar.copy(out=jg[:], in_=jp_t[i][:].rearrange("p t r -> p r t"))
+            jg = ring.tile([P, P, 4], BF16, name="ring", align_bytes=64)
             jg_t[i] = jg
+            nc.scalar.copy(out=jg[:], in_=jp_t[i][:].rearrange("p t r -> p r t"))
 
         def quant_j(i):
             c = sb.tile([P, P], U32, name="jcodes", align_bytes=64)
@@ -216,20 +225,20 @@ def tile_mopn_layer_pb_t_w4_kernel(tc, hid_bytes, hid_scale, Wd, Wo_words, Wo_sc
                 nc.sync.dma_start(out=oview[i // 2], in_=o[:])
 
         STAGES = [
-            (empty_j, 5),
-            (quant_j, 6),
-            (weave, 2),
-            (quant, 3),
+            (turn, 0),
+            (empty_s, 1),
+            (empty_j, LAG_M + 1),
+            (weave, LAG_W),
+            (quant_j, LAG_M + LAG_J),
+            (quant, LAG_Q),
             (widen_g, -1),
             (widen_s, -1),
             (empty_v, 1),
-            (empty_s, 1),
-            (add, 7),
-            (mm1, 4),
-            (mm2, 6),
-            (turn, 0),
+            (add, LAG_M + LAG_J + LAG_A),
+            (mm1, LAG_M),
+            (mm2, LAG_M + LAG_J),
         ]
-        for i in range(-1, TILES + 7):
+        for i in range(-1, TILES + LAG_M + LAG_J + LAG_A):
             if i % 2 == 0 and i // 2 + 5 < PAIRS and i >= 0:
                 load_hid(i // 2 + 5)
             if i % 2 == 0 and i // 2 + 4 < PAIRS and i >= 0:
@@ -237,7 +246,9 @@ def tile_mopn_layer_pb_t_w4_kernel(tc, hid_bytes, hid_scale, Wd, Wo_words, Wo_sc
             for stage, lag in STAGES:
                 if 0 <= i - lag < TILES:
                     stage(i - lag)
-            if i == 0:
+            if i == W_STEP:
                 group_w()
-            if i == 1:
-                prepare_w()
+            if i == W_STEP + 1:
+                quant_w()
+            if i == W_STEP + 2:
+                pad_w()

@@ -28,11 +28,16 @@ LAG_Q = 3
 LAG_J = 2
 LAG_A = 1
 LAG_M = 3
-V_TILES = LAG_M + LAG_J + 1
-M_S = 208
-G_COLS = 1280
+V_TILES = 3
+RING = 5
+F_COLS = 1152
+F_TILES = 6
+DRAIN = 1
+FIRST = 2
+SPLIT_LAST = 1
+M_S = 216
+G_COLS = 1344
 E_COLS = 1024
-W_STEP = 0
 M_V = 2 * P - M_S
 FLOPS = 2 * TOKENS * NS * H * DS + 2 * TOKENS * D * D
 
@@ -48,7 +53,7 @@ def tile_mopn_layer_pb_t_w4_kernel(tc, hid_bytes, hid_scale, Wd, Wo_words, Wo_sc
         keep = ctx.enter_context(tc.tile_pool(name="keep", bufs=1))
         loads = ctx.enter_context(tc.tile_pool(name="loads", bufs=8))
         sb = ctx.enter_context(tc.tile_pool(name="sb", bufs=6))
-        ring = ctx.enter_context(tc.tile_pool(name="ring", bufs=2 * LAG_J - 1))
+        ring = ctx.enter_context(tc.tile_pool(name="ring", bufs=RING))
         pst = ctx.enter_context(tc.psum_pool(name="pst", bufs=2))
 
         ctx.enter_context(tc.manual_schedule())
@@ -56,7 +61,6 @@ def tile_mopn_layer_pb_t_w4_kernel(tc, hid_bytes, hid_scale, Wd, Wo_words, Wo_sc
         scale_p = keep.tile([P, 4], F32, align_bytes=64)
         ident = keep.tile([P, P], F32, align_bytes=64)
         w_raw = keep.tile([P, NS, 4, DS], BF16, align_bytes=64)
-        w_grp = keep.tile([P, 4, NS, 32, 4], BF16, align_bytes=64)
         w_codes = keep.tile([P, 4, NS, 32], U32, align_bytes=64)
         w_scales = keep.tile([P, 4 * P], U8, align_bytes=64)
         wz_codes = keep.tile([P, 4, 640], U32, align_bytes=64)
@@ -66,11 +70,9 @@ def tile_mopn_layer_pb_t_w4_kernel(tc, hid_bytes, hid_scale, Wd, Wo_words, Wo_sc
         hbs = {}
         xts = {}
 
-        def load_hid(j, halves=1):
-            hb = loads.tile([P, 4096], U8, align_bytes=64)
-            w = 4096 // halves
-            for h in range(halves):
-                nc.sync.dma_start(out=hb[:, h * w : (h + 1) * w], in_=hid[j][:, h * w : (h + 1) * w])
+        def load_hid(j):
+            hb = loads.tile([P, 4096], U8, name="hb", align_bytes=64)
+            nc.sync.dma_start(out=hb[:], in_=hid[j])
             hbs[j] = hb
 
         def load_x(j):
@@ -78,9 +80,13 @@ def tile_mopn_layer_pb_t_w4_kernel(tc, hid_bytes, hid_scale, Wd, Wo_words, Wo_sc
             nc.sync.dma_start(out=xt[:], in_=xin[j])
             xts[j] = xt
 
-        nc.sync.dma_start(out=scale_p[:], in_=srow.rearrange("(p t) -> p t", t=4))
-        load_hid(0, 2)
+        hb0 = loads.tile([P, 4096], U8, name="hb", align_bytes=64)
+        hbs[0] = hb0
+        for c in range(0, 2048, 2048 // FIRST):
+            nc.sync.dma_start(out=hb0[:, c : c + 2048 // FIRST], in_=hid[0][:, c : c + 2048 // FIRST])
         nc.sync.dma_start(out=w_raw[:].rearrange("p n j d -> p n (j d)"), in_=Wd.rearrange("n (p j) d -> p n (j d)", j=4))
+        nc.sync.dma_start(out=hb0[:, 2048:4096], in_=hid[0][:, 2048:4096])
+        nc.sync.dma_start(out=scale_p[:], in_=srow.rearrange("(p t) -> p t", t=4))
         make_identity(nc, ident[:])
         nc.vector.memset(wo_scales[:].bitcast(I32), 0)
         nc.vector.memset(wz_codes[:].rearrange("p t z -> p (t z)").bitcast(I32), 0)
@@ -94,15 +100,18 @@ def tile_mopn_layer_pb_t_w4_kernel(tc, hid_bytes, hid_scale, Wd, Wo_words, Wo_sc
             load_hid(j)
             load_x(j - 1)
 
+        w_grp = []
+
         def group_w():
-            for n in range(NS):
-                nc.vector.tensor_copy(out=w_grp[:, :, n], in_=w_raw[:, n].rearrange("p j (m t) -> p t m j", t=4))
+            grp = ring.tile([P, 4, NS, 32, 4], BF16, name="ring", align_bytes=64)
+            nc.vector.tensor_copy(out=grp[:], in_=w_raw[:].rearrange("p n j (m t) -> p t n m j", t=4))
+            w_grp.append(grp)
 
         def quant_w():
             nc.vector.quantize_mx(
                 out=w_codes[:].rearrange("p t n m -> p (t n m)").bitcast(F8X4),
                 scales=w_scales[:],
-                in_=w_grp[:].rearrange("p t n m j -> p (t n m j)"),
+                in_=w_grp[0][:].rearrange("p t n m j -> p (t n m j)"),
             )
 
         def pad_w():
@@ -113,7 +122,7 @@ def tile_mopn_layer_pb_t_w4_kernel(tc, hid_bytes, hid_scale, Wd, Wo_words, Wo_sc
         xs_t, xt_t, g_t, c_t, s_t, jp_t, jg_t, jc_t, js_t, po_t, o_t, pw_t = ({} for z in range(12))
 
         def split(i):
-            return E_COLS if i < V_TILES else G_COLS
+            return E_COLS if i < V_TILES else F_COLS if i < F_TILES else G_COLS
 
         def widen_g(i):
             xs = ring.tile([P, 2 * HALF], BF16, name="ring", align_bytes=64)
@@ -144,7 +153,7 @@ def tile_mopn_layer_pb_t_w4_kernel(tc, hid_bytes, hid_scale, Wd, Wo_words, Wo_sc
             return xt_t[i][h][:].rearrange("p u a r -> p (u a r)").bitcast(BF16).rearrange("p (u m e) -> p u m e", u=2, e=2)
 
         def empty_s(i):
-            pw = sb.tile([P, 2, M_S, 2], BF16, align_bytes=64)
+            pw = ring.tile([P, 2, M_S, 2], BF16, name="ring", align_bytes=64)
             src = bank_view(i, 1)
             for e in range(2):
                 for u in range(2):
@@ -190,7 +199,7 @@ def tile_mopn_layer_pb_t_w4_kernel(tc, hid_bytes, hid_scale, Wd, Wo_words, Wo_sc
                     )
 
         def empty_j(i):
-            jg = ring.tile([P, P, 4], BF16, name="ring", align_bytes=64)
+            jg = sb.tile([P, P, 4], BF16, name="jg", align_bytes=64)
             jg_t[i] = jg
             nc.scalar.copy(out=jg[:], in_=jp_t[i][:].rearrange("p t r -> p r t"))
 
@@ -217,38 +226,68 @@ def tile_mopn_layer_pb_t_w4_kernel(tc, hid_bytes, hid_scale, Wd, Wo_words, Wo_sc
             if i % 2 == 0:
                 o_t[i // 2] = sb.tile([P, 2 * D], F32, name="o", align_bytes=64)
             o = o_t[i // 2]
-            cols = slice((i % 2) * D, (i % 2 + 1) * D)
-            nc.vector.tensor_tensor(out=o[:, cols], in0=po_t[i][:], in1=xts[i // 2][:, cols], op=ADD)
-            if i >= TILES - 2:
-                nc.sync.dma_start(out=oview[i // 2][:, cols], in_=o[:, cols])
-            elif i % 2 == 1:
+            parts = SPLIT_LAST if i == TILES - 1 else 1
+            for c in range(0, D, D // parts):
+                cols = slice((i % 2) * D + c, (i % 2) * D + c + D // parts)
+                nc.vector.tensor_tensor(out=o[:, cols], in0=po_t[i][:, c : c + D // parts], in1=xts[i // 2][:, cols], op=ADD)
+                if i >= TILES - 2:
+                    nc.sync.dma_start(out=oview[i // 2][:, cols], in_=o[:, cols])
+            if i < TILES - 2 and i % 2 == 1:
                 nc.sync.dma_start(out=oview[i // 2], in_=o[:])
 
         STAGES = [
             (turn, 0),
             (empty_s, 1),
             (empty_j, LAG_M + 1),
-            (weave, LAG_W),
             (quant_j, LAG_M + LAG_J),
+            (weave, LAG_W),
             (quant, LAG_Q),
             (widen_g, -1),
             (widen_s, -1),
             (empty_v, 1),
-            (add, LAG_M + LAG_J + LAG_A),
-            (mm1, LAG_M),
             (mm2, LAG_M + LAG_J),
+            (mm1, LAG_M),
+            (add, LAG_M + LAG_J + LAG_A),
         ]
-        for i in range(-1, TILES + LAG_M + LAG_J + LAG_A):
+        last = TILES if DRAIN else TILES + LAG_M + LAG_J + LAG_A
+        for i in range(-1, last):
             if i % 2 == 0 and i // 2 + 5 < PAIRS and i >= 0:
                 load_hid(i // 2 + 5)
             if i % 2 == 0 and i // 2 + 4 < PAIRS and i >= 0:
                 load_x(i // 2 + 4)
+            if i == 2:
+                pad_w()
             for stage, lag in STAGES:
                 if 0 <= i - lag < TILES:
                     stage(i - lag)
-            if i == W_STEP:
+            if i == -1:
                 group_w()
-            if i == W_STEP + 1:
+            if i == 0:
                 quant_w()
-            if i == W_STEP + 2:
-                pad_w()
+        if DRAIN:
+            n = TILES
+            empty_s(n - 1)
+            empty_j(n - 4)
+            weave(n - 2)
+            quant(n - 3)
+            mm1(n - 3)
+            quant_j(n - 5)
+            mm2(n - 5)
+            quant(n - 2)
+            empty_v(n - 1)
+            add(n - 6)
+            empty_j(n - 3)
+            mm1(n - 2)
+            weave(n - 1)
+            quant_j(n - 4)
+            mm2(n - 4)
+            quant(n - 1)
+            empty_j(n - 2)
+            mm1(n - 1)
+            empty_j(n - 1)
+            add(n - 5)
+            for i in range(n - 3, n):
+                quant_j(i)
+                add(i - 1)
+                mm2(i)
+            add(n - 1)

@@ -30,15 +30,18 @@ LAG_A = 1
 LAG_M = 3
 V_TILES = 3
 RING = 5
-F_COLS = 1152
+F_COLS = 1024
 F_TILES = 6
 DRAIN = 1
 FIRST = 2
 SPLIT_LAST = 1
-M_S = 216
-G_COLS = 1344
+M_S = 208
+M_FIRST = 208
+M_LAST = 256
+N_FIRST = 3
+N_LAST = 2
+G_COLS = 1280
 E_COLS = 1024
-M_V = 2 * P - M_S
 FLOPS = 2 * TOKENS * NS * H * DS + 2 * TOKENS * D * D
 
 
@@ -121,6 +124,9 @@ def tile_mopn_layer_pb_t_w4_kernel(tc, hid_bytes, hid_scale, Wd, Wo_words, Wo_sc
 
         xs_t, xt_t, g_t, c_t, s_t, jp_t, jg_t, jc_t, js_t, po_t, o_t, pw_t = ({} for z in range(12))
 
+        def m_s(i):
+            return M_FIRST if i < N_FIRST else M_LAST if i >= TILES - N_LAST else M_S
+
         def split(i):
             return E_COLS if i < V_TILES else F_COLS if i < F_TILES else G_COLS
 
@@ -153,16 +159,18 @@ def tile_mopn_layer_pb_t_w4_kernel(tc, hid_bytes, hid_scale, Wd, Wo_words, Wo_sc
             return xt_t[i][h][:].rearrange("p u a r -> p (u a r)").bitcast(BF16).rearrange("p (u m e) -> p u m e", u=2, e=2)
 
         def empty_s(i):
-            pw = ring.tile([P, 2, M_S, 2], BF16, name="ring", align_bytes=64)
+            pw = ring.tile([P, 2, m_s(i), 2], BF16, name="ring", align_bytes=64)
             src = bank_view(i, 1)
             for e in range(2):
                 for u in range(2):
-                    nc.scalar.activation(out=pw[:, u, :, e], in_=src[:, u, M_V:, e], func=COPY, scale=scale_p[:, 2 * u + e : 2 * u + e + 1])
+                    nc.scalar.activation(out=pw[:, u, :, e], in_=src[:, u, 2 * P - m_s(i) :, e], func=COPY, scale=scale_p[:, 2 * u + e : 2 * u + e + 1])
             pw_t[i] = pw
 
         def empty_v(i):
             g = sb.tile([P, 2 * HALF], BF16, name="g", align_bytes=64)
-            for h, m in ((0, 2 * P), (1, M_V)):
+            for h, m in ((0, 2 * P), (1, 2 * P - m_s(i))):
+                if m == 0:
+                    continue
                 nc.vector.tensor_tensor(
                     out=g[:, HALF * h : HALF * h + 4 * m].rearrange("p (m u e) -> p m u e", u=2, e=2),
                     in0=bank_view(i, h)[:, :, 0:m, :].rearrange("p u m e -> p m u e"),
@@ -173,7 +181,7 @@ def tile_mopn_layer_pb_t_w4_kernel(tc, hid_bytes, hid_scale, Wd, Wo_words, Wo_sc
 
         def weave(i):
             nc.vector.tensor_copy(
-                out=g_t[i][:, HALF + 4 * M_V :].bitcast(F32).rearrange("p (m u) -> p m u", u=2),
+                out=g_t[i][:, 2 * HALF - 4 * m_s(i) :].bitcast(F32).rearrange("p (m u) -> p m u", u=2),
                 in_=pw_t[i][:].rearrange("p u m e -> p (u m e)").bitcast(F32).rearrange("p (u m) -> p m u", u=2),
             )
 

@@ -35,12 +35,13 @@ F_TILES = 6
 DRAIN = 1
 FIRST = 2
 SPLIT_LAST = 1
-M_S = 208
-M_FIRST = 208
+M_S = 200
+M_FIRST = 200
 M_LAST = 256
+P_FROM = 3
 N_FIRST = 3
 N_LAST = 2
-G_COLS = 1280
+G_COLS = 1344
 E_COLS = 1024
 FLOPS = 2 * TOKENS * NS * H * DS + 2 * TOKENS * D * D
 
@@ -63,6 +64,7 @@ def tile_mopn_layer_pb_t_w4_kernel(tc, hid_bytes, hid_scale, Wd, Wo_words, Wo_sc
 
         scale_p = keep.tile([P, 4], F32, align_bytes=64)
         ident = keep.tile([P, P], F32, align_bytes=64)
+        ident_b = keep.tile([P, P], BF16, align_bytes=64)
         w_raw = keep.tile([P, NS, 4, DS], BF16, align_bytes=64)
         w_codes = keep.tile([P, 4, NS, 32], U32, align_bytes=64)
         w_scales = keep.tile([P, 4 * P], U8, align_bytes=64)
@@ -85,11 +87,12 @@ def tile_mopn_layer_pb_t_w4_kernel(tc, hid_bytes, hid_scale, Wd, Wo_words, Wo_sc
 
         hb0 = loads.tile([P, 4096], U8, name="hb", align_bytes=64)
         hbs[0] = hb0
-        for c in range(0, 2048, 2048 // FIRST):
+        for c in reversed(range(0, 2048, 2048 // FIRST)):
             nc.sync.dma_start(out=hb0[:, c : c + 2048 // FIRST], in_=hid[0][:, c : c + 2048 // FIRST])
         nc.sync.dma_start(out=w_raw[:].rearrange("p n j d -> p n (j d)"), in_=Wd.rearrange("n (p j) d -> p n (j d)", j=4))
         nc.sync.dma_start(out=hb0[:, 2048:4096], in_=hid[0][:, 2048:4096])
         nc.sync.dma_start(out=scale_p[:], in_=srow.rearrange("(p t) -> p t", t=4))
+        make_identity(nc, ident_b[:])
         make_identity(nc, ident[:])
         nc.vector.memset(wo_scales[:].bitcast(I32), 0)
         nc.vector.memset(wz_codes[:].rearrange("p t z -> p (t z)").bitcast(I32), 0)
@@ -135,25 +138,35 @@ def tile_mopn_layer_pb_t_w4_kernel(tc, hid_bytes, hid_scale, Wd, Wo_words, Wo_sc
             base = (i % 2) * NS * H
             eng = nc.vector if i < V_TILES else nc.gpsimd
             cut = split(i)
-            eng.tensor_copy(out=xs[:, 0:cut], in_=hbs[i // 2][:, base : base + cut].bitcast(F8))
+            eng.tensor_copy(out=xs[:, 2 * HALF - cut :], in_=hbs[i // 2][:, base + 2 * HALF - cut : base + 2 * HALF].bitcast(F8))
             xs_t[i] = xs
 
         def widen_s(i):
             base = (i % 2) * NS * H
             cut = split(i)
-            nc.scalar.copy(out=xs_t[i][:, cut:], in_=hbs[i // 2][:, base + cut : base + 2 * HALF].bitcast(F8))
+            nc.scalar.copy(out=xs_t[i][:, 0 : 2 * HALF - cut], in_=hbs[i // 2][:, base : base + 2 * HALF - cut].bitcast(F8))
 
         def turn(i):
-            banks = []
             words = xs_t[i][:].bitcast(F32)
-            for h in range(2):
-                xt = pst.tile([P, 2, 2, P], F32, name="xt%d" % h)
-                for a in range(2):
-                    n = 2 * h + a
-                    for u in range(2):
-                        nc.tensor.transpose(xt[:, u, a, :], words[:, 256 * n + u : 256 * (n + 1) : 2], ident[:])
-                banks.append(xt)
+            banks = [pst.tile([P, 2, 2, P], F32, name="xt%d" % h) for h in range(2)]
             xt_t[i] = banks
+
+            def plane(e):
+                nc.tensor.matmul(
+                    out=banks[1][:, 1, 1, :].bitcast(BF16)[:, P * e : P * (e + 1)],
+                    lhsT=xs_t[i][:, 3 * H + 2 + e : 4 * H : 4],
+                    rhs=ident_b[:],
+                    start=True,
+                    stop=True,
+                )
+
+            if i >= P_FROM:
+                plane(0)
+            for n in reversed(range(NS)):
+                for u in range(1 if n == 3 and i >= P_FROM else 2):
+                    nc.tensor.transpose(banks[n // 2][:, u, n % 2, :], words[:, 256 * n + u : 256 * (n + 1) : 2], ident[:])
+            if i >= P_FROM:
+                plane(1)
 
         def bank_view(i, h):
             return xt_t[i][h][:].rearrange("p u a r -> p (u a r)").bitcast(BF16).rearrange("p (u m e) -> p u m e", u=2, e=2)
@@ -161,9 +174,16 @@ def tile_mopn_layer_pb_t_w4_kernel(tc, hid_bytes, hid_scale, Wd, Wo_words, Wo_sc
         def empty_s(i):
             pw = ring.tile([P, 2, m_s(i), 2], BF16, name="ring", align_bytes=64)
             src = bank_view(i, 1)
+            lo = 2 * P - m_s(i)
             for e in range(2):
                 for u in range(2):
-                    nc.scalar.activation(out=pw[:, u, :, e], in_=src[:, u, 2 * P - m_s(i) :, e], func=COPY, scale=scale_p[:, 2 * u + e : 2 * u + e + 1])
+                    col = scale_p[:, 2 * u + e : 2 * u + e + 1]
+                    if u == 1 and i >= P_FROM:
+                        nc.scalar.activation(out=pw[:, u, 0 : P - lo, e], in_=src[:, u, lo:P, e], func=COPY, scale=col)
+                        flat = xt_t[i][1][:, 1, 1, :].bitcast(BF16)
+                        nc.scalar.activation(out=pw[:, u, P - lo :, e], in_=flat[:, P * e : P * (e + 1)], func=COPY, scale=col)
+                    else:
+                        nc.scalar.activation(out=pw[:, u, :, e], in_=src[:, u, lo:, e], func=COPY, scale=col)
             pw_t[i] = pw
 
         def empty_v(i):

@@ -20,29 +20,18 @@ NS = 4
 H = 512
 DS = 128
 D = NS * DS
+ROW = NS * H
 HALF = 2 * H
 TILES = TOKENS // P
 PAIRS = TILES // 2
-LAG_W = 2
-LAG_Q = 3
-LAG_J = 2
-LAG_A = 1
-LAG_M = 3
 V_TILES = 3
 RING = 5
 F_COLS = 1024
 F_TILES = 6
-DRAIN = 1
-FIRST = 2
-SPLIT_LAST = 1
-M_S = 200
-M_FIRST = 200
-M_LAST = 256
-P_FROM = 3
-N_FIRST = 3
+M_S = 192
+M_LAST = 192
 N_LAST = 2
 G_COLS = 1344
-E_COLS = 1024
 FLOPS = 2 * TOKENS * NS * H * DS + 2 * TOKENS * D * D
 
 
@@ -58,17 +47,17 @@ def tile_mopn_layer_pb_t_w4_kernel(tc, hid_bytes, hid_scale, Wd, Wo_words, Wo_sc
         loads = ctx.enter_context(tc.tile_pool(name="loads", bufs=8))
         sb = ctx.enter_context(tc.tile_pool(name="sb", bufs=6))
         ring = ctx.enter_context(tc.tile_pool(name="ring", bufs=RING))
-        pst = ctx.enter_context(tc.psum_pool(name="pst", bufs=2))
+        two = ctx.enter_context(tc.psum_pool(name="two", bufs=2))
+        one = ctx.enter_context(tc.psum_pool(name="one", bufs=1))
 
         ctx.enter_context(tc.manual_schedule())
 
         scale_p = keep.tile([P, 4], F32, align_bytes=64)
         ident = keep.tile([P, P], F32, align_bytes=64)
-        ident_b = keep.tile([P, P], BF16, align_bytes=64)
         w_raw = keep.tile([P, NS, 4, DS], BF16, align_bytes=64)
-        w_codes = keep.tile([P, 4, NS, 32], U32, align_bytes=64)
-        w_scales = keep.tile([P, 4 * P], U8, align_bytes=64)
-        wz_codes = keep.tile([P, 4, 640], U32, align_bytes=64)
+        w_grp = keep.tile([P, NS, DS, 4], BF16, align_bytes=64)
+        w_codes = keep.tile([P, D], U32, align_bytes=64)
+        w_scales = keep.tile([P, D], U8, align_bytes=64)
         wo_words = keep.tile([P, 2 * D], U8, align_bytes=64)
         wo_scales = keep.tile([P, D], U8, align_bytes=64)
 
@@ -76,7 +65,7 @@ def tile_mopn_layer_pb_t_w4_kernel(tc, hid_bytes, hid_scale, Wd, Wo_words, Wo_sc
         xts = {}
 
         def load_hid(j):
-            hb = loads.tile([P, 4096], U8, name="hb", align_bytes=64)
+            hb = loads.tile([P, 2 * ROW], U8, name="hb", align_bytes=64)
             nc.sync.dma_start(out=hb[:], in_=hid[j])
             hbs[j] = hb
 
@@ -85,17 +74,15 @@ def tile_mopn_layer_pb_t_w4_kernel(tc, hid_bytes, hid_scale, Wd, Wo_words, Wo_sc
             nc.sync.dma_start(out=xt[:], in_=xin[j])
             xts[j] = xt
 
-        hb0 = loads.tile([P, 4096], U8, name="hb", align_bytes=64)
+        hb0 = loads.tile([P, 2 * ROW], U8, name="hb", align_bytes=64)
         hbs[0] = hb0
-        for c in reversed(range(0, 2048, 2048 // FIRST)):
-            nc.sync.dma_start(out=hb0[:, c : c + 2048 // FIRST], in_=hid[0][:, c : c + 2048 // FIRST])
+        for c in (HALF, 0):
+            nc.sync.dma_start(out=hb0[:, c : c + HALF], in_=hid[0][:, c : c + HALF])
         nc.sync.dma_start(out=w_raw[:].rearrange("p n j d -> p n (j d)"), in_=Wd.rearrange("n (p j) d -> p n (j d)", j=4))
-        nc.sync.dma_start(out=hb0[:, 2048:4096], in_=hid[0][:, 2048:4096])
+        nc.sync.dma_start(out=hb0[:, ROW:], in_=hid[0][:, ROW:])
         nc.sync.dma_start(out=scale_p[:], in_=srow.rearrange("(p t) -> p t", t=4))
-        make_identity(nc, ident_b[:])
         make_identity(nc, ident[:])
         nc.vector.memset(wo_scales[:].bitcast(I32), 0)
-        nc.vector.memset(wz_codes[:].rearrange("p t z -> p (t z)").bitcast(I32), 0)
         load_hid(1)
         nc.sync.dma_start(out=wo_words[:], in_=Wo_words[0])
         wos = Wo_scales[0].bitcast(I32)
@@ -106,67 +93,40 @@ def tile_mopn_layer_pb_t_w4_kernel(tc, hid_bytes, hid_scale, Wd, Wo_words, Wo_sc
             load_hid(j)
             load_x(j - 1)
 
-        w_grp = []
-
         def group_w():
-            grp = ring.tile([P, 4, NS, 32, 4], BF16, name="ring", align_bytes=64)
-            nc.vector.tensor_copy(out=grp[:], in_=w_raw[:].rearrange("p n j (m t) -> p t n m j", t=4))
-            w_grp.append(grp)
+            nc.vector.tensor_copy(out=w_grp[:], in_=w_raw[:].rearrange("p n j d -> p n d j"))
 
         def quant_w():
-            nc.vector.quantize_mx(
-                out=w_codes[:].rearrange("p t n m -> p (t n m)").bitcast(F8X4),
-                scales=w_scales[:],
-                in_=w_grp[0][:].rearrange("p t n m j -> p (t n m j)"),
-            )
+            nc.vector.quantize_mx(out=w_codes[:].bitcast(F8X4), scales=w_scales[:], in_=w_grp[:].rearrange("p n d j -> p (n d j)"))
 
-        def pad_w():
-            nc.vector.tensor_copy(
-                out=wz_codes[:].rearrange("p t (n z) -> p t n z", z=160)[:, :, :, 0:32].bitcast(I32), in_=w_codes[:].bitcast(I32)
-            )
-
-        xs_t, xt_t, g_t, c_t, s_t, jp_t, jg_t, jc_t, js_t, po_t, o_t, pw_t = ({} for z in range(12))
+        xs_t, xt_t, g_t, c_t, s_t, jp_t, jb_t, jt_t, jg_t, jc_t, js_t, po_t, o_t, pw_t = ({} for z in range(14))
 
         def m_s(i):
-            return M_FIRST if i < N_FIRST else M_LAST if i >= TILES - N_LAST else M_S
+            return M_LAST if i >= TILES - N_LAST else M_S
 
         def split(i):
-            return E_COLS if i < V_TILES else F_COLS if i < F_TILES else G_COLS
+            return F_COLS if i < F_TILES else G_COLS
 
         def widen_g(i):
-            xs = ring.tile([P, 2 * HALF], BF16, name="ring", align_bytes=64)
-            base = (i % 2) * NS * H
+            xs = ring.tile([P, ROW], BF16, name="ring", align_bytes=64)
+            base = (i % 2) * ROW
             eng = nc.vector if i < V_TILES else nc.gpsimd
             cut = split(i)
-            eng.tensor_copy(out=xs[:, 2 * HALF - cut :], in_=hbs[i // 2][:, base + 2 * HALF - cut : base + 2 * HALF].bitcast(F8))
+            eng.tensor_copy(out=xs[:, ROW - cut :], in_=hbs[i // 2][:, base + ROW - cut : base + ROW].bitcast(F8))
             xs_t[i] = xs
 
         def widen_s(i):
-            base = (i % 2) * NS * H
+            base = (i % 2) * ROW
             cut = split(i)
-            nc.scalar.copy(out=xs_t[i][:, 0 : 2 * HALF - cut], in_=hbs[i // 2][:, base : base + 2 * HALF - cut].bitcast(F8))
+            nc.scalar.copy(out=xs_t[i][:, 0 : ROW - cut], in_=hbs[i // 2][:, base : base + ROW - cut].bitcast(F8))
 
         def turn(i):
             words = xs_t[i][:].bitcast(F32)
-            banks = [pst.tile([P, 2, 2, P], F32, name="xt%d" % h) for h in range(2)]
+            banks = [two.tile([P, 2, 2, P], F32, name="xt%d" % h) for h in range(2)]
             xt_t[i] = banks
-
-            def plane(e):
-                nc.tensor.matmul(
-                    out=banks[1][:, 1, 1, :].bitcast(BF16)[:, P * e : P * (e + 1)],
-                    lhsT=xs_t[i][:, 3 * H + 2 + e : 4 * H : 4],
-                    rhs=ident_b[:],
-                    start=True,
-                    stop=True,
-                )
-
-            if i >= P_FROM:
-                plane(0)
             for n in reversed(range(NS)):
-                for u in range(1 if n == 3 and i >= P_FROM else 2):
+                for u in range(2):
                     nc.tensor.transpose(banks[n // 2][:, u, n % 2, :], words[:, 256 * n + u : 256 * (n + 1) : 2], ident[:])
-            if i >= P_FROM:
-                plane(1)
 
         def bank_view(i, h):
             return xt_t[i][h][:].rearrange("p u a r -> p (u a r)").bitcast(BF16).rearrange("p (u m e) -> p u m e", u=2, e=2)
@@ -177,17 +137,11 @@ def tile_mopn_layer_pb_t_w4_kernel(tc, hid_bytes, hid_scale, Wd, Wo_words, Wo_sc
             lo = 2 * P - m_s(i)
             for e in range(2):
                 for u in range(2):
-                    col = scale_p[:, 2 * u + e : 2 * u + e + 1]
-                    if u == 1 and i >= P_FROM:
-                        nc.scalar.activation(out=pw[:, u, 0 : P - lo, e], in_=src[:, u, lo:P, e], func=COPY, scale=col)
-                        flat = xt_t[i][1][:, 1, 1, :].bitcast(BF16)
-                        nc.scalar.activation(out=pw[:, u, P - lo :, e], in_=flat[:, P * e : P * (e + 1)], func=COPY, scale=col)
-                    else:
-                        nc.scalar.activation(out=pw[:, u, :, e], in_=src[:, u, lo:, e], func=COPY, scale=col)
+                    nc.scalar.activation(out=pw[:, u, :, e], in_=src[:, u, lo:, e], func=COPY, scale=scale_p[:, 2 * u + e : 2 * u + e + 1])
             pw_t[i] = pw
 
         def empty_v(i):
-            g = sb.tile([P, 2 * HALF], BF16, name="g", align_bytes=64)
+            g = sb.tile([P, ROW], BF16, name="g", align_bytes=64)
             for h, m in ((0, 2 * P), (1, 2 * P - m_s(i))):
                 if m == 0:
                     continue
@@ -201,7 +155,7 @@ def tile_mopn_layer_pb_t_w4_kernel(tc, hid_bytes, hid_scale, Wd, Wo_words, Wo_sc
 
         def weave(i):
             nc.vector.tensor_copy(
-                out=g_t[i][:, 2 * HALF - 4 * m_s(i) :].bitcast(F32).rearrange("p (m u) -> p m u", u=2),
+                out=g_t[i][:, ROW - 4 * m_s(i) :].bitcast(F32).rearrange("p (m u) -> p m u", u=2),
                 in_=pw_t[i][:].rearrange("p u m e -> p (u m e)").bitcast(F32).rearrange("p (u m) -> p m u", u=2),
             )
 
@@ -211,34 +165,46 @@ def tile_mopn_layer_pb_t_w4_kernel(tc, hid_bytes, hid_scale, Wd, Wo_words, Wo_sc
             nc.vector.quantize_mx(out=c[:].bitcast(F8X4), scales=s[:], in_=g_t[i][:])
             c_t[i], s_t[i] = c, s
 
-        def mm1(i):
-            jp = pst.tile([P, 4, P], F32, name="jp")
+        def down(i):
+            jp = two.tile([P, D], F32, name="xt0") if i >= TILES - 2 else one.tile([P, D], F32, name="jp")
             jp_t[i] = jp
-            for t in range(4):
-                for n in range(NS):
-                    nc.tensor.matmul_mx(
-                        out=jp[:, t, :],
-                        lhsT=wz_codes[:, t, P * n : P * (n + 1)].bitcast(F8X4),
-                        lhsT_scale=w_scales[:, P * t : P * (t + 1)],
-                        rhs=c_t[i][:, P * n : P * (n + 1)].bitcast(F8X4),
-                        rhs_scale=s_t[i][:, P * n : P * (n + 1)],
-                        start=(n == 0),
-                        stop=(n == NS - 1),
-                    )
+            for n in range(NS):
+                cols = slice(P * n, P * (n + 1))
+                nc.tensor.matmul_mx(
+                    out=jp[:, cols],
+                    lhsT=c_t[i][:, cols].bitcast(F8X4),
+                    lhsT_scale=s_t[i][:, cols],
+                    rhs=w_codes[:, cols].bitcast(F8X4),
+                    rhs_scale=w_scales[:, cols],
+                    start=True,
+                    stop=True,
+                )
+
+        def round_j(i):
+            jb = sb.tile([P, 2, P, 2], BF16, name="jb", align_bytes=64)
+            jb_t[i] = jb
+            nc.scalar.copy(out=jb[:], in_=jp_t[i][:].rearrange("r (p u e) -> r u p e", u=2, e=2))
+
+        def turn_j(i):
+            words = jb_t[i][:].rearrange("r u p e -> r (u p e)").bitcast(F32)
+            jt = two.tile([P, 2, P], F32, name="xt1") if i in (TILES - 4, TILES - 2) else one.tile([P, 2, P], F32, name="jt")
+            jt_t[i] = jt
+            for u in range(2):
+                nc.tensor.transpose(jt[:, u, :], words[:, P * u : P * (u + 1)], ident[:])
 
         def empty_j(i):
-            jg = sb.tile([P, P, 4], BF16, name="jg", align_bytes=64)
+            jg = sb.tile([P, P, 2], F32, name="jg", align_bytes=64)
             jg_t[i] = jg
-            nc.scalar.copy(out=jg[:], in_=jp_t[i][:].rearrange("p t r -> p r t"))
+            nc.scalar.copy(out=jg[:], in_=jt_t[i][:].rearrange("p u r -> p r u"))
 
         def quant_j(i):
             c = sb.tile([P, P], U32, name="jcodes", align_bytes=64)
             s = sb.tile([P, P], U8, name="jscales", align_bytes=64)
-            nc.vector.quantize_mx(out=c[:].bitcast(F8X4), scales=s[:], in_=jg_t[i][:].rearrange("p r t -> p (r t)"))
+            nc.vector.quantize_mx(out=c[:].bitcast(F8X4), scales=s[:], in_=jg_t[i][:].rearrange("p r u -> p (r u)").bitcast(BF16))
             jc_t[i], js_t[i] = c, s
 
-        def mm2(i):
-            po = pst.tile([P, D], F32, name="po")
+        def mix(i):
+            po = two.tile([P, D], F32, name="po")
             nc.tensor.matmul_mx(
                 out=po[:],
                 lhsT=jc_t[i][:].bitcast(F8X4),
@@ -254,37 +220,34 @@ def tile_mopn_layer_pb_t_w4_kernel(tc, hid_bytes, hid_scale, Wd, Wo_words, Wo_sc
             if i % 2 == 0:
                 o_t[i // 2] = sb.tile([P, 2 * D], F32, name="o", align_bytes=64)
             o = o_t[i // 2]
-            parts = SPLIT_LAST if i == TILES - 1 else 1
-            for c in range(0, D, D // parts):
-                cols = slice((i % 2) * D + c, (i % 2) * D + c + D // parts)
-                nc.vector.tensor_tensor(out=o[:, cols], in0=po_t[i][:, c : c + D // parts], in1=xts[i // 2][:, cols], op=ADD)
-                if i >= TILES - 2:
-                    nc.sync.dma_start(out=oview[i // 2][:, cols], in_=o[:, cols])
-            if i < TILES - 2 and i % 2 == 1:
+            cols = slice((i % 2) * D, (i % 2 + 1) * D)
+            nc.vector.tensor_tensor(out=o[:, cols], in0=po_t[i][:], in1=xts[i // 2][:, cols], op=ADD)
+            if i >= TILES - 4:
+                nc.sync.dma_start(out=oview[i // 2][:, cols], in_=o[:, cols])
+            elif i % 2 == 1:
                 nc.sync.dma_start(out=oview[i // 2], in_=o[:])
 
         STAGES = [
             (turn, 0),
+            (turn_j, 5),
+            (round_j, 4),
             (empty_s, 1),
-            (empty_j, LAG_M + 1),
-            (quant_j, LAG_M + LAG_J),
-            (weave, LAG_W),
-            (quant, LAG_Q),
+            (empty_j, 5),
+            (quant_j, 6),
+            (weave, 2),
+            (quant, 3),
             (widen_g, -1),
             (widen_s, -1),
             (empty_v, 1),
-            (mm2, LAG_M + LAG_J),
-            (mm1, LAG_M),
-            (add, LAG_M + LAG_J + LAG_A),
+            (mix, 6),
+            (down, 3),
+            (add, 7),
         ]
-        last = TILES if DRAIN else TILES + LAG_M + LAG_J + LAG_A
-        for i in range(-1, last):
+        for i in range(-1, TILES):
             if i % 2 == 0 and i // 2 + 5 < PAIRS and i >= 0:
                 load_hid(i // 2 + 5)
-            if i % 2 == 0 and i // 2 + 4 < PAIRS and i >= 0:
-                load_x(i // 2 + 4)
-            if i == 2:
-                pad_w()
+            if i % 2 == 0 and i // 2 + 3 < PAIRS and i >= 2:
+                load_x(i // 2 + 3)
             for stage, lag in STAGES:
                 if 0 <= i - lag < TILES:
                     stage(i - lag)
@@ -292,30 +255,42 @@ def tile_mopn_layer_pb_t_w4_kernel(tc, hid_bytes, hid_scale, Wd, Wo_words, Wo_sc
                 group_w()
             if i == 0:
                 quant_w()
-        if DRAIN:
-            n = TILES
-            empty_s(n - 1)
-            empty_j(n - 4)
-            weave(n - 2)
-            quant(n - 3)
-            mm1(n - 3)
-            quant_j(n - 5)
-            mm2(n - 5)
-            quant(n - 2)
-            empty_v(n - 1)
-            add(n - 6)
-            empty_j(n - 3)
-            mm1(n - 2)
-            weave(n - 1)
-            quant_j(n - 4)
-            mm2(n - 4)
-            quant(n - 1)
-            empty_j(n - 2)
-            mm1(n - 1)
-            empty_j(n - 1)
-            add(n - 5)
-            for i in range(n - 3, n):
-                quant_j(i)
-                add(i - 1)
-                mm2(i)
-            add(n - 1)
+        n = TILES
+        turn_j(n - 5)
+        round_j(n - 4)
+        empty_s(n - 1)
+        quant_j(n - 6)
+        weave(n - 2)
+        quant(n - 3)
+        mix(n - 6)
+        empty_j(n - 5)
+        turn_j(n - 4)
+        down(n - 3)
+        empty_v(n - 1)
+        add(n - 7)
+        quant(n - 2)
+        round_j(n - 3)
+        empty_j(n - 4)
+        turn_j(n - 3)
+        down(n - 2)
+        weave(n - 1)
+        quant_j(n - 5)
+        quant(n - 1)
+        mix(n - 5)
+        down(n - 1)
+        empty_j(n - 3)
+        round_j(n - 2)
+        add(n - 6)
+        quant_j(n - 4)
+        mix(n - 4)
+        turn_j(n - 2)
+        round_j(n - 1)
+        empty_j(n - 2)
+        turn_j(n - 1)
+        empty_j(n - 1)
+        add(n - 5)
+        for i in range(n - 3, n):
+            quant_j(i)
+            add(i - 1)
+            mix(i)
+        add(n - 1)

@@ -24,14 +24,14 @@ ROW = NS * H
 HALF = 2 * H
 TILES = TOKENS // P
 PAIRS = TILES // 2
-V_TILES = 3
-RING = 5
-F_COLS = 1024
-F_TILES = 6
-M_S = 192
-M_LAST = 192
-N_LAST = 2
-G_COLS = 1344
+V_COLS = 1280
+G_COLS = 1472
+G_FILL = 1152
+M_A = 256
+M_B = 144
+M_A_FILL = 192
+M_B_FILL = 128
+N_FILL = 3
 FLOPS = 2 * TOKENS * NS * H * DS + 2 * TOKENS * D * D
 
 
@@ -44,11 +44,10 @@ def tile_mopn_layer_pb_t_w4_kernel(tc, hid_bytes, hid_scale, Wd, Wo_words, Wo_sc
 
     with ExitStack() as ctx:
         keep = ctx.enter_context(tc.tile_pool(name="keep", bufs=1))
-        loads = ctx.enter_context(tc.tile_pool(name="loads", bufs=8))
-        sb = ctx.enter_context(tc.tile_pool(name="sb", bufs=6))
-        ring = ctx.enter_context(tc.tile_pool(name="ring", bufs=RING))
-        two = ctx.enter_context(tc.psum_pool(name="two", bufs=2))
-        one = ctx.enter_context(tc.psum_pool(name="one", bufs=1))
+        loads = ctx.enter_context(tc.tile_pool(name="loads", bufs=5))
+        sb = ctx.enter_context(tc.tile_pool(name="sb", bufs=3))
+        ring = ctx.enter_context(tc.tile_pool(name="ring", bufs=3))
+        ps = ctx.enter_context(tc.psum_pool(name="ps", bufs=2))
 
         ctx.enter_context(tc.manual_schedule())
 
@@ -60,38 +59,34 @@ def tile_mopn_layer_pb_t_w4_kernel(tc, hid_bytes, hid_scale, Wd, Wo_words, Wo_sc
         w_scales = keep.tile([P, D], U8, align_bytes=64)
         wo_words = keep.tile([P, 2 * D], U8, align_bytes=64)
         wo_scales = keep.tile([P, D], U8, align_bytes=64)
+        xs_first = keep.tile([P, 2 * ROW], BF16, align_bytes=64)
 
-        hbs = {}
-        xts = {}
+        hb_t, x_t, xs_t, xt_t, g_t, c_t, s_t, jp_t, jb_t, jt_t, jg_t, jc_t, js_t, po_t, o_t, pw_t = ({} for z in range(16))
 
-        def load_hid(j):
-            hb = loads.tile([P, 2 * ROW], U8, name="hb", align_bytes=64)
-            nc.sync.dma_start(out=hb[:], in_=hid[j])
-            hbs[j] = hb
+        def load_hid(k, cuts=(0, 2 * ROW)):
+            hb_t[k] = loads.tile([P, 2 * ROW], U8, name="hb", align_bytes=64)
+            for lo, hi in zip(cuts[0::2], cuts[1::2]):
+                nc.sync.dma_start(out=hb_t[k][:, lo:hi], in_=hid[k][:, lo:hi])
 
-        def load_x(j):
-            xt = loads.tile([P, 2 * D], BF16, align_bytes=64)
-            nc.sync.dma_start(out=xt[:], in_=xin[j])
-            xts[j] = xt
+        def load_x(k):
+            x_t[k] = loads.tile([P, 2 * D], BF16, name="x", align_bytes=64)
+            nc.sync.dma_start(out=x_t[k][:], in_=xin[k])
 
-        hb0 = loads.tile([P, 2 * ROW], U8, name="hb", align_bytes=64)
-        hbs[0] = hb0
-        for c in (HALF, 0):
-            nc.sync.dma_start(out=hb0[:, c : c + HALF], in_=hid[0][:, c : c + HALF])
-        nc.sync.dma_start(out=w_raw[:].rearrange("p n j d -> p n (j d)"), in_=Wd.rearrange("n (p j) d -> p n (j d)", j=4))
-        nc.sync.dma_start(out=hb0[:, ROW:], in_=hid[0][:, ROW:])
+        cut = ROW - V_COLS
+        load_hid(0, (cut, ROW, 0, cut, ROW, 2 * ROW))
         nc.sync.dma_start(out=scale_p[:], in_=srow.rearrange("(p t) -> p t", t=4))
+        load_hid(1)
+        nc.sync.dma_start(out=w_raw[:].rearrange("p n j d -> p n (j d)"), in_=Wd.rearrange("n (p j) d -> p n (j d)", j=4))
+        load_hid(2)
         make_identity(nc, ident[:])
         nc.vector.memset(wo_scales[:].bitcast(I32), 0)
-        load_hid(1)
         nc.sync.dma_start(out=wo_words[:], in_=Wo_words[0])
         wos = Wo_scales[0].bitcast(I32)
         for q in range(4):
             nc.sync.dma_start(out=wo_scales[32 * q : 32 * q + 4, :].bitcast(I32), in_=wos[4 * q : 4 * q + 4, :])
         load_x(0)
-        for j in range(2, 5):
-            load_hid(j)
-            load_x(j - 1)
+        load_hid(3)
+        load_x(1)
 
         def group_w():
             nc.vector.tensor_copy(out=w_grp[:], in_=w_raw[:].rearrange("p n j d -> p n d j"))
@@ -99,198 +94,238 @@ def tile_mopn_layer_pb_t_w4_kernel(tc, hid_bytes, hid_scale, Wd, Wo_words, Wo_sc
         def quant_w():
             nc.vector.quantize_mx(out=w_codes[:].bitcast(F8X4), scales=w_scales[:], in_=w_grp[:].rearrange("p n d j -> p (n d j)"))
 
-        xs_t, xt_t, g_t, c_t, s_t, jp_t, jb_t, jt_t, jg_t, jc_t, js_t, po_t, o_t, pw_t = ({} for z in range(14))
-
         def m_s(i):
-            return M_LAST if i >= TILES - N_LAST else M_S
+            return (M_A_FILL, M_B_FILL)[i % 2] if i // 2 < N_FILL else (M_A, M_B)[i % 2]
 
-        def split(i):
-            return F_COLS if i < F_TILES else G_COLS
+        def wide(k):
+            return V_COLS if k == 0 else G_FILL if k <= N_FILL else G_COLS
 
-        def widen_g(i):
-            xs = ring.tile([P, ROW], BF16, name="ring", align_bytes=64)
-            base = (i % 2) * ROW
-            eng = nc.vector if i < V_TILES else nc.gpsimd
-            cut = split(i)
-            eng.tensor_copy(out=xs[:, ROW - cut :], in_=hbs[i // 2][:, base + ROW - cut : base + ROW].bitcast(F8))
-            xs_t[i] = xs
+        def widen(eng, k, lo, hi):
+            eng(out=xs_t[k][:, lo:hi], in_=hb_t[k][:, lo:hi].bitcast(F8))
+
+        def widen_g(k):
+            xs_t[k] = ring.tile([P, 2 * ROW], BF16, name="ring", align_bytes=64)
+            widen(nc.gpsimd.tensor_copy, k, ROW - wide(k), ROW + wide(k))
 
         def widen_s(i):
-            base = (i % 2) * ROW
-            cut = split(i)
-            nc.scalar.copy(out=xs_t[i][:, 0 : ROW - cut], in_=hbs[i // 2][:, base : base + ROW - cut].bitcast(F8))
+            k = i // 2
+            if i % 2 == 0:
+                widen(nc.scalar.copy, k, 0, ROW - wide(k))
+            else:
+                widen(nc.scalar.copy, k, ROW + wide(k), 2 * ROW)
+
+        def space(i, h, a):
+            return 2 * h + a if i % 2 == 0 else 3 - 2 * h - a
 
         def turn(i):
-            words = xs_t[i][:].bitcast(F32)
-            banks = [two.tile([P, 2, 2, P], F32, name="xt%d" % h) for h in range(2)]
-            xt_t[i] = banks
-            for n in reversed(range(NS)):
-                for u in range(2):
-                    nc.tensor.transpose(banks[n // 2][:, u, n % 2, :], words[:, 256 * n + u : 256 * (n + 1) : 2], ident[:])
+            words = xs_t[i // 2][:, (i % 2) * ROW : (i % 2 + 1) * ROW].bitcast(F32)
+            xt_t[i] = [ps.tile([P, 2, 2, P], F32, name="xt%d" % h) for h in range(2)]
+            for h in (1, 0):
+                for a in (1, 0):
+                    n = space(i, h, a)
+                    for u in range(2):
+                        nc.tensor.transpose(xt_t[i][h][:, u, a, :], words[:, 256 * n + u : 256 * (n + 1) : 2], ident[:])
 
         def bank_view(i, h):
             return xt_t[i][h][:].rearrange("p u a r -> p (u a r)").bitcast(BF16).rearrange("p (u m e) -> p u m e", u=2, e=2)
 
         def empty_s(i):
-            pw = ring.tile([P, 2, m_s(i), 2], BF16, name="ring", align_bytes=64)
+            pw_t[i] = sb.tile([P, 2, m_s(i), 2], BF16, name="pw", bufs=4, align_bytes=64)
             src = bank_view(i, 1)
             lo = 2 * P - m_s(i)
             for e in range(2):
                 for u in range(2):
-                    nc.scalar.activation(out=pw[:, u, :, e], in_=src[:, u, lo:, e], func=COPY, scale=scale_p[:, 2 * u + e : 2 * u + e + 1])
-            pw_t[i] = pw
+                    nc.scalar.activation(out=pw_t[i][:, u, :, e], in_=src[:, u, lo:, e], func=COPY, scale=scale_p[:, 2 * u + e : 2 * u + e + 1])
 
-        def empty_v(i):
-            g = sb.tile([P, ROW], BF16, name="g", align_bytes=64)
-            for h, m in ((0, 2 * P), (1, 2 * P - m_s(i))):
-                if m == 0:
-                    continue
-                nc.vector.tensor_tensor(
-                    out=g[:, HALF * h : HALF * h + 4 * m].rearrange("p (m u e) -> p m u e", u=2, e=2),
-                    in0=bank_view(i, h)[:, :, 0:m, :].rearrange("p u m e -> p m u e"),
-                    in1=scale_p[:].rearrange("p (u e) -> p u e", u=2).unsqueeze(1).to_broadcast([P, m, 2, 2]),
-                    op=MULT,
-                )
-            g_t[i] = g
+        def empty_v(i, halves=(0, 1)):
+            k = i // 2
+            if k not in g_t:
+                g_t[k] = ring.tile([P, 2 * ROW], BF16, name="ring", align_bytes=64)
+            for h in halves:
+                m = 2 * P - h * m_s(i)
+                lo = (i % 2) * ROW + HALF * h
+                if m > 0:
+                    nc.vector.tensor_tensor(
+                        out=g_t[k][:, lo : lo + 4 * m].rearrange("p (m u e) -> p m u e", u=2, e=2),
+                        in0=bank_view(i, h)[:, :, 0:m, :].rearrange("p u m e -> p m u e"),
+                        in1=scale_p[:].rearrange("p (u e) -> p u e", u=2).unsqueeze(1).to_broadcast([P, m, 2, 2]),
+                        op=MULT,
+                    )
 
         def weave(i):
+            hi = (i % 2 + 1) * ROW
             nc.vector.tensor_copy(
-                out=g_t[i][:, ROW - 4 * m_s(i) :].bitcast(F32).rearrange("p (m u) -> p m u", u=2),
+                out=g_t[i // 2][:, hi - 4 * m_s(i) : hi].bitcast(F32).rearrange("p (m u) -> p m u", u=2),
                 in_=pw_t[i][:].rearrange("p u m e -> p (u m e)").bitcast(F32).rearrange("p (u m) -> p m u", u=2),
             )
 
-        def quant(i):
-            c = sb.tile([P, 512], U32, name="codes", align_bytes=64)
-            s = sb.tile([P, 512], U8, name="scales", align_bytes=64)
-            nc.vector.quantize_mx(out=c[:].bitcast(F8X4), scales=s[:], in_=g_t[i][:])
-            c_t[i], s_t[i] = c, s
+        def quant(*tiles):
+            lo, wid = (tiles[0] % 2) * ROW, len(tiles) * ROW
+            codes = sb.tile([P, wid // 4], U32, name="codes", align_bytes=64)
+            scales = sb.tile([P, wid // 4], U8, name="scales", align_bytes=64)
+            nc.vector.quantize_mx(out=codes[:].bitcast(F8X4), scales=scales[:], in_=g_t[tiles[0] // 2][:, lo : lo + wid])
+            for z, i in enumerate(tiles):
+                c_t[i], s_t[i] = codes[:, D * z : D * (z + 1)], scales[:, D * z : D * (z + 1)]
 
-        def down(i):
-            jp = two.tile([P, D], F32, name="xt0") if i >= TILES - 2 else one.tile([P, D], F32, name="jp")
-            jp_t[i] = jp
-            for n in range(NS):
-                cols = slice(P * n, P * (n + 1))
-                nc.tensor.matmul_mx(
-                    out=jp[:, cols],
-                    lhsT=c_t[i][:, cols].bitcast(F8X4),
-                    lhsT_scale=s_t[i][:, cols],
-                    rhs=w_codes[:, cols].bitcast(F8X4),
-                    rhs_scale=w_scales[:, cols],
-                    start=True,
-                    stop=True,
-                )
+        def down(i, tag="jp"):
+            jp_t[i] = ps.tile([P, D], F32, name=tag)
+            for h in range(2):
+                for a in range(2):
+                    n = space(i, h, a)
+                    tok = slice(P * (2 * h + a), P * (2 * h + a + 1))
+                    chan = slice(P * n, P * (n + 1))
+                    nc.tensor.matmul_mx(
+                        out=jp_t[i][:, chan],
+                        lhsT=c_t[i][:, tok].bitcast(F8X4),
+                        lhsT_scale=s_t[i][:, tok],
+                        rhs=w_codes[:, chan].bitcast(F8X4),
+                        rhs_scale=w_scales[:, chan],
+                        start=True,
+                        stop=True,
+                    )
 
         def round_j(i):
-            jb = sb.tile([P, 2, P, 2], BF16, name="jb", align_bytes=64)
-            jb_t[i] = jb
-            nc.scalar.copy(out=jb[:], in_=jp_t[i][:].rearrange("r (p u e) -> r u p e", u=2, e=2))
+            jb_t[i] = sb.tile([P, 2, P, 2], BF16, name="jb", bufs=4, align_bytes=64)
+            nc.scalar.copy(out=jb_t[i][:], in_=jp_t[i][:].rearrange("r (p u e) -> r u p e", u=2, e=2))
 
-        def turn_j(i):
-            words = jb_t[i][:].rearrange("r u p e -> r (u p e)").bitcast(F32)
-            jt = two.tile([P, 2, P], F32, name="xt1") if i in (TILES - 4, TILES - 2) else one.tile([P, 2, P], F32, name="jt")
-            jt_t[i] = jt
-            for u in range(2):
-                nc.tensor.transpose(jt[:, u, :], words[:, P * u : P * (u + 1)], ident[:])
+        def turn_j(*tiles):
+            jt_t[tiles] = ps.tile([P, 2, len(tiles), P], F32, name="jp")
+            for z, i in enumerate(tiles):
+                words = jb_t[i][:].rearrange("r u p e -> r (u p e)").bitcast(F32)
+                for u in range(2):
+                    nc.tensor.transpose(jt_t[tiles][:, u, z, :], words[:, P * u : P * (u + 1)], ident[:])
 
-        def empty_j(i):
-            jg = sb.tile([P, P, 2], F32, name="jg", align_bytes=64)
-            jg_t[i] = jg
-            nc.scalar.copy(out=jg[:], in_=jt_t[i][:].rearrange("p u r -> p r u"))
+        def empty_j(*tiles):
+            jg_t[tiles] = sb.tile([P, len(tiles) * P, 2], F32, name="jg", align_bytes=64)
+            nc.scalar.copy(out=jg_t[tiles][:], in_=jt_t[tiles][:].rearrange("p u i r -> p (i r) u"))
 
-        def quant_j(i):
-            c = sb.tile([P, P], U32, name="jcodes", align_bytes=64)
-            s = sb.tile([P, P], U8, name="jscales", align_bytes=64)
-            nc.vector.quantize_mx(out=c[:].bitcast(F8X4), scales=s[:], in_=jg_t[i][:].rearrange("p r u -> p (r u)").bitcast(BF16))
-            jc_t[i], js_t[i] = c, s
+        def quant_j(*tiles):
+            codes = sb.tile([P, len(tiles) * P], U32, name="jcodes", align_bytes=64)
+            scales = sb.tile([P, len(tiles) * P], U8, name="jscales", align_bytes=64)
+            nc.vector.quantize_mx(out=codes[:].bitcast(F8X4), scales=scales[:], in_=jg_t[tiles][:].rearrange("p r u -> p (r u)").bitcast(BF16))
+            for z, i in enumerate(tiles):
+                jc_t[i], js_t[i] = codes[:, P * z : P * (z + 1)], scales[:, P * z : P * (z + 1)]
 
-        def mix(i):
-            po = two.tile([P, D], F32, name="po")
+        def mix(i, tag="po"):
+            po_t[i] = ps.tile([P, D], F32, name=tag)
             nc.tensor.matmul_mx(
-                out=po[:],
-                lhsT=jc_t[i][:].bitcast(F8X4),
-                lhsT_scale=js_t[i][:],
+                out=po_t[i][:],
+                lhsT=jc_t[i].bitcast(F8X4),
+                lhsT_scale=js_t[i],
                 rhs=wo_words[:].bitcast(F4X4),
                 rhs_scale=wo_scales[:],
                 start=True,
                 stop=True,
             )
-            po_t[i] = po
 
         def add(i):
+            k = i // 2
             if i % 2 == 0:
-                o_t[i // 2] = sb.tile([P, 2 * D], F32, name="o", align_bytes=64)
-            o = o_t[i // 2]
+                o_t[k] = sb.tile([P, 2 * D], F32, name="o", align_bytes=64)
             cols = slice((i % 2) * D, (i % 2 + 1) * D)
-            nc.vector.tensor_tensor(out=o[:, cols], in0=po_t[i][:], in1=xts[i // 2][:, cols], op=ADD)
-            if i >= TILES - 4:
-                nc.sync.dma_start(out=oview[i // 2][:, cols], in_=o[:, cols])
+            nc.vector.tensor_tensor(out=o_t[k][:, cols], in0=po_t[i][:], in1=x_t[k][:, cols], op=ADD)
+            if k >= PAIRS - 2:
+                nc.sync.dma_start(out=oview[k][:, cols], in_=o_t[k][:, cols])
             elif i % 2 == 1:
-                nc.sync.dma_start(out=oview[i // 2], in_=o[:])
+                nc.sync.dma_start(out=oview[k], in_=o_t[k][:])
 
-        STAGES = [
-            (turn, 0),
-            (turn_j, 5),
-            (round_j, 4),
-            (empty_s, 1),
-            (empty_j, 5),
-            (quant_j, 6),
-            (weave, 2),
-            (quant, 3),
-            (widen_g, -1),
-            (widen_s, -1),
-            (empty_v, 1),
-            (mix, 6),
-            (down, 3),
-            (add, 7),
-        ]
-        for i in range(-1, TILES):
-            if i % 2 == 0 and i // 2 + 5 < PAIRS and i >= 0:
-                load_hid(i // 2 + 5)
-            if i % 2 == 0 and i // 2 + 3 < PAIRS and i >= 2:
-                load_x(i // 2 + 3)
-            for stage, lag in STAGES:
-                if 0 <= i - lag < TILES:
-                    stage(i - lag)
-            if i == -1:
-                group_w()
-            if i == 0:
+        xs_t[0] = xs_first
+        widen(nc.vector.tensor_copy, 0, ROW - V_COLS, ROW)
+        widen_s(0)
+        widen(nc.vector.tensor_copy, 0, ROW, ROW + V_COLS)
+        widen_s(1)
+        turn(0)
+        turn(1)
+        empty_v(0, (1,))
+        widen_g(1)
+        empty_s(0)
+        empty_v(0, (0,))
+        empty_s(1)
+        widen_s(2)
+        widen_s(3)
+        empty_v(1)
+        group_w()
+
+        BACK = 3
+        for p in range(1, PAIRS - 1):
+            a, b = 2 * p, 2 * p + 1
+            c, d = a - 2 * BACK, b - 2 * BACK
+            if p + 3 < PAIRS:
+                load_hid(p + 3)
+            if p >= 2:
+                load_x(p)
+            turn(a)
+            turn(b)
+            weave(a - 2)
+            weave(b - 2)
+            if p == 1:
                 quant_w()
+            if c >= 0:
+                quant_j(c, d)
+            quant(a - 2, b - 2)
+            empty_s(a)
+            empty_v(a)
+            empty_s(b)
+            widen_g(p + 1)
+            down(a - 2)
+            down(b - 2)
+            if c >= 0:
+                mix(c)
+                mix(d)
+            round_j(a - 2)
+            round_j(b - 2)
+            turn_j(a - 2, b - 2)
+            widen_s(a + 2)
+            empty_j(a - 2, b - 2)
+            widen_s(b + 2)
+            empty_v(b)
+            if c >= 0:
+                add(c)
+                add(d)
         n = TILES
-        turn_j(n - 5)
-        round_j(n - 4)
+        load_x(PAIRS - 1)
+        turn(n - 2)
+        turn(n - 1)
+        weave(n - 4)
+        weave(n - 3)
+        quant_j(n - 8, n - 7)
+        quant(n - 4, n - 3)
+        empty_s(n - 2)
+        empty_v(n - 2)
         empty_s(n - 1)
-        quant_j(n - 6)
-        weave(n - 2)
-        quant(n - 3)
-        mix(n - 6)
-        empty_j(n - 5)
-        turn_j(n - 4)
+        down(n - 4)
         down(n - 3)
-        empty_v(n - 1)
-        add(n - 7)
+        mix(n - 8)
+        mix(n - 7)
+        weave(n - 2)
+        empty_v(n - 1, (0,))
         quant(n - 2)
+        round_j(n - 4)
         round_j(n - 3)
-        empty_j(n - 4)
-        turn_j(n - 3)
         down(n - 2)
+        empty_v(n - 1, (1,))
         weave(n - 1)
-        quant_j(n - 5)
+        quant_j(n - 6, n - 5)
         quant(n - 1)
-        mix(n - 5)
-        down(n - 1)
-        empty_j(n - 3)
+        turn_j(n - 4, n - 3)
+        mix(n - 6, "xt0")
+        mix(n - 5, "xt1")
         round_j(n - 2)
-        add(n - 6)
-        quant_j(n - 4)
-        mix(n - 4)
-        turn_j(n - 2)
+        down(n - 1)
+        empty_j(n - 4, n - 3)
         round_j(n - 1)
-        empty_j(n - 2)
-        turn_j(n - 1)
-        empty_j(n - 1)
+        turn_j(n - 2, n - 1)
+        empty_j(n - 2, n - 1)
+        add(n - 8)
+        add(n - 7)
+        quant_j(n - 4, n - 3)
+        mix(n - 4, "xt0")
+        mix(n - 3, "xt1")
+        add(n - 6)
         add(n - 5)
+        add(n - 4)
+        quant_j(n - 2, n - 1)
+        mix(n - 2)
+        mix(n - 1)
         for i in range(n - 3, n):
-            quant_j(i)
-            add(i - 1)
-            mix(i)
-        add(n - 1)
+            add(i)

@@ -25,10 +25,10 @@ HALF = 2 * H
 TILES = TOKENS // P
 PAIRS = TILES // 2
 V_COLS = 1280
-G_COLS = 1472
+G_COLS = 1408
 G_FILL = 1152
 M_A = 256
-M_B = 144
+M_B = 192
 M_A_FILL = 192
 M_B_FILL = 128
 N_FILL = 3
@@ -54,7 +54,6 @@ def tile_mopn_layer_pb_t_w4_kernel(tc, hid_bytes, hid_scale, Wd, Wo_words, Wo_sc
         scale_p = keep.tile([P, 4], F32, align_bytes=64)
         ident = keep.tile([P, P], F32, align_bytes=64)
         w_raw = keep.tile([P, NS, 4, DS], BF16, align_bytes=64)
-        w_grp = keep.tile([P, NS, DS, 4], BF16, align_bytes=64)
         w_codes = keep.tile([P, D], U32, align_bytes=64)
         w_scales = keep.tile([P, D], U8, align_bytes=64)
         wo_words = keep.tile([P, 2 * D], U8, align_bytes=64)
@@ -87,6 +86,8 @@ def tile_mopn_layer_pb_t_w4_kernel(tc, hid_bytes, hid_scale, Wd, Wo_words, Wo_sc
         load_x(0)
         load_hid(3)
         load_x(1)
+
+        w_grp = ring.tile([P, NS, DS, 4], BF16, name="ring", align_bytes=64)
 
         def group_w():
             nc.vector.tensor_copy(out=w_grp[:], in_=w_raw[:].rearrange("p n j d -> p n d j"))
@@ -129,34 +130,55 @@ def tile_mopn_layer_pb_t_w4_kernel(tc, hid_bytes, hid_scale, Wd, Wo_words, Wo_sc
         def bank_view(i, h):
             return xt_t[i][h][:].rearrange("p u a r -> p (u a r)").bitcast(BF16).rearrange("p (u m e) -> p u m e", u=2, e=2)
 
+        def s_cols(i):
+            return slice(2 * P - m_s(i), 2 * P) if i % 2 == 0 else slice(0, m_s(i))
+
+        def v_cols(i, h):
+            if h == 0:
+                return slice(0, 2 * P)
+            return slice(0, 2 * P - m_s(i)) if i % 2 == 0 else slice(m_s(i), 2 * P)
+
+        def place(i, h):
+            return h if i % 2 == 0 else 1 - h
+
         def empty_s(i):
-            pw_t[i] = sb.tile([P, 2, m_s(i), 2], BF16, name="pw", bufs=4, align_bytes=64)
-            src = bank_view(i, 1)
-            lo = 2 * P - m_s(i)
+            k = i // 2
+            if i % 2 == 0:
+                pw_t[k] = sb.tile([P, 2, m_s(i) + m_s(i + 1), 2], BF16, name="pw", bufs=2, align_bytes=64)
+            lo = (i % 2) * m_s(2 * k)
             for e in range(2):
                 for u in range(2):
-                    nc.scalar.activation(out=pw_t[i][:, u, :, e], in_=src[:, u, lo:, e], func=COPY, scale=scale_p[:, 2 * u + e : 2 * u + e + 1])
+                    nc.scalar.activation(
+                        out=pw_t[k][:, u, lo : lo + m_s(i), e],
+                        in_=bank_view(i, 1)[:, u, s_cols(i), e],
+                        func=COPY,
+                        scale=scale_p[:, 2 * u + e : 2 * u + e + 1],
+                    )
 
         def empty_v(i, halves=(0, 1)):
             k = i // 2
             if k not in g_t:
-                g_t[k] = ring.tile([P, 2 * ROW], BF16, name="ring", align_bytes=64)
+                g_t[k] = ring.tile([P, 2 * ROW], BF16, name="ring", align_bytes=64) if k == 1 else sb.tile([P, 2 * ROW], BF16, name="g", bufs=2, align_bytes=64)
             for h in halves:
-                m = 2 * P - h * m_s(i)
-                lo = (i % 2) * ROW + HALF * h
+                cols = v_cols(i, h)
+                m = cols.stop - cols.start
+                lo = (i % 2) * ROW + HALF * place(i, h) + 4 * cols.start
                 if m > 0:
                     nc.vector.tensor_tensor(
                         out=g_t[k][:, lo : lo + 4 * m].rearrange("p (m u e) -> p m u e", u=2, e=2),
-                        in0=bank_view(i, h)[:, :, 0:m, :].rearrange("p u m e -> p m u e"),
+                        in0=bank_view(i, h)[:, :, cols, :].rearrange("p u m e -> p m u e"),
                         in1=scale_p[:].rearrange("p (u e) -> p u e", u=2).unsqueeze(1).to_broadcast([P, m, 2, 2]),
                         op=MULT,
                     )
 
-        def weave(i):
-            hi = (i % 2 + 1) * ROW
+        def weave(*tiles):
+            k = tiles[0] // 2
+            lo = (tiles[0] % 2) * m_s(2 * k)
+            m = sum(m_s(i) for i in tiles)
+            at = ROW - 4 * m_s(2 * k) + 4 * lo
             nc.vector.tensor_copy(
-                out=g_t[i // 2][:, hi - 4 * m_s(i) : hi].bitcast(F32).rearrange("p (m u) -> p m u", u=2),
-                in_=pw_t[i][:].rearrange("p u m e -> p (u m e)").bitcast(F32).rearrange("p (u m) -> p m u", u=2),
+                out=g_t[k][:, at : at + 4 * m].bitcast(F32).rearrange("p (m u) -> p m u", u=2),
+                in_=pw_t[k][:].rearrange("p u m e -> p u (m e)").bitcast(F32)[:, :, lo : lo + m].rearrange("p u m -> p m u"),
             )
 
         def quant(*tiles):
@@ -172,7 +194,7 @@ def tile_mopn_layer_pb_t_w4_kernel(tc, hid_bytes, hid_scale, Wd, Wo_words, Wo_sc
             for h in range(2):
                 for a in range(2):
                     n = space(i, h, a)
-                    tok = slice(P * (2 * h + a), P * (2 * h + a + 1))
+                    tok = slice(P * (2 * place(i, h) + a), P * (2 * place(i, h) + a + 1))
                     chan = slice(P * n, P * (n + 1))
                     nc.tensor.matmul_mx(
                         out=jp_t[i][:, chan],
@@ -196,7 +218,7 @@ def tile_mopn_layer_pb_t_w4_kernel(tc, hid_bytes, hid_scale, Wd, Wo_words, Wo_sc
                     nc.tensor.transpose(jt_t[tiles][:, u, z, :], words[:, P * u : P * (u + 1)], ident[:])
 
         def empty_j(*tiles):
-            jg_t[tiles] = sb.tile([P, len(tiles) * P, 2], F32, name="jg", align_bytes=64)
+            jg_t[tiles] = ring.tile([P, len(tiles) * P, 2], F32, name="ring", align_bytes=64)
             nc.scalar.copy(out=jg_t[tiles][:], in_=jt_t[tiles][:].rearrange("p u i r -> p (i r) u"))
 
         def quant_j(*tiles):
@@ -221,12 +243,14 @@ def tile_mopn_layer_pb_t_w4_kernel(tc, hid_bytes, hid_scale, Wd, Wo_words, Wo_sc
         def add(i):
             k = i // 2
             if i % 2 == 0:
-                o_t[k] = sb.tile([P, 2 * D], F32, name="o", align_bytes=64)
-            cols = slice((i % 2) * D, (i % 2 + 1) * D)
-            nc.vector.tensor_tensor(out=o_t[k][:, cols], in0=po_t[i][:], in1=x_t[k][:, cols], op=ADD)
-            if k >= PAIRS - 2:
-                nc.sync.dma_start(out=oview[k][:, cols], in_=o_t[k][:, cols])
-            elif i % 2 == 1:
+                o_t[k] = sb.tile([P, 2 * D], F32, name="o", bufs=4, align_bytes=64)
+            parts = 2 if i == TILES - 1 else 1
+            for lo in range(0, D, D // parts):
+                cols = slice((i % 2) * D + lo, (i % 2) * D + lo + D // parts)
+                nc.vector.tensor_tensor(out=o_t[k][:, cols], in0=po_t[i][:, lo : lo + D // parts], in1=x_t[k][:, cols], op=ADD)
+                if k >= PAIRS - 2:
+                    nc.sync.dma_start(out=oview[k][:, cols], in_=o_t[k][:, cols])
+            if k < PAIRS - 2 and i % 2 == 1:
                 nc.sync.dma_start(out=oview[k], in_=o_t[k][:])
 
         xs_t[0] = xs_first
@@ -256,8 +280,9 @@ def tile_mopn_layer_pb_t_w4_kernel(tc, hid_bytes, hid_scale, Wd, Wo_words, Wo_sc
                 load_x(p)
             turn(a)
             turn(b)
-            weave(a - 2)
-            weave(b - 2)
+            if p >= 2:
+                empty_j(a - 4, b - 4)
+            weave(a - 2, b - 2)
             if p == 1:
                 quant_w()
             if c >= 0:
@@ -276,7 +301,6 @@ def tile_mopn_layer_pb_t_w4_kernel(tc, hid_bytes, hid_scale, Wd, Wo_words, Wo_sc
             round_j(b - 2)
             turn_j(a - 2, b - 2)
             widen_s(a + 2)
-            empty_j(a - 2, b - 2)
             widen_s(b + 2)
             empty_v(b)
             if c >= 0:
@@ -286,8 +310,8 @@ def tile_mopn_layer_pb_t_w4_kernel(tc, hid_bytes, hid_scale, Wd, Wo_words, Wo_sc
         load_x(PAIRS - 1)
         turn(n - 2)
         turn(n - 1)
-        weave(n - 4)
-        weave(n - 3)
+        empty_j(n - 6, n - 5)
+        weave(n - 4, n - 3)
         quant_j(n - 8, n - 7)
         quant(n - 4, n - 3)
         empty_s(n - 2)
@@ -297,35 +321,30 @@ def tile_mopn_layer_pb_t_w4_kernel(tc, hid_bytes, hid_scale, Wd, Wo_words, Wo_sc
         down(n - 3)
         mix(n - 8)
         mix(n - 7)
-        weave(n - 2)
-        empty_v(n - 1, (0,))
-        quant(n - 2)
         round_j(n - 4)
         round_j(n - 3)
-        down(n - 2)
-        empty_v(n - 1, (1,))
-        weave(n - 1)
-        quant_j(n - 6, n - 5)
-        quant(n - 1)
         turn_j(n - 4, n - 3)
+        empty_v(n - 1)
+        weave(n - 2, n - 1)
+        quant_j(n - 6, n - 5)
+        quant(n - 2)
+        quant(n - 1)
+        empty_j(n - 4, n - 3)
         mix(n - 6, "xt0")
         mix(n - 5, "xt1")
-        round_j(n - 2)
+        down(n - 2)
         down(n - 1)
-        empty_j(n - 4, n - 3)
+        round_j(n - 2)
         round_j(n - 1)
-        turn_j(n - 2, n - 1)
-        empty_j(n - 2, n - 1)
-        add(n - 8)
-        add(n - 7)
         quant_j(n - 4, n - 3)
         mix(n - 4, "xt0")
         mix(n - 3, "xt1")
-        add(n - 6)
-        add(n - 5)
-        add(n - 4)
+        turn_j(n - 2, n - 1)
+        empty_j(n - 2, n - 1)
+        for i in range(n - 8, n - 4):
+            add(i)
         quant_j(n - 2, n - 1)
         mix(n - 2)
         mix(n - 1)
-        for i in range(n - 3, n):
+        for i in range(n - 4, n):
             add(i)

@@ -25,13 +25,14 @@ HALF = 2 * H
 TILES = TOKENS // P
 PAIRS = TILES // 2
 V_COLS = 1280
-G_COLS = 1408
+G_COLS = 1024
 G_FILL = 1152
 M_A = 256
-M_B = 192
+M_B = 96
 M_A_FILL = 192
 M_B_FILL = 128
 N_FILL = 3
+M_LAST = 256
 FLOPS = 2 * TOKENS * NS * H * DS + 2 * TOKENS * D * D
 
 
@@ -96,7 +97,7 @@ def tile_mopn_layer_pb_t_w4_kernel(tc, hid_bytes, hid_scale, Wd, Wo_words, Wo_sc
             nc.vector.quantize_mx(out=w_codes[:].bitcast(F8X4), scales=w_scales[:], in_=w_grp[:].rearrange("p n d j -> p (n d j)"))
 
         def m_s(i):
-            return (M_A_FILL, M_B_FILL)[i % 2] if i // 2 < N_FILL else (M_A, M_B)[i % 2]
+            return (M_A_FILL, M_B_FILL)[i % 2] if i // 2 < N_FILL else M_LAST if i == TILES - 1 else (M_A, M_B)[i % 2]
 
         def wide(k):
             return V_COLS if k == 0 else G_FILL if k <= N_FILL else G_COLS
@@ -171,12 +172,12 @@ def tile_mopn_layer_pb_t_w4_kernel(tc, hid_bytes, hid_scale, Wd, Wo_words, Wo_sc
                         op=MULT,
                     )
 
-        def weave(*tiles):
+        def weave(eng, *tiles):
             k = tiles[0] // 2
             lo = (tiles[0] % 2) * m_s(2 * k)
             m = sum(m_s(i) for i in tiles)
             at = ROW - 4 * m_s(2 * k) + 4 * lo
-            nc.vector.tensor_copy(
+            eng.tensor_copy(
                 out=g_t[k][:, at : at + 4 * m].bitcast(F32).rearrange("p (m u) -> p m u", u=2),
                 in_=pw_t[k][:].rearrange("p u m e -> p u (m e)").bitcast(F32)[:, :, lo : lo + m].rearrange("p u m -> p m u"),
             )
@@ -248,9 +249,9 @@ def tile_mopn_layer_pb_t_w4_kernel(tc, hid_bytes, hid_scale, Wd, Wo_words, Wo_sc
             for lo in range(0, D, D // parts):
                 cols = slice((i % 2) * D + lo, (i % 2) * D + lo + D // parts)
                 nc.vector.tensor_tensor(out=o_t[k][:, cols], in0=po_t[i][:, lo : lo + D // parts], in1=x_t[k][:, cols], op=ADD)
-                if k >= PAIRS - 2:
+                if k >= PAIRS - 4:
                     nc.sync.dma_start(out=oview[k][:, cols], in_=o_t[k][:, cols])
-            if k < PAIRS - 2 and i % 2 == 1:
+            if k < PAIRS - 4 and i % 2 == 1:
                 nc.sync.dma_start(out=oview[k], in_=o_t[k][:])
 
         xs_t[0] = xs_first
@@ -282,7 +283,8 @@ def tile_mopn_layer_pb_t_w4_kernel(tc, hid_bytes, hid_scale, Wd, Wo_words, Wo_sc
             turn(b)
             if p >= 2:
                 empty_j(a - 4, b - 4)
-            weave(a - 2, b - 2)
+            if p <= N_FILL:
+                weave(nc.vector, a - 2, b - 2)
             if p == 1:
                 quant_w()
             if c >= 0:
@@ -303,6 +305,8 @@ def tile_mopn_layer_pb_t_w4_kernel(tc, hid_bytes, hid_scale, Wd, Wo_words, Wo_sc
             widen_s(a + 2)
             widen_s(b + 2)
             empty_v(b)
+            if p >= N_FILL:
+                weave(nc.gpsimd, a, b)
             if c >= 0:
                 add(c)
                 add(d)
@@ -311,7 +315,6 @@ def tile_mopn_layer_pb_t_w4_kernel(tc, hid_bytes, hid_scale, Wd, Wo_words, Wo_sc
         turn(n - 2)
         turn(n - 1)
         empty_j(n - 6, n - 5)
-        weave(n - 4, n - 3)
         quant_j(n - 8, n - 7)
         quant(n - 4, n - 3)
         empty_s(n - 2)
@@ -325,7 +328,9 @@ def tile_mopn_layer_pb_t_w4_kernel(tc, hid_bytes, hid_scale, Wd, Wo_words, Wo_sc
         round_j(n - 3)
         turn_j(n - 4, n - 3)
         empty_v(n - 1)
-        weave(n - 2, n - 1)
+        for i in range(n - 8, n - 7):
+            add(i)
+        weave(nc.vector, n - 2, n - 1)
         quant_j(n - 6, n - 5)
         quant(n - 2)
         quant(n - 1)
@@ -338,13 +343,17 @@ def tile_mopn_layer_pb_t_w4_kernel(tc, hid_bytes, hid_scale, Wd, Wo_words, Wo_sc
         round_j(n - 1)
         quant_j(n - 4, n - 3)
         mix(n - 4, "xt0")
+        turn_j(n - 2)
+        turn_j(n - 1)
         mix(n - 3, "xt1")
-        turn_j(n - 2, n - 1)
-        empty_j(n - 2, n - 1)
-        for i in range(n - 8, n - 4):
+        empty_j(n - 2)
+        empty_j(n - 1)
+        for i in range(n - 7, n - 4):
             add(i)
-        quant_j(n - 2, n - 1)
+        quant_j(n - 2)
         mix(n - 2)
+        add(n - 4)
+        quant_j(n - 1)
         mix(n - 1)
-        for i in range(n - 4, n):
+        for i in range(n - 3, n):
             add(i)

@@ -24,13 +24,14 @@ ROW = NS * H
 HALF = 2 * H
 TILES = TOKENS // P
 PAIRS = TILES // 2
-V_COLS = 1280
-G_COLS = 1024
-G_FILL = 1152
+V_COLS = 1024
+G_COLS = 960
+G_FIRST = 512
+G_FILL = 1024
 M_A = 256
-M_B = 96
-M_A_FILL = 192
-M_B_FILL = 128
+M_B = 136
+M_A_FILL = 256
+M_B_FILL = 96
 N_FILL = 3
 M_LAST = 256
 FLOPS = 2 * TOKENS * NS * H * DS + 2 * TOKENS * D * D
@@ -54,7 +55,7 @@ def tile_mopn_layer_pb_t_w4_kernel(tc, hid_bytes, hid_scale, Wd, Wo_words, Wo_sc
 
         scale_p = keep.tile([P, 4], F32, align_bytes=64)
         ident = keep.tile([P, P], F32, align_bytes=64)
-        w_raw = keep.tile([P, NS, 4, DS], BF16, align_bytes=64)
+        w_raw = [keep.tile([P, 2, 4, DS], BF16, name="w_raw%d" % h, align_bytes=64) for h in range(2)]
         w_codes = keep.tile([P, D], U32, align_bytes=64)
         w_scales = keep.tile([P, D], U8, align_bytes=64)
         wo_words = keep.tile([P, 2 * D], U8, align_bytes=64)
@@ -73,10 +74,13 @@ def tile_mopn_layer_pb_t_w4_kernel(tc, hid_bytes, hid_scale, Wd, Wo_words, Wo_sc
             nc.sync.dma_start(out=x_t[k][:], in_=xin[k])
 
         cut = ROW - V_COLS
-        load_hid(0, (cut, ROW, 0, cut, ROW, 2 * ROW))
+        wd_rows = Wd.rearrange("n (p j) d -> p n (j d)", j=4)
+        load_hid(0, (cut, ROW, 0, cut))
         nc.sync.dma_start(out=scale_p[:], in_=srow.rearrange("(p t) -> p t", t=4))
+        nc.sync.dma_start(out=w_raw[0][:].rearrange("p n j d -> p n (j d)"), in_=wd_rows[:, 0:2, :])
+        nc.sync.dma_start(out=hb_t[0][:, ROW:], in_=hid[0][:, ROW:])
+        nc.sync.dma_start(out=w_raw[1][:].rearrange("p n j d -> p n (j d)"), in_=wd_rows[:, 2:4, :])
         load_hid(1)
-        nc.sync.dma_start(out=w_raw[:].rearrange("p n j d -> p n (j d)"), in_=Wd.rearrange("n (p j) d -> p n (j d)", j=4))
         load_hid(2)
         make_identity(nc, ident[:])
         nc.vector.memset(wo_scales[:].bitcast(I32), 0)
@@ -91,7 +95,8 @@ def tile_mopn_layer_pb_t_w4_kernel(tc, hid_bytes, hid_scale, Wd, Wo_words, Wo_sc
         w_grp = ring.tile([P, NS, DS, 4], BF16, name="ring", align_bytes=64)
 
         def group_w():
-            nc.vector.tensor_copy(out=w_grp[:], in_=w_raw[:].rearrange("p n j d -> p n d j"))
+            for h in range(2):
+                nc.gpsimd.tensor_copy(out=w_grp[:, 2 * h : 2 * h + 2], in_=w_raw[h][:].rearrange("p n j d -> p n d j"))
 
         def quant_w():
             nc.vector.quantize_mx(out=w_codes[:].bitcast(F8X4), scales=w_scales[:], in_=w_grp[:].rearrange("p n d j -> p (n d j)"))
@@ -100,7 +105,7 @@ def tile_mopn_layer_pb_t_w4_kernel(tc, hid_bytes, hid_scale, Wd, Wo_words, Wo_sc
             return (M_A_FILL, M_B_FILL)[i % 2] if i // 2 < N_FILL else M_LAST if i == TILES - 1 else (M_A, M_B)[i % 2]
 
         def wide(k):
-            return V_COLS if k == 0 else G_FILL if k <= N_FILL else G_COLS
+            return V_COLS if k == 0 else G_FIRST if k == 1 else G_FILL if k <= N_FILL else G_COLS
 
         def widen(eng, k, lo, hi):
             eng(out=xs_t[k][:, lo:hi], in_=hb_t[k][:, lo:hi].bitcast(F8))
@@ -257,8 +262,9 @@ def tile_mopn_layer_pb_t_w4_kernel(tc, hid_bytes, hid_scale, Wd, Wo_words, Wo_sc
         xs_t[0] = xs_first
         widen(nc.vector.tensor_copy, 0, ROW - V_COLS, ROW)
         widen_s(0)
-        widen(nc.vector.tensor_copy, 0, ROW, ROW + V_COLS)
-        widen_s(1)
+        widen(nc.scalar.copy, 0, ROW, ROW + HALF)
+        widen(nc.scalar.copy, 0, ROW + HALF, 2 * ROW)
+        group_w()
         turn(0)
         turn(1)
         empty_v(0, (1,))
@@ -269,7 +275,6 @@ def tile_mopn_layer_pb_t_w4_kernel(tc, hid_bytes, hid_scale, Wd, Wo_words, Wo_sc
         widen_s(2)
         widen_s(3)
         empty_v(1)
-        group_w()
 
         BACK = 3
         for p in range(1, PAIRS - 1):

@@ -24,12 +24,11 @@ ROW = NS * H
 HALF = 2 * H
 TILES = TOKENS // P
 PAIRS = TILES // 2
-V_COLS = 1024
-G_COLS = 960
-G_FIRST = 512
+G_COLS = 896
+G_FIRST = 896
 G_FILL = 1024
 M_A = 256
-M_B = 136
+M_B = 112
 M_A_FILL = 256
 M_B_FILL = 96
 N_FILL = 3
@@ -73,9 +72,8 @@ def tile_mopn_layer_pb_t_w4_kernel(tc, hid_bytes, hid_scale, Wd, Wo_words, Wo_sc
             x_t[k] = loads.tile([P, 2 * D], BF16, name="x", align_bytes=64)
             nc.sync.dma_start(out=x_t[k][:], in_=xin[k])
 
-        cut = ROW - V_COLS
         wd_rows = Wd.rearrange("n (p j) d -> p n (j d)", j=4)
-        load_hid(0, (cut, ROW, 0, cut))
+        load_hid(0, (0, HALF, HALF, ROW))
         nc.sync.dma_start(out=scale_p[:], in_=srow.rearrange("(p t) -> p t", t=4))
         nc.sync.dma_start(out=w_raw[0][:].rearrange("p n j d -> p n (j d)"), in_=wd_rows[:, 0:2, :])
         nc.sync.dma_start(out=hb_t[0][:, ROW:], in_=hid[0][:, ROW:])
@@ -96,7 +94,7 @@ def tile_mopn_layer_pb_t_w4_kernel(tc, hid_bytes, hid_scale, Wd, Wo_words, Wo_sc
 
         def group_w():
             for h in range(2):
-                nc.gpsimd.tensor_copy(out=w_grp[:, 2 * h : 2 * h + 2], in_=w_raw[h][:].rearrange("p n j d -> p n d j"))
+                nc.vector.tensor_copy(out=w_grp[:, 2 * h : 2 * h + 2], in_=w_raw[h][:].rearrange("p n j d -> p n d j"))
 
         def quant_w():
             nc.vector.quantize_mx(out=w_codes[:].bitcast(F8X4), scales=w_scales[:], in_=w_grp[:].rearrange("p n d j -> p (n d j)"))
@@ -105,7 +103,7 @@ def tile_mopn_layer_pb_t_w4_kernel(tc, hid_bytes, hid_scale, Wd, Wo_words, Wo_sc
             return (M_A_FILL, M_B_FILL)[i % 2] if i // 2 < N_FILL else M_LAST if i == TILES - 1 else (M_A, M_B)[i % 2]
 
         def wide(k):
-            return V_COLS if k == 0 else G_FIRST if k == 1 else G_FILL if k <= N_FILL else G_COLS
+            return G_FIRST if k == 1 else G_FILL if k <= N_FILL else G_COLS
 
         def widen(eng, k, lo, hi):
             eng(out=xs_t[k][:, lo:hi], in_=hb_t[k][:, lo:hi].bitcast(F8))
@@ -127,7 +125,7 @@ def tile_mopn_layer_pb_t_w4_kernel(tc, hid_bytes, hid_scale, Wd, Wo_words, Wo_sc
         def turn(i):
             words = xs_t[i // 2][:, (i % 2) * ROW : (i % 2 + 1) * ROW].bitcast(F32)
             xt_t[i] = [ps.tile([P, 2, 2, P], F32, name="xt%d" % h) for h in range(2)]
-            for h in (1, 0):
+            for h in (0, 1) if i < 2 else (1, 0):
                 for a in (1, 0):
                     n = space(i, h, a)
                     for u in range(2):
@@ -260,17 +258,16 @@ def tile_mopn_layer_pb_t_w4_kernel(tc, hid_bytes, hid_scale, Wd, Wo_words, Wo_sc
                 nc.sync.dma_start(out=oview[k], in_=o_t[k][:])
 
         xs_t[0] = xs_first
-        widen(nc.vector.tensor_copy, 0, ROW - V_COLS, ROW)
-        widen_s(0)
-        widen(nc.scalar.copy, 0, ROW, ROW + HALF)
+        widen(nc.vector.tensor_copy, 0, 0, HALF)
+        widen(nc.scalar.copy, 0, HALF, ROW)
         widen(nc.scalar.copy, 0, ROW + HALF, 2 * ROW)
+        widen(nc.scalar.copy, 0, ROW, ROW + HALF)
         group_w()
         turn(0)
         turn(1)
-        empty_v(0, (1,))
         widen_g(1)
         empty_s(0)
-        empty_v(0, (0,))
+        empty_v(0)
         empty_s(1)
         widen_s(2)
         widen_s(3)

@@ -12,7 +12,6 @@ F8X4 = mybir.dt.float8_e4m3fn_x4
 F4X4 = mybir.dt.float4_e2m1fn_x4
 MULT = mybir.AluOpType.mult
 ADD = mybir.AluOpType.add
-COPY = mybir.ActivationFunctionType.Copy
 
 P = 128
 TOKENS = 4096
@@ -24,15 +23,10 @@ ROW = NS * H
 HALF = 2 * H
 TILES = TOKENS // P
 PAIRS = TILES // 2
-G_COLS = 896
-G_FIRST = 896
-G_FILL = 1024
-M_A = 256
-M_B = 112
-M_A_FILL = 256
-M_B_FILL = 96
+M_B = 128
+M_B_FILL = 48
+M_FIRST = 96
 N_FILL = 3
-M_LAST = 256
 FLOPS = 2 * TOKENS * NS * H * DS + 2 * TOKENS * D * D
 
 
@@ -47,7 +41,7 @@ def tile_mopn_layer_pb_t_w4_kernel(tc, hid_bytes, hid_scale, Wd, Wo_words, Wo_sc
         keep = ctx.enter_context(tc.tile_pool(name="keep", bufs=1))
         loads = ctx.enter_context(tc.tile_pool(name="loads", bufs=5))
         sb = ctx.enter_context(tc.tile_pool(name="sb", bufs=3))
-        ring = ctx.enter_context(tc.tile_pool(name="ring", bufs=3))
+        ring = ctx.enter_context(tc.tile_pool(name="ring", bufs=1))
         ps = ctx.enter_context(tc.psum_pool(name="ps", bufs=2))
 
         ctx.enter_context(tc.manual_schedule())
@@ -59,7 +53,6 @@ def tile_mopn_layer_pb_t_w4_kernel(tc, hid_bytes, hid_scale, Wd, Wo_words, Wo_sc
         w_scales = keep.tile([P, D], U8, align_bytes=64)
         wo_words = keep.tile([P, 2 * D], U8, align_bytes=64)
         wo_scales = keep.tile([P, D], U8, align_bytes=64)
-        xs_first = keep.tile([P, 2 * ROW], BF16, align_bytes=64)
 
         hb_t, x_t, xs_t, xt_t, g_t, c_t, s_t, jp_t, jb_t, jt_t, jg_t, jc_t, js_t, po_t, o_t, pw_t = ({} for z in range(16))
 
@@ -90,7 +83,7 @@ def tile_mopn_layer_pb_t_w4_kernel(tc, hid_bytes, hid_scale, Wd, Wo_words, Wo_sc
         load_hid(3)
         load_x(1)
 
-        w_grp = ring.tile([P, NS, DS, 4], BF16, name="ring", align_bytes=64)
+        w_grp = ring.tile([P, NS, DS, 4], BF16, name="slot2", align_bytes=64)
 
         def group_w():
             for h in range(2):
@@ -100,34 +93,24 @@ def tile_mopn_layer_pb_t_w4_kernel(tc, hid_bytes, hid_scale, Wd, Wo_words, Wo_sc
             nc.vector.quantize_mx(out=w_codes[:].bitcast(F8X4), scales=w_scales[:], in_=w_grp[:].rearrange("p n d j -> p (n d j)"))
 
         def m_s(i):
-            return (M_A_FILL, M_B_FILL)[i % 2] if i // 2 < N_FILL else M_LAST if i == TILES - 1 else (M_A, M_B)[i % 2]
-
-        def wide(k):
-            return G_FIRST if k == 1 else G_FILL if k <= N_FILL else G_COLS
-
-        def widen(eng, k, lo, hi):
-            eng(out=xs_t[k][:, lo:hi], in_=hb_t[k][:, lo:hi].bitcast(F8))
-
-        def widen_g(k):
-            xs_t[k] = ring.tile([P, 2 * ROW], BF16, name="ring", align_bytes=64)
-            widen(nc.gpsimd.tensor_copy, k, ROW - wide(k), ROW + wide(k))
-
-        def widen_s(i):
-            k = i // 2
+            if i < 2:
+                return M_FIRST
             if i % 2 == 0:
-                widen(nc.scalar.copy, k, 0, ROW - wide(k))
-            else:
-                widen(nc.scalar.copy, k, ROW + wide(k), 2 * ROW)
+                return 2 * P
+            return M_B_FILL if i // 2 < N_FILL else 0 if i == TILES - 1 else M_B
 
-        def space(i, h, a):
-            return 2 * h + a if i % 2 == 0 else 3 - 2 * h - a
+        def widen(i, eng=nc.scalar.copy, lo=0, hi=ROW):
+            if i not in xs_t:
+                xs_t[i] = sb.tile([P, ROW], BF16, name="xs", align_bytes=64)
+            base = (i % 2) * ROW
+            eng(out=xs_t[i][:, lo:hi], in_=hb_t[i // 2][:, base + lo : base + hi].bitcast(F8))
 
         def turn(i):
-            words = xs_t[i // 2][:, (i % 2) * ROW : (i % 2 + 1) * ROW].bitcast(F32)
+            words = xs_t[i][:].bitcast(F32)
             xt_t[i] = [ps.tile([P, 2, 2, P], F32, name="xt%d" % h) for h in range(2)]
             for h in (0, 1) if i < 2 else (1, 0):
-                for a in (1, 0):
-                    n = space(i, h, a)
+                for a in range(2):
+                    n = 2 * h + a
                     for u in range(2):
                         nc.tensor.transpose(xt_t[i][h][:, u, a, :], words[:, 256 * n + u : 256 * (n + 1) : 2], ident[:])
 
@@ -145,45 +128,41 @@ def tile_mopn_layer_pb_t_w4_kernel(tc, hid_bytes, hid_scale, Wd, Wo_words, Wo_sc
         def place(i, h):
             return h if i % 2 == 0 else 1 - h
 
+        def g_tile(k):
+            if k not in g_t:
+                g_t[k] = ring.tile([P, 2 * ROW], BF16, name="slot%d" % (2 if k == 1 else k % 3), align_bytes=64)
+            return g_t[k]
+
         def empty_s(i):
             k = i // 2
             if i % 2 == 0:
-                pw_t[k] = sb.tile([P, 2, m_s(i) + m_s(i + 1), 2], BF16, name="pw", bufs=2, align_bytes=64)
+                pw_t[k] = sb.tile([P, m_s(i) + m_s(i + 1), 2], F32, name="pw", bufs=2, align_bytes=64)
             lo = (i % 2) * m_s(2 * k)
-            for e in range(2):
-                for u in range(2):
-                    nc.scalar.activation(
-                        out=pw_t[k][:, u, lo : lo + m_s(i), e],
-                        in_=bank_view(i, 1)[:, u, s_cols(i), e],
-                        func=COPY,
-                        scale=scale_p[:, 2 * u + e : 2 * u + e + 1],
-                    )
+            nc.scalar.copy(out=pw_t[k][:, lo : lo + m_s(i), :], in_=xt_t[i][1][:].rearrange("p u a r -> p (a r) u")[:, s_cols(i), :])
+
+        def scale_g(k):
+            m = m_s(2 * k) + m_s(2 * k + 1)
+            at = ROW - 4 * m_s(2 * k)
+            nc.gpsimd.tensor_tensor(
+                out=g_tile(k)[:, at : at + 4 * m].rearrange("p (m t) -> p m t", t=4),
+                in0=pw_t[k][:].rearrange("p m u -> p (m u)").bitcast(BF16).rearrange("p (m t) -> p m t", t=4),
+                in1=scale_p[:].unsqueeze(1).to_broadcast([P, m, 4]),
+                op=MULT,
+            )
 
         def empty_v(i, halves=(0, 1)):
             k = i // 2
-            if k not in g_t:
-                g_t[k] = ring.tile([P, 2 * ROW], BF16, name="ring", align_bytes=64) if k == 1 else sb.tile([P, 2 * ROW], BF16, name="g", bufs=2, align_bytes=64)
             for h in halves:
                 cols = v_cols(i, h)
                 m = cols.stop - cols.start
                 lo = (i % 2) * ROW + HALF * place(i, h) + 4 * cols.start
                 if m > 0:
                     nc.vector.tensor_tensor(
-                        out=g_t[k][:, lo : lo + 4 * m].rearrange("p (m u e) -> p m u e", u=2, e=2),
+                        out=g_tile(k)[:, lo : lo + 4 * m].rearrange("p (m u e) -> p m u e", u=2, e=2),
                         in0=bank_view(i, h)[:, :, cols, :].rearrange("p u m e -> p m u e"),
                         in1=scale_p[:].rearrange("p (u e) -> p u e", u=2).unsqueeze(1).to_broadcast([P, m, 2, 2]),
                         op=MULT,
                     )
-
-        def weave(eng, *tiles):
-            k = tiles[0] // 2
-            lo = (tiles[0] % 2) * m_s(2 * k)
-            m = sum(m_s(i) for i in tiles)
-            at = ROW - 4 * m_s(2 * k) + 4 * lo
-            eng.tensor_copy(
-                out=g_t[k][:, at : at + 4 * m].bitcast(F32).rearrange("p (m u) -> p m u", u=2),
-                in_=pw_t[k][:].rearrange("p u m e -> p u (m e)").bitcast(F32)[:, :, lo : lo + m].rearrange("p u m -> p m u"),
-            )
 
         def quant(*tiles):
             lo, wid = (tiles[0] % 2) * ROW, len(tiles) * ROW
@@ -197,7 +176,7 @@ def tile_mopn_layer_pb_t_w4_kernel(tc, hid_bytes, hid_scale, Wd, Wo_words, Wo_sc
             jp_t[i] = ps.tile([P, D], F32, name=tag)
             for h in range(2):
                 for a in range(2):
-                    n = space(i, h, a)
+                    n = 2 * h + a
                     tok = slice(P * (2 * place(i, h) + a), P * (2 * place(i, h) + a + 1))
                     chan = slice(P * n, P * (n + 1))
                     nc.tensor.matmul_mx(
@@ -222,7 +201,8 @@ def tile_mopn_layer_pb_t_w4_kernel(tc, hid_bytes, hid_scale, Wd, Wo_words, Wo_sc
                     nc.tensor.transpose(jt_t[tiles][:, u, z, :], words[:, P * u : P * (u + 1)], ident[:])
 
         def empty_j(*tiles):
-            jg_t[tiles] = ring.tile([P, len(tiles) * P, 2], F32, name="ring", align_bytes=64)
+            tag = "slot%d" % (tiles[0] // 2 % 3) if len(tiles) == 2 else "last%d" % (tiles[0] % 2)
+            jg_t[tiles] = ring.tile([P, len(tiles) * P, 2], F32, name=tag, align_bytes=64)
             nc.scalar.copy(out=jg_t[tiles][:], in_=jt_t[tiles][:].rearrange("p u i r -> p (i r) u"))
 
         def quant_j(*tiles):
@@ -257,21 +237,23 @@ def tile_mopn_layer_pb_t_w4_kernel(tc, hid_bytes, hid_scale, Wd, Wo_words, Wo_sc
             if k < PAIRS - 4 and i % 2 == 1:
                 nc.sync.dma_start(out=oview[k], in_=o_t[k][:])
 
-        xs_t[0] = xs_first
-        widen(nc.vector.tensor_copy, 0, 0, HALF)
-        widen(nc.scalar.copy, 0, HALF, ROW)
-        widen(nc.scalar.copy, 0, ROW + HALF, 2 * ROW)
-        widen(nc.scalar.copy, 0, ROW, ROW + HALF)
+        widen(0, nc.vector.tensor_copy, 0, HALF)
+        widen(0, nc.scalar.copy, HALF, ROW)
+        widen(1, nc.scalar.copy, 0, HALF)
+        widen(1, nc.scalar.copy, HALF, ROW)
         group_w()
         turn(0)
         turn(1)
-        widen_g(1)
         empty_s(0)
-        empty_v(0)
         empty_s(1)
-        widen_s(2)
-        widen_s(3)
-        empty_v(1)
+        scale_g(0)
+        for h in range(2):
+            empty_v(0, (h,))
+            empty_v(1, (h,))
+        widen(2)
+        widen(3)
+        turn(2)
+        empty_s(2)
 
         BACK = 3
         for p in range(1, PAIRS - 1):
@@ -281,47 +263,41 @@ def tile_mopn_layer_pb_t_w4_kernel(tc, hid_bytes, hid_scale, Wd, Wo_words, Wo_sc
                 load_hid(p + 3)
             if p >= 2:
                 load_x(p)
-            turn(a)
             turn(b)
             if p >= 2:
                 empty_j(a - 4, b - 4)
-            if p <= N_FILL:
-                weave(nc.vector, a - 2, b - 2)
+            empty_s(b)
             if p == 1:
                 quant_w()
             if c >= 0:
                 quant_j(c, d)
             quant(a - 2, b - 2)
-            empty_s(a)
+            scale_g(p)
             empty_v(a)
-            empty_s(b)
-            widen_g(p + 1)
+            widen(a + 2)
             down(a - 2)
             down(b - 2)
             if c >= 0:
                 mix(c)
                 mix(d)
+            turn(a + 2)
             round_j(a - 2)
             round_j(b - 2)
             turn_j(a - 2, b - 2)
-            widen_s(a + 2)
-            widen_s(b + 2)
+            widen(b + 2)
+            empty_s(a + 2)
             empty_v(b)
-            if p >= N_FILL:
-                weave(nc.gpsimd, a, b)
             if c >= 0:
                 add(c)
                 add(d)
         n = TILES
         load_x(PAIRS - 1)
-        turn(n - 2)
         turn(n - 1)
         empty_j(n - 6, n - 5)
         quant_j(n - 8, n - 7)
         quant(n - 4, n - 3)
-        empty_s(n - 2)
+        scale_g(PAIRS - 1)
         empty_v(n - 2)
-        empty_s(n - 1)
         down(n - 4)
         down(n - 3)
         mix(n - 8)
@@ -332,7 +308,6 @@ def tile_mopn_layer_pb_t_w4_kernel(tc, hid_bytes, hid_scale, Wd, Wo_words, Wo_sc
         empty_v(n - 1)
         for i in range(n - 8, n - 7):
             add(i)
-        weave(nc.vector, n - 2, n - 1)
         quant_j(n - 6, n - 5)
         quant(n - 2)
         quant(n - 1)

@@ -12,6 +12,7 @@ F8X4 = mybir.dt.float8_e4m3fn_x4
 F4X4 = mybir.dt.float4_e2m1fn_x4
 MULT = mybir.AluOpType.mult
 ADD = mybir.AluOpType.add
+COPY = mybir.ActivationFunctionType.Copy
 
 P = 128
 TOKENS = 4096
@@ -23,10 +24,11 @@ ROW = NS * H
 HALF = 2 * H
 TILES = TOKENS // P
 PAIRS = TILES // 2
-M_B = 128
-M_B_FILL = 48
+M_B = 136
+M_B_FILL = 32
 M_FIRST = 96
 N_FILL = 3
+Z_COLS = 192
 FLOPS = 2 * TOKENS * NS * H * DS + 2 * TOKENS * D * D
 
 
@@ -85,9 +87,8 @@ def tile_mopn_layer_pb_t_w4_kernel(tc, hid_bytes, hid_scale, Wd, Wo_words, Wo_sc
 
         w_grp = ring.tile([P, NS, DS, 4], BF16, name="slot2", align_bytes=64)
 
-        def group_w():
-            for h in range(2):
-                nc.vector.tensor_copy(out=w_grp[:, 2 * h : 2 * h + 2], in_=w_raw[h][:].rearrange("p n j d -> p n d j"))
+        def group_w(h):
+            nc.vector.tensor_copy(out=w_grp[:, 2 * h : 2 * h + 2], in_=w_raw[h][:].rearrange("p n j d -> p n d j"))
 
         def quant_w():
             nc.vector.quantize_mx(out=w_codes[:].bitcast(F8X4), scales=w_scales[:], in_=w_grp[:].rearrange("p n d j -> p (n d j)"))
@@ -105,6 +106,9 @@ def tile_mopn_layer_pb_t_w4_kernel(tc, hid_bytes, hid_scale, Wd, Wo_words, Wo_sc
             base = (i % 2) * ROW
             eng(out=xs_t[i][:, lo:hi], in_=hb_t[i // 2][:, base + lo : base + hi].bitcast(F8))
 
+        def table_first(out, in_):
+            nc.scalar.activation(out=out, in_=in_, func=COPY)
+
         def turn(i):
             words = xs_t[i][:].bitcast(F32)
             xt_t[i] = [ps.tile([P, 2, 2, P], F32, name="xt%d" % h) for h in range(2)]
@@ -117,13 +121,22 @@ def tile_mopn_layer_pb_t_w4_kernel(tc, hid_bytes, hid_scale, Wd, Wo_words, Wo_sc
         def bank_view(i, h):
             return xt_t[i][h][:].rearrange("p u a r -> p (u a r)").bitcast(BF16).rearrange("p (u m e) -> p u m e", u=2, e=2)
 
+        def z_s(i):
+            return Z_COLS if i == TILES - 1 else 0
+
+        def scale_s(i):
+            lo = m_s(i)
+            dst = g_tile(i // 2)[:, ROW + 4 * lo : ROW + 4 * (lo + z_s(i))].rearrange("p (m t) -> p m t", t=4)
+            for t in range(4):
+                nc.scalar.activation(out=dst[:, :, t], in_=bank_view(i, 1)[:, t // 2, lo : lo + z_s(i), t % 2], func=COPY, scale=scale_p[:, t : t + 1])
+
         def s_cols(i):
             return slice(2 * P - m_s(i), 2 * P) if i % 2 == 0 else slice(0, m_s(i))
 
         def v_cols(i, h):
             if h == 0:
                 return slice(0, 2 * P)
-            return slice(0, 2 * P - m_s(i)) if i % 2 == 0 else slice(m_s(i), 2 * P)
+            return slice(0, 2 * P - m_s(i)) if i % 2 == 0 else slice(m_s(i) + z_s(i), 2 * P)
 
         def place(i, h):
             return h if i % 2 == 0 else 1 - h
@@ -238,18 +251,21 @@ def tile_mopn_layer_pb_t_w4_kernel(tc, hid_bytes, hid_scale, Wd, Wo_words, Wo_sc
                 nc.sync.dma_start(out=oview[k], in_=o_t[k][:])
 
         widen(0, nc.vector.tensor_copy, 0, HALF)
-        widen(0, nc.scalar.copy, HALF, ROW)
+        widen(0, table_first, HALF, HALF + 64)
+        widen(0, nc.scalar.copy, HALF + 64, ROW)
         widen(1, nc.scalar.copy, 0, HALF)
         widen(1, nc.scalar.copy, HALF, ROW)
-        group_w()
         turn(0)
         turn(1)
+        group_w(0)
+        empty_v(0, (0,))
+        group_w(1)
         empty_s(0)
         empty_s(1)
         scale_g(0)
-        for h in range(2):
-            empty_v(0, (h,))
-            empty_v(1, (h,))
+        empty_v(1, (0,))
+        empty_v(0, (1,))
+        empty_v(1, (1,))
         widen(2)
         widen(3)
         turn(2)
@@ -297,6 +313,7 @@ def tile_mopn_layer_pb_t_w4_kernel(tc, hid_bytes, hid_scale, Wd, Wo_words, Wo_sc
         quant_j(n - 8, n - 7)
         quant(n - 4, n - 3)
         scale_g(PAIRS - 1)
+        scale_s(n - 1)
         empty_v(n - 2)
         down(n - 4)
         down(n - 3)
@@ -325,12 +342,12 @@ def tile_mopn_layer_pb_t_w4_kernel(tc, hid_bytes, hid_scale, Wd, Wo_words, Wo_sc
         mix(n - 3, "xt1")
         empty_j(n - 2)
         empty_j(n - 1)
-        for i in range(n - 7, n - 4):
+        for i in range(n - 7, n - 3):
             add(i)
         quant_j(n - 2)
         mix(n - 2)
-        add(n - 4)
+        add(n - 3)
         quant_j(n - 1)
         mix(n - 1)
-        for i in range(n - 3, n):
+        for i in range(n - 2, n):
             add(i)

@@ -24,11 +24,12 @@ ROW = NS * H
 HALF = 2 * H
 TILES = TOKENS // P
 PAIRS = TILES // 2
-M_B = 136
+M_B = 120
 M_B_FILL = 32
 M_FIRST = 96
 N_FILL = 3
-Z_COLS = 192
+Z_LAST = 192
+Z_COLS = 32
 FLOPS = 2 * TOKENS * NS * H * DS + 2 * TOKENS * D * D
 
 
@@ -122,7 +123,7 @@ def tile_mopn_layer_pb_t_w4_kernel(tc, hid_bytes, hid_scale, Wd, Wo_words, Wo_sc
             return xt_t[i][h][:].rearrange("p u a r -> p (u a r)").bitcast(BF16).rearrange("p (u m e) -> p u m e", u=2, e=2)
 
         def z_s(i):
-            return Z_COLS if i == TILES - 1 else 0
+            return Z_LAST if i == TILES - 1 else Z_COLS if i % 2 == 1 and i // 2 >= N_FILL else 0
 
         def scale_s(i):
             lo = m_s(i)
@@ -291,6 +292,8 @@ def tile_mopn_layer_pb_t_w4_kernel(tc, hid_bytes, hid_scale, Wd, Wo_words, Wo_sc
             scale_g(p)
             empty_v(a)
             widen(a + 2)
+            if p >= N_FILL:
+                scale_s(b)
             down(a - 2)
             down(b - 2)
             if c >= 0:

@@ -24,12 +24,13 @@ ROW = NS * H
 HALF = 2 * H
 TILES = TOKENS // P
 PAIRS = TILES // 2
-M_B = 120
+M_B = 152
 M_B_FILL = 32
 M_FIRST = 96
 N_FILL = 3
+RUN = 8
 Z_LAST = 192
-Z_COLS = 32
+Z_COLS = 16
 FLOPS = 2 * TOKENS * NS * H * DS + 2 * TOKENS * D * D
 
 
@@ -50,6 +51,7 @@ def tile_mopn_layer_pb_t_w4_kernel(tc, hid_bytes, hid_scale, Wd, Wo_words, Wo_sc
         ctx.enter_context(tc.manual_schedule())
 
         scale_p = keep.tile([P, 4], F32, align_bytes=64)
+        scale_run = keep.tile([P, RUN, 4], F32, align_bytes=64)
         ident = keep.tile([P, P], F32, align_bytes=64)
         w_raw = [keep.tile([P, 2, 4, DS], BF16, name="w_raw%d" % h, align_bytes=64) for h in range(2)]
         w_codes = keep.tile([P, D], U32, align_bytes=64)
@@ -158,9 +160,9 @@ def tile_mopn_layer_pb_t_w4_kernel(tc, hid_bytes, hid_scale, Wd, Wo_words, Wo_sc
             m = m_s(2 * k) + m_s(2 * k + 1)
             at = ROW - 4 * m_s(2 * k)
             nc.gpsimd.tensor_tensor(
-                out=g_tile(k)[:, at : at + 4 * m].rearrange("p (m t) -> p m t", t=4),
-                in0=pw_t[k][:].rearrange("p m u -> p (m u)").bitcast(BF16).rearrange("p (m t) -> p m t", t=4),
-                in1=scale_p[:].unsqueeze(1).to_broadcast([P, m, 4]),
+                out=g_tile(k)[:, at : at + 4 * m].rearrange("p (m t) -> p m t", t=4 * RUN),
+                in0=pw_t[k][:].rearrange("p m u -> p (m u)").bitcast(BF16).rearrange("p (m t) -> p m t", t=4 * RUN),
+                in1=scale_run[:].rearrange("p r t -> p (r t)").unsqueeze(1).to_broadcast([P, m // RUN, 4 * RUN]),
                 op=MULT,
             )
 
@@ -258,6 +260,7 @@ def tile_mopn_layer_pb_t_w4_kernel(tc, hid_bytes, hid_scale, Wd, Wo_words, Wo_sc
         widen(1, nc.scalar.copy, HALF, ROW)
         turn(0)
         turn(1)
+        nc.vector.tensor_copy(out=scale_run[:], in_=scale_p[:].unsqueeze(1).to_broadcast([P, RUN, 4]))
         group_w(0)
         empty_v(0, (0,))
         group_w(1)

@@ -24,13 +24,13 @@ ROW = NS * H
 HALF = 2 * H
 TILES = TOKENS // P
 PAIRS = TILES // 2
-M_B = 152
+M_B = 144
 M_B_FILL = 32
 M_FIRST = 96
 N_FILL = 3
 RUN = 8
 Z_LAST = 192
-Z_COLS = 16
+Z_COLS = 20
 FLOPS = 2 * TOKENS * NS * H * DS + 2 * TOKENS * D * D
 
 
@@ -156,12 +156,14 @@ def tile_mopn_layer_pb_t_w4_kernel(tc, hid_bytes, hid_scale, Wd, Wo_words, Wo_sc
             lo = (i % 2) * m_s(2 * k)
             nc.scalar.copy(out=pw_t[k][:, lo : lo + m_s(i), :], in_=xt_t[i][1][:].rearrange("p u a r -> p (a r) u")[:, s_cols(i), :])
 
-        def scale_g(k):
-            m = m_s(2 * k) + m_s(2 * k + 1)
-            at = ROW - 4 * m_s(2 * k)
+        def scale_g(*tiles):
+            k = tiles[0] // 2
+            lo = (tiles[0] % 2) * m_s(2 * k)
+            m = sum(m_s(i) for i in tiles)
+            at = ROW - 4 * m_s(2 * k) + 4 * lo
             nc.gpsimd.tensor_tensor(
                 out=g_tile(k)[:, at : at + 4 * m].rearrange("p (m t) -> p m t", t=4 * RUN),
-                in0=pw_t[k][:].rearrange("p m u -> p (m u)").bitcast(BF16).rearrange("p (m t) -> p m t", t=4 * RUN),
+                in0=pw_t[k][:, lo : lo + m, :].rearrange("p m u -> p (m u)").bitcast(BF16).rearrange("p (m t) -> p m t", t=4 * RUN),
                 in1=scale_run[:].rearrange("p r t -> p (r t)").unsqueeze(1).to_broadcast([P, m // RUN, 4 * RUN]),
                 op=MULT,
             )
@@ -266,7 +268,7 @@ def tile_mopn_layer_pb_t_w4_kernel(tc, hid_bytes, hid_scale, Wd, Wo_words, Wo_sc
         group_w(1)
         empty_s(0)
         empty_s(1)
-        scale_g(0)
+        scale_g(0, 1)
         empty_v(1, (0,))
         empty_v(0, (1,))
         empty_v(1, (1,))
@@ -292,7 +294,11 @@ def tile_mopn_layer_pb_t_w4_kernel(tc, hid_bytes, hid_scale, Wd, Wo_words, Wo_sc
             if c >= 0:
                 quant_j(c, d)
             quant(a - 2, b - 2)
-            scale_g(p)
+            if p <= N_FILL:
+                scale_g(a)
+                scale_g(b)
+            else:
+                scale_g(a, b)
             empty_v(a)
             widen(a + 2)
             if p >= N_FILL:
@@ -318,7 +324,7 @@ def tile_mopn_layer_pb_t_w4_kernel(tc, hid_bytes, hid_scale, Wd, Wo_words, Wo_sc
         empty_j(n - 6, n - 5)
         quant_j(n - 8, n - 7)
         quant(n - 4, n - 3)
-        scale_g(PAIRS - 1)
+        scale_g(n - 2)
         scale_s(n - 1)
         empty_v(n - 2)
         down(n - 4)

@@ -21,16 +21,18 @@ H = 512
 DS = 128
 D = NS * DS
 ROW = NS * H
-HALF = 2 * H
 TILES = TOKENS // P
 PAIRS = TILES // 2
-M_B = 144
-M_B_FILL = 32
-M_FIRST = 96
-N_FILL = 3
-RUN = 8
-Z_LAST = 192
-Z_COLS = 20
+UNITS = 2 * NS
+G_UNITS = 3
+G_FIRST = 3
+G_SECOND = 2
+G_LAST = 3
+LATE = 1
+BACK = 3
+G_ADDS = 0
+Z_LAST = 64
+SINGLE_STORES = 4
 FLOPS = 2 * TOKENS * NS * H * DS + 2 * TOKENS * D * D
 
 
@@ -46,191 +48,148 @@ def tile_mopn_layer_pb_t_w4_kernel(tc, hid_bytes, hid_scale, Wd, Wo_words, Wo_sc
         loads = ctx.enter_context(tc.tile_pool(name="loads", bufs=5))
         sb = ctx.enter_context(tc.tile_pool(name="sb", bufs=3))
         ring = ctx.enter_context(tc.tile_pool(name="ring", bufs=1))
-        ps = ctx.enter_context(tc.psum_pool(name="ps", bufs=2))
+        ps = ctx.enter_context(tc.psum_pool(name="ps", bufs=4))
 
         ctx.enter_context(tc.manual_schedule())
 
         scale_p = keep.tile([P, 4], F32, align_bytes=64)
-        scale_run = keep.tile([P, RUN, 4], F32, align_bytes=64)
+        scale_row = keep.tile([P, 2, P, 2], F32, align_bytes=64)
         ident = keep.tile([P, P], F32, align_bytes=64)
-        w_raw = [keep.tile([P, 2, 4, DS], BF16, name="w_raw%d" % h, align_bytes=64) for h in range(2)]
+        w_raw = keep.tile([P, NS, 4, DS], BF16, align_bytes=64)
+        w_grp = keep.tile([P, NS, DS, 4], BF16, align_bytes=64)
         w_codes = keep.tile([P, D], U32, align_bytes=64)
         w_scales = keep.tile([P, D], U8, align_bytes=64)
         wo_words = keep.tile([P, 2 * D], U8, align_bytes=64)
         wo_scales = keep.tile([P, D], U8, align_bytes=64)
 
-        hb_t, x_t, xs_t, xt_t, g_t, c_t, s_t, jp_t, jb_t, jt_t, jg_t, jc_t, js_t, po_t, o_t, pw_t = ({} for z in range(16))
+        hb_t, x_t, xv_t, xg_t, gs_t, bank_t, q_t, c_t, s_t, jp_t, jb_t, jt_t, jg_t, jc_t, js_t, po_t, o_t, r_t = ({} for z in range(18))
 
-        def load_hid(k, cuts=(0, 2 * ROW)):
-            hb_t[k] = loads.tile([P, 2 * ROW], U8, name="hb", align_bytes=64)
-            for lo, hi in zip(cuts[0::2], cuts[1::2]):
-                nc.sync.dma_start(out=hb_t[k][:, lo:hi], in_=hid[k][:, lo:hi])
+        def g_units(k):
+            return {0: 0, 1: G_FIRST, 2: G_SECOND, PAIRS - 1: G_LAST}.get(k, G_UNITS)
+
+        def v_units(k):
+            return UNITS - g_units(k)
+
+        def by_bank(lo, hi):
+            return [(u, min(u + 2, hi)) for u in range(lo, hi, 2)]
+
+        def load_hid(k, lo=0, hi=UNITS):
+            if k not in hb_t:
+                hb_t[k] = loads.tile([P, 2 * ROW], U8, name="hb", align_bytes=64)
+            nc.sync.dma_start(out=hb_t[k][:, H * lo : H * hi], in_=hid[k][:, H * lo : H * hi])
 
         def load_x(k):
             x_t[k] = loads.tile([P, 2 * D], BF16, name="x", align_bytes=64)
             nc.sync.dma_start(out=x_t[k][:], in_=xin[k])
 
-        wd_rows = Wd.rearrange("n (p j) d -> p n (j d)", j=4)
-        load_hid(0, (0, HALF, HALF, ROW))
-        nc.sync.dma_start(out=scale_p[:], in_=srow.rearrange("(p t) -> p t", t=4))
-        nc.sync.dma_start(out=w_raw[0][:].rearrange("p n j d -> p n (j d)"), in_=wd_rows[:, 0:2, :])
-        nc.sync.dma_start(out=hb_t[0][:, ROW:], in_=hid[0][:, ROW:])
-        nc.sync.dma_start(out=w_raw[1][:].rearrange("p n j d -> p n (j d)"), in_=wd_rows[:, 2:4, :])
-        load_hid(1)
-        load_hid(2)
-        make_identity(nc, ident[:])
-        nc.vector.memset(wo_scales[:].bitcast(I32), 0)
-        nc.sync.dma_start(out=wo_words[:], in_=Wo_words[0])
-        wos = Wo_scales[0].bitcast(I32)
-        for q in range(4):
-            nc.sync.dma_start(out=wo_scales[32 * q : 32 * q + 4, :].bitcast(I32), in_=wos[4 * q : 4 * q + 4, :])
-        load_x(0)
-        load_hid(3)
-        load_x(1)
+        def widen_v(k, lo, hi, eng=nc.scalar.copy):
+            xv = sb.tile([P, (hi - lo) * H], BF16, name="xv", bufs=6, align_bytes=64)
+            eng(out=xv[:], in_=hb_t[k][:, H * lo : H * hi].bitcast(F8))
+            for u in range(lo, hi):
+                xv_t[k, u] = xv[:, H * (u - lo) : H * (u - lo + 1)]
 
-        w_grp = ring.tile([P, NS, DS, 4], BF16, name="slot2", align_bytes=64)
+        def widen_g(k):
+            xg_t[k] = sb.tile([P, g_units(k) * H], BF16, name="xg", bufs=2, align_bytes=64)
+            nc.scalar.copy(out=xg_t[k][:], in_=hb_t[k][:, H * v_units(k) :].bitcast(F8))
 
-        def group_w(h):
-            nc.vector.tensor_copy(out=w_grp[:, 2 * h : 2 * h + 2], in_=w_raw[h][:].rearrange("p n j d -> p n d j"))
-
-        def quant_w():
-            nc.vector.quantize_mx(out=w_codes[:].bitcast(F8X4), scales=w_scales[:], in_=w_grp[:].rearrange("p n d j -> p (n d j)"))
-
-        def m_s(i):
-            if i < 2:
-                return M_FIRST
-            if i % 2 == 0:
-                return 2 * P
-            return M_B_FILL if i // 2 < N_FILL else 0 if i == TILES - 1 else M_B
-
-        def widen(i, eng=nc.scalar.copy, lo=0, hi=ROW):
-            if i not in xs_t:
-                xs_t[i] = sb.tile([P, ROW], BF16, name="xs", align_bytes=64)
-            base = (i % 2) * ROW
-            eng(out=xs_t[i][:, lo:hi], in_=hb_t[i // 2][:, base + lo : base + hi].bitcast(F8))
-
-        def table_first(out, in_):
-            nc.scalar.activation(out=out, in_=in_, func=COPY)
-
-        def turn(i):
-            words = xs_t[i][:].bitcast(F32)
-            xt_t[i] = [ps.tile([P, 2, 2, P], F32, name="xt%d" % h) for h in range(2)]
-            for h in (0, 1) if i < 2 else (1, 0):
-                for a in range(2):
-                    n = 2 * h + a
-                    for u in range(2):
-                        nc.tensor.transpose(xt_t[i][h][:, u, a, :], words[:, 256 * n + u : 256 * (n + 1) : 2], ident[:])
-
-        def bank_view(i, h):
-            return xt_t[i][h][:].rearrange("p u a r -> p (u a r)").bitcast(BF16).rearrange("p (u m e) -> p u m e", u=2, e=2)
-
-        def z_s(i):
-            return Z_LAST if i == TILES - 1 else Z_COLS if i % 2 == 1 and i // 2 >= N_FILL else 0
-
-        def scale_s(i):
-            lo = m_s(i)
-            dst = g_tile(i // 2)[:, ROW + 4 * lo : ROW + 4 * (lo + z_s(i))].rearrange("p (m t) -> p m t", t=4)
-            for t in range(4):
-                nc.scalar.activation(out=dst[:, :, t], in_=bank_view(i, 1)[:, t // 2, lo : lo + z_s(i), t % 2], func=COPY, scale=scale_p[:, t : t + 1])
-
-        def s_cols(i):
-            return slice(2 * P - m_s(i), 2 * P) if i % 2 == 0 else slice(0, m_s(i))
-
-        def v_cols(i, h):
-            if h == 0:
-                return slice(0, 2 * P)
-            return slice(0, 2 * P - m_s(i)) if i % 2 == 0 else slice(m_s(i) + z_s(i), 2 * P)
-
-        def place(i, h):
-            return h if i % 2 == 0 else 1 - h
-
-        def g_tile(k):
-            if k not in g_t:
-                g_t[k] = ring.tile([P, 2 * ROW], BF16, name="slot%d" % (2 if k == 1 else k % 3), align_bytes=64)
-            return g_t[k]
-
-        def empty_s(i):
-            k = i // 2
-            if i % 2 == 0:
-                pw_t[k] = sb.tile([P, m_s(i) + m_s(i + 1), 2], F32, name="pw", bufs=2, align_bytes=64)
-            lo = (i % 2) * m_s(2 * k)
-            nc.scalar.copy(out=pw_t[k][:, lo : lo + m_s(i), :], in_=xt_t[i][1][:].rearrange("p u a r -> p (a r) u")[:, s_cols(i), :])
-
-        def scale_g(*tiles):
-            k = tiles[0] // 2
-            lo = (tiles[0] % 2) * m_s(2 * k)
-            m = sum(m_s(i) for i in tiles)
-            at = ROW - 4 * m_s(2 * k) + 4 * lo
+        def scale_g(k):
+            n = g_units(k)
+            gs_t[k] = ring.tile([P, 2, n, P, 2], BF16, name="slot%d" % (k % 2), align_bytes=64)
             nc.gpsimd.tensor_tensor(
-                out=g_tile(k)[:, at : at + 4 * m].rearrange("p (m t) -> p m t", t=4 * RUN),
-                in0=pw_t[k][:, lo : lo + m, :].rearrange("p m u -> p (m u)").bitcast(BF16).rearrange("p (m t) -> p m t", t=4 * RUN),
-                in1=scale_run[:].rearrange("p r t -> p (r t)").unsqueeze(1).to_broadcast([P, m // RUN, 4 * RUN]),
+                out=gs_t[k][:],
+                in0=xg_t[k][:].rearrange("r (n p u e) -> r u n p e", p=P, u=2, e=2),
+                in1=scale_row[:].unsqueeze(2).to_broadcast([P, 2, n, P, 2]),
                 op=MULT,
             )
 
-        def empty_v(i, halves=(0, 1)):
-            k = i // 2
-            for h in halves:
-                cols = v_cols(i, h)
-                m = cols.stop - cols.start
-                lo = (i % 2) * ROW + HALF * place(i, h) + 4 * cols.start
-                if m > 0:
-                    nc.vector.tensor_tensor(
-                        out=g_tile(k)[:, lo : lo + 4 * m].rearrange("p (m u e) -> p m u e", u=2, e=2),
-                        in0=bank_view(i, h)[:, :, cols, :].rearrange("p u m e -> p m u e"),
-                        in1=scale_p[:].rearrange("p (u e) -> p u e", u=2).unsqueeze(1).to_broadcast([P, m, 2, 2]),
-                        op=MULT,
-                    )
+        def turn_v(k, lo, hi):
+            bank_t[k, lo] = ps.tile([P, 2, hi - lo, P], F32, name="for_vector")
+            for a in range(hi - lo):
+                words = xv_t[k, lo + a].bitcast(F32)
+                for u in range(2):
+                    nc.tensor.transpose(bank_t[k, lo][:, u, a, :], words[:, u::2], ident[:])
 
-        def quant(*tiles):
-            lo, wid = (tiles[0] % 2) * ROW, len(tiles) * ROW
-            codes = sb.tile([P, wid // 4], U32, name="codes", align_bytes=64)
-            scales = sb.tile([P, wid // 4], U8, name="scales", align_bytes=64)
-            nc.vector.quantize_mx(out=codes[:].bitcast(F8X4), scales=scales[:], in_=g_t[tiles[0] // 2][:, lo : lo + wid])
-            for z, i in enumerate(tiles):
-                c_t[i], s_t[i] = codes[:, D * z : D * (z + 1)], scales[:, D * z : D * (z + 1)]
+        def turn_g(k, lo, hi):
+            bank_t[k, lo] = ps.tile([P, 2, hi - lo, P], F32, name="for_scalar")
+            words = gs_t[k][:].rearrange("r u n p e -> r u n (p e)").bitcast(F32)
+            for a in range(hi - lo):
+                for u in range(2):
+                    nc.tensor.transpose(bank_t[k, lo][:, u, a, :], words[:, u, lo - v_units(k) + a, :], ident[:])
 
-        def down(i, tag="jp"):
-            jp_t[i] = ps.tile([P, D], F32, name=tag)
-            for h in range(2):
-                for a in range(2):
-                    n = 2 * h + a
-                    tok = slice(P * (2 * place(i, h) + a), P * (2 * place(i, h) + a + 1))
-                    chan = slice(P * n, P * (n + 1))
-                    nc.tensor.matmul_mx(
-                        out=jp_t[i][:, chan],
-                        lhsT=c_t[i][:, tok].bitcast(F8X4),
-                        lhsT_scale=s_t[i][:, tok],
-                        rhs=w_codes[:, chan].bitcast(F8X4),
-                        rhs_scale=w_scales[:, chan],
-                        start=True,
-                        stop=True,
-                    )
+        def q_cols(k, lo, hi):
+            i = 2 * k + lo // NS
+            if i not in q_t:
+                if i % 2 == 0:
+                    q_t[i] = ring.tile([P, ROW], BF16, name="slot%d" % (k % 2), align_bytes=64)
+                else:
+                    q_t[i] = sb.tile([P, ROW], BF16, name="second", bufs=2, align_bytes=64)
+            return q_t[i][:, H * (lo % NS) : H * (lo % NS + hi - lo)]
+
+        def bank_pairs(k, lo):
+            return bank_t[k, lo][:].rearrange("p u a r -> p (u a r)").bitcast(BF16).rearrange("p (u m e) -> p m u e", u=2, e=2)
+
+        def scale_v(k, lo, hi, skip=0):
+            m = (hi - lo) * P - skip
+            nc.vector.tensor_tensor(
+                out=q_cols(k, lo, hi).rearrange("p (m u e) -> p m u e", u=2, e=2)[:, skip:],
+                in0=bank_pairs(k, lo)[:, skip:],
+                in1=scale_p[:].rearrange("p (u e) -> p u e", u=2).unsqueeze(1).to_broadcast([P, m, 2, 2]),
+                op=MULT,
+            )
+
+        def scale_s(k, lo, hi, m):
+            dst = q_cols(k, lo, hi).rearrange("p (m t) -> p m t", t=4)
+            for t in range(4):
+                nc.scalar.activation(out=dst[:, :m, t], in_=bank_pairs(k, lo)[:, :m, t // 2, t % 2], func=COPY, scale=scale_p[:, t : t + 1])
+
+        def empty_g(k, lo, hi):
+            nc.scalar.copy(
+                out=q_cols(k, lo, hi).bitcast(F32).rearrange("p (m u) -> p m u", u=2),
+                in_=bank_t[k, lo][:].rearrange("p u a r -> p (a r) u"),
+            )
+
+        def quant(i):
+            c_t[i] = sb.tile([P, D], U32, name="codes", align_bytes=64)
+            s_t[i] = sb.tile([P, D], U8, name="scales", align_bytes=64)
+            nc.vector.quantize_mx(out=c_t[i][:].bitcast(F8X4), scales=s_t[i][:], in_=q_t[i][:])
+
+        def down(i):
+            jp_t[i] = ps.tile([P, D], F32, name="for_scalar")
+            for n in range(NS):
+                cols = slice(P * n, P * (n + 1))
+                nc.tensor.matmul_mx(
+                    out=jp_t[i][:, cols],
+                    lhsT=c_t[i][:, cols].bitcast(F8X4),
+                    lhsT_scale=s_t[i][:, cols],
+                    rhs=w_codes[:, cols].bitcast(F8X4),
+                    rhs_scale=w_scales[:, cols],
+                    start=True,
+                    stop=True,
+                )
 
         def round_j(i):
             jb_t[i] = sb.tile([P, 2, P, 2], BF16, name="jb", bufs=4, align_bytes=64)
             nc.scalar.copy(out=jb_t[i][:], in_=jp_t[i][:].rearrange("r (p u e) -> r u p e", u=2, e=2))
 
         def turn_j(*tiles):
-            jt_t[tiles] = ps.tile([P, 2, len(tiles), P], F32, name="jp")
+            jt_t[tiles] = ps.tile([P, 2, len(tiles), P], F32, name="for_scalar")
             for z, i in enumerate(tiles):
                 words = jb_t[i][:].rearrange("r u p e -> r (u p e)").bitcast(F32)
                 for u in range(2):
                     nc.tensor.transpose(jt_t[tiles][:, u, z, :], words[:, P * u : P * (u + 1)], ident[:])
 
         def empty_j(*tiles):
-            tag = "slot%d" % (tiles[0] // 2 % 3) if len(tiles) == 2 else "last%d" % (tiles[0] % 2)
-            jg_t[tiles] = ring.tile([P, len(tiles) * P, 2], F32, name=tag, align_bytes=64)
+            jg_t[tiles] = sb.tile([P, len(tiles) * P, 2], F32, name="jg", align_bytes=64)
             nc.scalar.copy(out=jg_t[tiles][:], in_=jt_t[tiles][:].rearrange("p u i r -> p (i r) u"))
 
         def quant_j(*tiles):
-            codes = sb.tile([P, len(tiles) * P], U32, name="jcodes", align_bytes=64)
-            scales = sb.tile([P, len(tiles) * P], U8, name="jscales", align_bytes=64)
+            codes = sb.tile([P, len(tiles) * P], U32, name="jcodes", bufs=5, align_bytes=64)
+            scales = sb.tile([P, len(tiles) * P], U8, name="jscales", bufs=5, align_bytes=64)
             nc.vector.quantize_mx(out=codes[:].bitcast(F8X4), scales=scales[:], in_=jg_t[tiles][:].rearrange("p r u -> p (r u)").bitcast(BF16))
             for z, i in enumerate(tiles):
                 jc_t[i], js_t[i] = codes[:, P * z : P * (z + 1)], scales[:, P * z : P * (z + 1)]
 
-        def mix(i, tag="po"):
+        def mix(i, tag="for_vector"):
             po_t[i] = ps.tile([P, D], F32, name=tag)
             nc.tensor.matmul_mx(
                 out=po_t[i][:],
@@ -242,6 +201,17 @@ def tile_mopn_layer_pb_t_w4_kernel(tc, hid_bytes, hid_scale, Wd, Wo_words, Wo_sc
                 stop=True,
             )
 
+        def empty_o(i):
+            k = i // 2
+            if i % 2 == 0:
+                r_t[k] = sb.tile([P, 2 * D], F32, name="res", bufs=2, align_bytes=64)
+            nc.scalar.copy(out=r_t[k][:, (i % 2) * D : (i % 2 + 1) * D], in_=po_t[i][:])
+
+        def add_g(k, slot):
+            o_t[k] = ring.tile([P, 2 * D], F32, name="slot%d" % slot, align_bytes=64)
+            nc.gpsimd.tensor_tensor(out=o_t[k][:], in0=r_t[k][:], in1=x_t[k][:], op=ADD)
+            nc.sync.dma_start(out=oview[k], in_=o_t[k][:])
+
         def add(i):
             k = i // 2
             if i % 2 == 0:
@@ -250,116 +220,132 @@ def tile_mopn_layer_pb_t_w4_kernel(tc, hid_bytes, hid_scale, Wd, Wo_words, Wo_sc
             for lo in range(0, D, D // parts):
                 cols = slice((i % 2) * D + lo, (i % 2) * D + lo + D // parts)
                 nc.vector.tensor_tensor(out=o_t[k][:, cols], in0=po_t[i][:, lo : lo + D // parts], in1=x_t[k][:, cols], op=ADD)
-                if k >= PAIRS - 4:
+                if k >= PAIRS - SINGLE_STORES:
                     nc.sync.dma_start(out=oview[k][:, cols], in_=o_t[k][:, cols])
-            if k < PAIRS - 4 and i % 2 == 1:
+            if k < PAIRS - SINGLE_STORES and i % 2 == 1:
                 nc.sync.dma_start(out=oview[k], in_=o_t[k][:])
 
-        widen(0, nc.vector.tensor_copy, 0, HALF)
-        widen(0, table_first, HALF, HALF + 64)
-        widen(0, nc.scalar.copy, HALF + 64, ROW)
-        widen(1, nc.scalar.copy, 0, HALF)
-        widen(1, nc.scalar.copy, HALF, ROW)
-        turn(0)
-        turn(1)
-        nc.vector.tensor_copy(out=scale_run[:], in_=scale_p[:].unsqueeze(1).to_broadcast([P, RUN, 4]))
-        group_w(0)
-        empty_v(0, (0,))
-        group_w(1)
-        empty_s(0)
-        empty_s(1)
-        scale_g(0, 1)
-        empty_v(1, (0,))
-        empty_v(0, (1,))
-        empty_v(1, (1,))
-        widen(2)
-        widen(3)
-        turn(2)
-        empty_s(2)
+        nc.sync.dma_start(out=scale_p[:], in_=srow.rearrange("(p t) -> p t", t=4))
+        load_hid(0, 0, 2)
+        load_hid(0, 2, 4)
+        load_hid(1, v_units(1), UNITS)
+        load_hid(0, 4, UNITS)
+        load_hid(1, 0, v_units(1))
+        nc.sync.dma_start(out=w_raw[:].rearrange("p n j d -> p n (j d)"), in_=Wd.rearrange("n (p j) d -> p n (j d)", j=4))
+        load_hid(2)
+        make_identity(nc, ident[:])
+        nc.vector.memset(wo_scales[:].bitcast(I32), 0)
+        nc.sync.dma_start(out=wo_words[:], in_=Wo_words[0])
+        wos = Wo_scales[0].bitcast(I32)
+        for q in range(4):
+            nc.sync.dma_start(out=wo_scales[32 * q : 32 * q + 4, :].bitcast(I32), in_=wos[4 * q : 4 * q + 4, :])
+        load_hid(3)
+        load_x(0)
 
-        BACK = 3
-        for p in range(1, PAIRS - 1):
-            a, b = 2 * p, 2 * p + 1
-            c, d = a - 2 * BACK, b - 2 * BACK
+        spread = ps.tile([P, 2, 2, P], F32, name="for_scalar")
+        for t in range(4):
+            nc.tensor.transpose(spread[:, t // 2, t % 2, :], scale_p[:, t : t + 1].to_broadcast([P, P]), ident[:])
+        widen_v(0, 0, 1, nc.vector.tensor_copy)
+        widen_v(0, 1, 2, nc.vector.tensor_copy)
+        nc.vector.tensor_copy(out=scale_row[:], in_=spread[:].rearrange("r u e p -> r u p e"))
+
+        widen_v(0, 2, 4)
+        widen_g(1)
+        scale_g(1)
+        widen_v(0, 4, 6)
+        widen_v(0, 6, 8)
+        first_banks = [(0, 1), (1, 2)] + by_bank(2, UNITS)
+        for lo, hi in first_banks:
+            turn_v(0, lo, hi)
+            scale_v(0, lo, hi)
+        widen_v(1, 0, 2)
+        nc.scalar.copy(out=w_grp[:], in_=w_raw[:].rearrange("p n j d -> p n d j"))
+        widen_g(2)
+        widen_v(1, 2, v_units(1))
+        turn_v(1, 0, 2)
+
+        n = TILES
+        for p in range(1, PAIRS):
+            a, b = 2 * p - 2, 2 * p - 1
+            c, d = 2 * (p - BACK), 2 * (p - BACK) + 1
+            last = p == PAIRS - 1
+            adds = (c, d) if BACK <= p < PAIRS - LATE else ()
             if p + 3 < PAIRS:
                 load_hid(p + 3)
+            load_x(p)
+            if not last and p > 1:
+                widen_v(p + 1, 0, v_units(p + 1))
+            for lo, hi in by_bank(v_units(p), UNITS):
+                turn_g(p, lo, hi)
             if p >= 2:
-                load_x(p)
-            turn(b)
-            if p >= 2:
-                empty_j(a - 4, b - 4)
-            empty_s(b)
+                turn_j(a - 2, b - 2)
             if p == 1:
-                quant_w()
-            if c >= 0:
-                quant_j(c, d)
-            quant(a - 2, b - 2)
-            if p <= N_FILL:
-                scale_g(a)
-                scale_g(b)
+                turn_v(1, 2, 4)
+                quant(b)
+                quant(a)
+                nc.vector.quantize_mx(out=w_codes[:].bitcast(F8X4), scales=w_scales[:], in_=w_grp[:].rearrange("p n d j -> p (n d j)"))
             else:
-                scale_g(a, b)
-            empty_v(a)
-            widen(a + 2)
-            if p >= N_FILL:
-                scale_s(b)
-            down(a - 2)
-            down(b - 2)
-            if c >= 0:
-                mix(c)
-                mix(d)
-            turn(a + 2)
-            round_j(a - 2)
-            round_j(b - 2)
-            turn_j(a - 2, b - 2)
-            widen(b + 2)
-            empty_s(a + 2)
-            empty_v(b)
-            if c >= 0:
-                add(c)
-                add(d)
-        n = TILES
-        load_x(PAIRS - 1)
-        turn(n - 1)
-        empty_j(n - 6, n - 5)
-        quant_j(n - 8, n - 7)
-        quant(n - 4, n - 3)
-        scale_g(n - 2)
-        scale_s(n - 1)
-        empty_v(n - 2)
-        down(n - 4)
-        down(n - 3)
-        mix(n - 8)
-        mix(n - 7)
-        round_j(n - 4)
-        round_j(n - 3)
+                if c >= 0:
+                    quant_j(c, d)
+                quant(a)
+                quant(b)
+            if not last:
+                scale_g(p + 1)
+            elif G_ADDS:
+                add_g(p - BACK - 1, 0)
+            for lo, hi in by_bank(v_units(p), UNITS):
+                empty_g(p, lo, hi)
+            if p >= 2:
+                empty_j(a - 2, b - 2)
+            if p == 1:
+                widen_v(p + 1, 0, v_units(p + 1))
+            for i in adds:
+                mix(i)
+            down(a)
+            down(b)
+            scale_v(p, 0, 2)
+            round_j(a)
+            round_j(b)
+            if v_units(p) > NS:
+                turn_v(p, NS, v_units(p))
+            scale_v(p, 2, 4)
+            if p + 2 < PAIRS:
+                widen_g(p + 2)
+            if not last:
+                turn_v(p + 1, 0, 2)
+            for i in adds:
+                add(i)
+            if v_units(p) > NS:
+                scale_v(p, NS, v_units(p))
+            if not last:
+                turn_v(p + 1, 2, 4)
+
+        first = n - 2 * BACK - 2 * LATE
         turn_j(n - 4, n - 3)
-        empty_v(n - 1)
-        for i in range(n - 8, n - 7):
-            add(i)
-        quant_j(n - 6, n - 5)
+        empty_j(n - 4, n - 3)
+        mix(first)
+        mix(first + 1)
         quant(n - 2)
         quant(n - 1)
-        empty_j(n - 4, n - 3)
-        mix(n - 6, "xt0")
-        mix(n - 5, "xt1")
+        for i in range(n - 2 * BACK, n - 2, 2):
+            quant_j(i, i + 1)
         down(n - 2)
         down(n - 1)
         round_j(n - 2)
         round_j(n - 1)
-        quant_j(n - 4, n - 3)
-        mix(n - 4, "xt0")
+        mix(first + 2)
+        mix(first + 3)
         turn_j(n - 2)
-        turn_j(n - 1)
-        mix(n - 3, "xt1")
         empty_j(n - 2)
+        turn_j(n - 1)
         empty_j(n - 1)
-        for i in range(n - 7, n - 3):
+        for i in range(first, n):
+            if i == n - 4:
+                quant_j(n - 2)
+            if i == n - 3:
+                quant_j(n - 1)
             add(i)
-        quant_j(n - 2)
-        mix(n - 2)
-        add(n - 3)
-        quant_j(n - 1)
-        mix(n - 1)
-        for i in range(n - 2, n):
-            add(i)
+            if i + 4 < n - 2:
+                mix(i + 4)
+            if i == n - 4 or i == n - 3:
+                mix(i + 2)

@@ -31,7 +31,7 @@ G_LAST = 3
 LATE = 1
 BACK = 3
 G_ADDS = 0
-Z_LAST = 64
+T_COLS = 256
 SINGLE_STORES = 4
 FLOPS = 2 * TOKENS * NS * H * DS + 2 * TOKENS * D * D
 
@@ -55,14 +55,14 @@ def tile_mopn_layer_pb_t_w4_kernel(tc, hid_bytes, hid_scale, Wd, Wo_words, Wo_sc
         scale_p = keep.tile([P, 4], F32, align_bytes=64)
         scale_row = keep.tile([P, 2, P, 2], F32, align_bytes=64)
         ident = keep.tile([P, P], F32, align_bytes=64)
+        ident_bf = keep.tile([P, P], BF16, align_bytes=64)
         w_raw = keep.tile([P, NS, 4, DS], BF16, align_bytes=64)
-        w_grp = keep.tile([P, NS, DS, 4], BF16, align_bytes=64)
         w_codes = keep.tile([P, D], U32, align_bytes=64)
         w_scales = keep.tile([P, D], U8, align_bytes=64)
         wo_words = keep.tile([P, 2 * D], U8, align_bytes=64)
         wo_scales = keep.tile([P, D], U8, align_bytes=64)
 
-        hb_t, x_t, xv_t, xg_t, gs_t, bank_t, q_t, c_t, s_t, jp_t, jb_t, jt_t, jg_t, jc_t, js_t, po_t, o_t, r_t = ({} for z in range(18))
+        hb_t, x_t, xv_t, xg_t, gs_t, bank_t, q_t, c_t, s_t, jp_t, jb_t, jt_t, jg_t, jc_t, js_t, po_t, o_t, r_t, pt_t, rt_t = ({} for z in range(20))
 
         def g_units(k):
             return {0: 0, 1: G_FIRST, 2: G_SECOND, PAIRS - 1: G_LAST}.get(k, G_UNITS)
@@ -94,7 +94,7 @@ def tile_mopn_layer_pb_t_w4_kernel(tc, hid_bytes, hid_scale, Wd, Wo_words, Wo_sc
 
         def scale_g(k):
             n = g_units(k)
-            gs_t[k] = ring.tile([P, 2, n, P, 2], BF16, name="slot%d" % (k % 2), align_bytes=64)
+            gs_t[k] = ring.tile([P, 2, n, P, 2], BF16, name="slot%d" % ((k + 1) % 2), align_bytes=64)
             nc.gpsimd.tensor_tensor(
                 out=gs_t[k][:],
                 in0=xg_t[k][:].rearrange("r (n p u e) -> r u n p e", p=P, u=2, e=2),
@@ -117,13 +117,13 @@ def tile_mopn_layer_pb_t_w4_kernel(tc, hid_bytes, hid_scale, Wd, Wo_words, Wo_sc
                     nc.tensor.transpose(bank_t[k, lo][:, u, a, :], words[:, u, lo - v_units(k) + a, :], ident[:])
 
         def q_cols(k, lo, hi):
-            i = 2 * k + lo // NS
-            if i not in q_t:
-                if i % 2 == 0:
-                    q_t[i] = ring.tile([P, ROW], BF16, name="slot%d" % (k % 2), align_bytes=64)
-                else:
-                    q_t[i] = sb.tile([P, ROW], BF16, name="second", bufs=2, align_bytes=64)
-            return q_t[i][:, H * (lo % NS) : H * (lo % NS + hi - lo)]
+            if k == 1 and lo < NS:
+                if "first" not in q_t:
+                    q_t["first"] = ring.tile([P, ROW], BF16, name="slot0", align_bytes=64)
+                return q_t["first"][:, H * lo : H * hi]
+            if k not in q_t:
+                q_t[k] = sb.tile([P, 2 * ROW], BF16, name="q", bufs=2, align_bytes=64)
+            return q_t[k][:, H * lo : H * hi]
 
         def bank_pairs(k, lo):
             return bank_t[k, lo][:].rearrange("p u a r -> p (u a r)").bitcast(BF16).rearrange("p (u m e) -> p m u e", u=2, e=2)
@@ -148,10 +148,13 @@ def tile_mopn_layer_pb_t_w4_kernel(tc, hid_bytes, hid_scale, Wd, Wo_words, Wo_sc
                 in_=bank_t[k, lo][:].rearrange("p u a r -> p (a r) u"),
             )
 
-        def quant(i):
-            c_t[i] = sb.tile([P, D], U32, name="codes", align_bytes=64)
-            s_t[i] = sb.tile([P, D], U8, name="scales", align_bytes=64)
-            nc.vector.quantize_mx(out=c_t[i][:].bitcast(F8X4), scales=s_t[i][:], in_=q_t[i][:])
+        def quant(k, lo, hi):
+            codes = sb.tile([P, (hi - lo) * P], U32, name="codes", align_bytes=64)
+            scales = sb.tile([P, (hi - lo) * P], U8, name="scales", align_bytes=64)
+            nc.vector.quantize_mx(out=codes[:].bitcast(F8X4), scales=scales[:], in_=q_cols(k, lo, hi))
+            for u in range(lo, hi):
+                cols = slice(P * (u - lo), P * (u - lo + 1))
+                c_t[k, u], s_t[k, u] = codes[:, cols], scales[:, cols]
 
         def down(i):
             jp_t[i] = ps.tile([P, D], F32, name="for_scalar")
@@ -159,8 +162,8 @@ def tile_mopn_layer_pb_t_w4_kernel(tc, hid_bytes, hid_scale, Wd, Wo_words, Wo_sc
                 cols = slice(P * n, P * (n + 1))
                 nc.tensor.matmul_mx(
                     out=jp_t[i][:, cols],
-                    lhsT=c_t[i][:, cols].bitcast(F8X4),
-                    lhsT_scale=s_t[i][:, cols],
+                    lhsT=c_t[i // 2, NS * (i % 2) + n].bitcast(F8X4),
+                    lhsT_scale=s_t[i // 2, NS * (i % 2) + n],
                     rhs=w_codes[:, cols].bitcast(F8X4),
                     rhs_scale=w_scales[:, cols],
                     start=True,
@@ -179,7 +182,8 @@ def tile_mopn_layer_pb_t_w4_kernel(tc, hid_bytes, hid_scale, Wd, Wo_words, Wo_sc
                     nc.tensor.transpose(jt_t[tiles][:, u, z, :], words[:, P * u : P * (u + 1)], ident[:])
 
         def empty_j(*tiles):
-            jg_t[tiles] = sb.tile([P, len(tiles) * P, 2], F32, name="jg", align_bytes=64)
+            tag = "slot%d" % ((tiles[0] // 2 + 1) % 2) if tiles[0] < TILES - 6 else "last%d" % (tiles[0] % 4)
+            jg_t[tiles] = ring.tile([P, len(tiles) * P, 2], F32, name=tag, align_bytes=64)
             nc.scalar.copy(out=jg_t[tiles][:], in_=jt_t[tiles][:].rearrange("p u i r -> p (i r) u"))
 
         def quant_j(*tiles):
@@ -189,37 +193,79 @@ def tile_mopn_layer_pb_t_w4_kernel(tc, hid_bytes, hid_scale, Wd, Wo_words, Wo_sc
             for z, i in enumerate(tiles):
                 jc_t[i], js_t[i] = codes[:, P * z : P * (z + 1)], scales[:, P * z : P * (z + 1)]
 
+        def t_cols(i):
+            if i == TILES - 7:
+                return D
+            return T_COLS if i % 2 == 1 and i < TILES - 8 else 0
+
         def mix(i, tag="for_vector"):
-            po_t[i] = ps.tile([P, D], F32, name=tag)
+            w = D - t_cols(i)
+            po_t[i] = ps.tile([P, w], F32, name=tag)
             nc.tensor.matmul_mx(
                 out=po_t[i][:],
                 lhsT=jc_t[i].bitcast(F8X4),
                 lhsT_scale=js_t[i],
-                rhs=wo_words[:].bitcast(F4X4),
-                rhs_scale=wo_scales[:],
+                rhs=wo_words[:, : 2 * w].bitcast(F4X4),
+                rhs_scale=wo_scales[:, :w],
                 start=True,
                 stop=True,
             )
 
-        def empty_o(i):
-            k = i // 2
-            if i % 2 == 0:
-                r_t[k] = sb.tile([P, 2 * D], F32, name="res", bufs=2, align_bytes=64)
-            nc.scalar.copy(out=r_t[k][:, (i % 2) * D : (i % 2 + 1) * D], in_=po_t[i][:])
+        def mix_t(i):
+            lo = D - t_cols(i)
+            pt_t[i] = ps.tile([P, t_cols(i)], F32, name="for_scalar")
+            for c in range(0, t_cols(i), P):
+                nc.tensor.matmul_mx(
+                    out=pt_t[i][:, c : c + P],
+                    lhsT=wo_words[:, 2 * (lo + c) : 2 * (lo + c + P)].bitcast(F4X4),
+                    lhsT_scale=wo_scales[:, lo + c : lo + c + P],
+                    rhs=jc_t[i].bitcast(F8X4),
+                    rhs_scale=js_t[i],
+                    start=True,
+                    stop=True,
+                )
 
-        def add_g(k, slot):
-            o_t[k] = ring.tile([P, 2 * D], F32, name="slot%d" % slot, align_bytes=64)
-            nc.gpsimd.tensor_tensor(out=o_t[k][:], in0=r_t[k][:], in1=x_t[k][:], op=ADD)
-            nc.sync.dma_start(out=oview[k], in_=o_t[k][:])
+        def empty_t(i):
+            rt_t[i] = sb.tile([P, t_cols(i)], F32, name="rt", bufs=2, align_bytes=64)
+            nc.scalar.copy(out=rt_t[i][:], in_=pt_t[i][:])
+
+        def sum_t(i):
+            w = t_cols(i)
+            lo = (i % 2 + 1) * D - w
+            pt_t[i] = ps.tile([P, w], F32, name="for_scalar")
+            nc.tensor.matmul(out=pt_t[i][:], lhsT=ident_bf[:], rhs=x_t[i // 2][:, lo : lo + w], start=True, stop=False)
+            for c in range(0, w, P):
+                nc.tensor.matmul(out=pt_t[i][:, c : c + P], lhsT=rt_t[i][:, c : c + P], rhs=ident[:], is_transpose=True, start=False, stop=c + P == w)
+
+        def o_tile(k):
+            if k not in o_t:
+                o_t[k] = sb.tile([P, 2 * D], F32, name="o", bufs=4, align_bytes=64)
+            return o_t[k]
+
+        def empty_sum(i):
+            lo = (i % 2 + 1) * D - t_cols(i)
+            nc.scalar.copy(out=o_tile(i // 2)[:, lo : lo + t_cols(i)], in_=pt_t[i][:])
+
+        def empty_o(i):
+            r_t[i] = sb.tile([P, D], F32, name="res", bufs=1, align_bytes=64)
+            nc.scalar.copy(out=r_t[i][:], in_=po_t[i][:])
+
+        def store(i, lo=0, w=D):
+            cols = slice((i % 2) * D + lo, (i % 2) * D + lo + w)
+            nc.sync.dma_start(out=oview[i // 2][:, cols], in_=o_tile(i // 2)[:, cols])
+
+        def add_g(i):
+            cols = slice((i % 2) * D, (i % 2 + 1) * D)
+            nc.gpsimd.tensor_tensor(out=o_tile(i // 2)[:, cols], in0=r_t[i][:], in1=x_t[i // 2][:, cols], op=ADD)
+            store(i)
 
         def add(i):
             k = i // 2
-            if i % 2 == 0:
-                o_t[k] = sb.tile([P, 2 * D], F32, name="o", bufs=4, align_bytes=64)
+            w = D - t_cols(i)
             parts = 2 if i == TILES - 1 else 1
-            for lo in range(0, D, D // parts):
-                cols = slice((i % 2) * D + lo, (i % 2) * D + lo + D // parts)
-                nc.vector.tensor_tensor(out=o_t[k][:, cols], in0=po_t[i][:, lo : lo + D // parts], in1=x_t[k][:, cols], op=ADD)
+            for lo in range(0, w, w // parts):
+                cols = slice((i % 2) * D + lo, (i % 2) * D + lo + w // parts)
+                nc.vector.tensor_tensor(out=o_tile(k)[:, cols], in0=po_t[i][:, lo : lo + w // parts], in1=x_t[k][:, cols], op=ADD)
                 if k >= PAIRS - SINGLE_STORES:
                     nc.sync.dma_start(out=oview[k][:, cols], in_=o_t[k][:, cols])
             if k < PAIRS - SINGLE_STORES and i % 2 == 1:
@@ -234,6 +280,7 @@ def tile_mopn_layer_pb_t_w4_kernel(tc, hid_bytes, hid_scale, Wd, Wo_words, Wo_sc
         nc.sync.dma_start(out=w_raw[:].rearrange("p n j d -> p n (j d)"), in_=Wd.rearrange("n (p j) d -> p n (j d)", j=4))
         load_hid(2)
         make_identity(nc, ident[:])
+        make_identity(nc, ident_bf[:])
         nc.vector.memset(wo_scales[:].bitcast(I32), 0)
         nc.sync.dma_start(out=wo_words[:], in_=Wo_words[0])
         wos = Wo_scales[0].bitcast(I32)
@@ -259,7 +306,8 @@ def tile_mopn_layer_pb_t_w4_kernel(tc, hid_bytes, hid_scale, Wd, Wo_words, Wo_sc
             turn_v(0, lo, hi)
             scale_v(0, lo, hi)
         widen_v(1, 0, 2)
-        nc.scalar.copy(out=w_grp[:], in_=w_raw[:].rearrange("p n j d -> p n d j"))
+        w_grp = ring.tile([P, NS, DS, 4], BF16, name="slot1", align_bytes=64)
+        nc.scalar.copy(out=w_grp[:].rearrange("p n (c i) j -> p n c j i", i=4), in_=w_raw[:].rearrange("p n j (c i) -> p n c j i", i=4))
         widen_g(2)
         widen_v(1, 2, v_units(1))
         turn_v(1, 0, 2)
@@ -269,7 +317,6 @@ def tile_mopn_layer_pb_t_w4_kernel(tc, hid_bytes, hid_scale, Wd, Wo_words, Wo_sc
             a, b = 2 * p - 2, 2 * p - 1
             c, d = 2 * (p - BACK), 2 * (p - BACK) + 1
             last = p == PAIRS - 1
-            adds = (c, d) if BACK <= p < PAIRS - LATE else ()
             if p + 3 < PAIRS:
                 load_hid(p + 3)
             load_x(p)
@@ -277,75 +324,87 @@ def tile_mopn_layer_pb_t_w4_kernel(tc, hid_bytes, hid_scale, Wd, Wo_words, Wo_sc
                 widen_v(p + 1, 0, v_units(p + 1))
             for lo, hi in by_bank(v_units(p), UNITS):
                 turn_g(p, lo, hi)
-            if p >= 2:
-                turn_j(a - 2, b - 2)
+            if last:
+                turn_v(p, NS, v_units(p))
             if p == 1:
                 turn_v(1, 2, 4)
-                quant(b)
-                quant(a)
                 nc.vector.quantize_mx(out=w_codes[:].bitcast(F8X4), scales=w_scales[:], in_=w_grp[:].rearrange("p n d j -> p (n d j)"))
+            if c >= 0:
+                quant_j(c, d)
+            if p == 2:
+                quant(p - 1, 0, NS)
+                quant(p - 1, NS, UNITS)
             else:
-                if c >= 0:
-                    quant_j(c, d)
-                quant(a)
-                quant(b)
+                quant(p - 1, 0, UNITS)
             if not last:
                 scale_g(p + 1)
-            elif G_ADDS:
-                add_g(p - BACK - 1, 0)
             for lo, hi in by_bank(v_units(p), UNITS):
                 empty_g(p, lo, hi)
-            if p >= 2:
-                empty_j(a - 2, b - 2)
             if p == 1:
                 widen_v(p + 1, 0, v_units(p + 1))
-            for i in adds:
-                mix(i)
+            if p >= 2:
+                turn_j(a - 2, b - 2)
+                empty_j(a - 2, b - 2)
+            if c >= 0 and not last:
+                mix_t(d)
+                empty_t(d)
+                mix(c)
+                mix(d)
             down(a)
             down(b)
+            if last:
+                mix_t(d)
             scale_v(p, 0, 2)
             round_j(a)
             round_j(b)
-            if v_units(p) > NS:
+            if c >= 0 and not last:
+                sum_t(d)
+                empty_sum(d)
+            if last:
+                empty_t(d)
+            if not last:
                 turn_v(p, NS, v_units(p))
             scale_v(p, 2, 4)
             if p + 2 < PAIRS:
                 widen_g(p + 2)
             if not last:
                 turn_v(p + 1, 0, 2)
-            for i in adds:
-                add(i)
-            if v_units(p) > NS:
-                scale_v(p, NS, v_units(p))
+            if c >= 0 and not last:
+                add(c)
+                add(d)
+            scale_v(p, NS, v_units(p))
             if not last:
                 turn_v(p + 1, 2, 4)
 
-        first = n - 2 * BACK - 2 * LATE
         turn_j(n - 4, n - 3)
+        sum_t(n - 7)
         empty_j(n - 4, n - 3)
-        mix(first)
-        mix(first + 1)
-        quant(n - 2)
-        quant(n - 1)
-        for i in range(n - 2 * BACK, n - 2, 2):
-            quant_j(i, i + 1)
+        empty_sum(n - 7)
+        store(n - 7)
+        mix(n - 8)
+        quant(PAIRS - 1, 0, NS)
+        quant(PAIRS - 1, NS, UNITS)
+        quant_j(n - 6, n - 5)
         down(n - 2)
         down(n - 1)
         round_j(n - 2)
         round_j(n - 1)
-        mix(first + 2)
-        mix(first + 3)
+        add(n - 8)
+        quant_j(n - 4, n - 3)
+        mix(n - 6)
+        mix(n - 5)
         turn_j(n - 2)
         empty_j(n - 2)
         turn_j(n - 1)
         empty_j(n - 1)
-        for i in range(first, n):
-            if i == n - 4:
-                quant_j(n - 2)
-            if i == n - 3:
-                quant_j(n - 1)
+        mix(n - 4)
+        mix(n - 3)
+        add(n - 6)
+        add(n - 5)
+        quant_j(n - 2)
+        mix(n - 2)
+        add(n - 4)
+        quant_j(n - 1)
+        mix(n - 1)
+        for i in range(n - 3, n):
             add(i)
-            if i + 4 < n - 2:
-                mix(i + 4)
-            if i == n - 4 or i == n - 3:
-                mix(i + 2)

@@ -32,6 +32,8 @@ LATE = 1
 BACK = 3
 G_ADDS = 0
 T_COLS = 256
+T_ODD = 256
+G_COLS = 32
 SINGLE_STORES = 4
 FLOPS = 2 * TOKENS * NS * H * DS + 2 * TOKENS * D * D
 
@@ -131,8 +133,8 @@ def tile_mopn_layer_pb_t_w4_kernel(tc, hid_bytes, hid_scale, Wd, Wo_words, Wo_sc
         def scale_v(k, lo, hi, skip=0):
             m = (hi - lo) * P - skip
             nc.vector.tensor_tensor(
-                out=q_cols(k, lo, hi).rearrange("p (m u e) -> p m u e", u=2, e=2)[:, skip:],
-                in0=bank_pairs(k, lo)[:, skip:],
+                out=q_cols(k, lo, hi).rearrange("p (m u e) -> p m u e", u=2, e=2)[:, :m],
+                in0=bank_pairs(k, lo)[:, :m],
                 in1=scale_p[:].rearrange("p (u e) -> p u e", u=2).unsqueeze(1).to_broadcast([P, m, 2, 2]),
                 op=MULT,
             )
@@ -141,6 +143,22 @@ def tile_mopn_layer_pb_t_w4_kernel(tc, hid_bytes, hid_scale, Wd, Wo_words, Wo_sc
             dst = q_cols(k, lo, hi).rearrange("p (m t) -> p m t", t=4)
             for t in range(4):
                 nc.scalar.activation(out=dst[:, :m, t], in_=bank_pairs(k, lo)[:, :m, t // 2, t % 2], func=COPY, scale=scale_p[:, t : t + 1])
+
+        def copy_words(k):
+            words = sb.tile([P, G_COLS + P, 2], F32, name="words", bufs=1, align_bytes=64)
+            if G_COLS:
+                nc.scalar.copy(out=words[:, :G_COLS, :], in_=bank_t[k, 2][:].rearrange("p u a r -> p (a r) u")[:, 2 * P - G_COLS :, :])
+            nc.scalar.copy(out=words[:, G_COLS:, :], in_=bank_t[k, NS][:].rearrange("p u a r -> p (a r) u"))
+            return words
+
+        def scale_turned(k, words):
+            m = G_COLS + P
+            nc.gpsimd.tensor_tensor(
+                out=q_cols(k, NS - 1, NS + 1)[:, 2 * H - 4 * m :].rearrange("p (m t) -> p m t", t=4),
+                in0=words[:].rearrange("p m u -> p (m u)").bitcast(BF16).rearrange("p (m t) -> p m t", t=4),
+                in1=scale_p[:].unsqueeze(1).to_broadcast([P, m, 4]),
+                op=MULT,
+            )
 
         def empty_g(k, lo, hi):
             nc.scalar.copy(
@@ -182,7 +200,7 @@ def tile_mopn_layer_pb_t_w4_kernel(tc, hid_bytes, hid_scale, Wd, Wo_words, Wo_sc
                     nc.tensor.transpose(jt_t[tiles][:, u, z, :], words[:, P * u : P * (u + 1)], ident[:])
 
         def empty_j(*tiles):
-            tag = "slot%d" % ((tiles[0] // 2 + 1) % 2) if tiles[0] < TILES - 6 else "last%d" % (tiles[0] % 4)
+            tag = "slot%d" % ((tiles[0] // 2 + 1) % 2) if tiles[0] < TILES - 4 else "last%d" % (tiles[0] % 4)
             jg_t[tiles] = ring.tile([P, len(tiles) * P, 2], F32, name=tag, align_bytes=64)
             nc.scalar.copy(out=jg_t[tiles][:], in_=jt_t[tiles][:].rearrange("p u i r -> p (i r) u"))
 
@@ -194,22 +212,21 @@ def tile_mopn_layer_pb_t_w4_kernel(tc, hid_bytes, hid_scale, Wd, Wo_words, Wo_sc
                 jc_t[i], js_t[i] = codes[:, P * z : P * (z + 1)], scales[:, P * z : P * (z + 1)]
 
         def t_cols(i):
-            if i == TILES - 7:
-                return D
-            return T_COLS if i % 2 == 1 and i < TILES - 8 else 0
+            return (T_COLS if i % 4 == 1 else T_ODD) if i % 2 == 1 and i < TILES - 8 else 0
 
         def mix(i, tag="for_vector"):
             w = D - t_cols(i)
             po_t[i] = ps.tile([P, w], F32, name=tag)
-            nc.tensor.matmul_mx(
-                out=po_t[i][:],
-                lhsT=jc_t[i].bitcast(F8X4),
-                lhsT_scale=js_t[i],
-                rhs=wo_words[:, : 2 * w].bitcast(F4X4),
-                rhs_scale=wo_scales[:, :w],
-                start=True,
-                stop=True,
-            )
+            for lo, hi in ((0, w),) if w != 3 * P else ((0, 2 * P), (2 * P, w)):
+                nc.tensor.matmul_mx(
+                    out=po_t[i][:, lo:hi],
+                    lhsT=jc_t[i].bitcast(F8X4),
+                    lhsT_scale=js_t[i],
+                    rhs=wo_words[:, 2 * lo : 2 * hi].bitcast(F4X4),
+                    rhs_scale=wo_scales[:, lo:hi],
+                    start=True,
+                    stop=True,
+                )
 
         def mix_t(i):
             lo = D - t_cols(i)
@@ -256,13 +273,14 @@ def tile_mopn_layer_pb_t_w4_kernel(tc, hid_bytes, hid_scale, Wd, Wo_words, Wo_sc
 
         def add_g(i):
             cols = slice((i % 2) * D, (i % 2 + 1) * D)
-            nc.gpsimd.tensor_tensor(out=o_tile(i // 2)[:, cols], in0=r_t[i][:], in1=x_t[i // 2][:, cols], op=ADD)
-            store(i)
+            o = ring.tile([P, D], F32, name="slot0", align_bytes=64)
+            nc.gpsimd.tensor_tensor(out=o[:], in0=r_t[i][:], in1=x_t[i // 2][:, cols], op=ADD)
+            nc.sync.dma_start(out=oview[i // 2][:, cols], in_=o[:])
 
         def add(i):
             k = i // 2
             w = D - t_cols(i)
-            parts = 2 if i == TILES - 1 else 1
+            parts = 2 if i == TILES - 2 else 1
             for lo in range(0, w, w // parts):
                 cols = slice((i % 2) * D + lo, (i % 2) * D + lo + w // parts)
                 nc.vector.tensor_tensor(out=o_tile(k)[:, cols], in0=po_t[i][:, lo : lo + w // parts], in1=x_t[k][:, cols], op=ADD)
@@ -317,18 +335,26 @@ def tile_mopn_layer_pb_t_w4_kernel(tc, hid_bytes, hid_scale, Wd, Wo_words, Wo_sc
             a, b = 2 * p - 2, 2 * p - 1
             c, d = 2 * (p - BACK), 2 * (p - BACK) + 1
             last = p == PAIRS - 1
+            adds = c >= 0 and not last
             if p + 3 < PAIRS:
                 load_hid(p + 3)
             load_x(p)
             if not last and p > 1:
                 widen_v(p + 1, 0, v_units(p + 1))
-            for lo, hi in by_bank(v_units(p), UNITS):
-                turn_g(p, lo, hi)
             if last:
                 turn_v(p, NS, v_units(p))
+                words = copy_words(p)
+            for lo, hi in by_bank(v_units(p), UNITS):
+                turn_g(p, lo, hi)
+                empty_g(p, lo, hi)
             if p == 1:
                 turn_v(1, 2, 4)
+                widen_v(p + 1, 0, v_units(p + 1))
                 nc.vector.quantize_mx(out=w_codes[:].bitcast(F8X4), scales=w_scales[:], in_=w_grp[:].rearrange("p n d j -> p (n d j)"))
+            if p >= 2:
+                turn_j(a - 2, b - 2)
+            if not last:
+                turn_v(p, NS, v_units(p))
             if c >= 0:
                 quant_j(c, d)
             if p == 2:
@@ -338,73 +364,70 @@ def tile_mopn_layer_pb_t_w4_kernel(tc, hid_bytes, hid_scale, Wd, Wo_words, Wo_sc
                 quant(p - 1, 0, UNITS)
             if not last:
                 scale_g(p + 1)
-            for lo, hi in by_bank(v_units(p), UNITS):
-                empty_g(p, lo, hi)
-            if p == 1:
-                widen_v(p + 1, 0, v_units(p + 1))
+            else:
+                scale_turned(p, words)
             if p >= 2:
-                turn_j(a - 2, b - 2)
                 empty_j(a - 2, b - 2)
-            if c >= 0 and not last:
+            if adds:
                 mix_t(d)
                 empty_t(d)
+            if c >= 0:
                 mix(c)
-                mix(d)
+            if True and p + 2 < PAIRS:
+                widen_g(p + 2)
             down(a)
             down(b)
             if last:
-                mix_t(d)
+                mix(d, "for_scalar")
             scale_v(p, 0, 2)
+            if adds:
+                mix(d)
             round_j(a)
             round_j(b)
-            if c >= 0 and not last:
+            if adds:
                 sum_t(d)
                 empty_sum(d)
             if last:
-                empty_t(d)
-            if not last:
-                turn_v(p, NS, v_units(p))
-            scale_v(p, 2, 4)
-            if p + 2 < PAIRS:
+                empty_o(d)
+            scale_v(p, 2, 4, G_COLS if last else 0)
+            if not True and p + 2 < PAIRS:
                 widen_g(p + 2)
             if not last:
                 turn_v(p + 1, 0, 2)
-            if c >= 0 and not last:
+            if not last:
+                scale_v(p, NS, v_units(p))
+                turn_v(p + 1, 2, 4)
+            if adds:
                 add(c)
                 add(d)
-            scale_v(p, NS, v_units(p))
-            if not last:
-                turn_v(p + 1, 2, 4)
 
         turn_j(n - 4, n - 3)
-        sum_t(n - 7)
         empty_j(n - 4, n - 3)
-        empty_sum(n - 7)
-        store(n - 7)
-        mix(n - 8)
-        quant(PAIRS - 1, 0, NS)
         quant(PAIRS - 1, NS, UNITS)
         quant_j(n - 6, n - 5)
-        down(n - 2)
+        quant(PAIRS - 1, 0, NS)
         down(n - 1)
-        round_j(n - 2)
-        round_j(n - 1)
-        add(n - 8)
-        quant_j(n - 4, n - 3)
         mix(n - 6)
+        down(n - 2)
+        round_j(n - 1)
+        round_j(n - 2)
+        add(n - 8)
+        add_g(n - 7)
         mix(n - 5)
-        turn_j(n - 2)
-        empty_j(n - 2)
+        add(n - 6)
+        quant_j(n - 4, n - 3)
         turn_j(n - 1)
         empty_j(n - 1)
+        turn_j(n - 2)
+        empty_j(n - 2)
         mix(n - 4)
         mix(n - 3)
-        add(n - 6)
         add(n - 5)
-        quant_j(n - 2)
-        mix(n - 2)
-        add(n - 4)
         quant_j(n - 1)
         mix(n - 1)
-        for i in range(n - 3, n):
-            add(i)
+        quant_j(n - 2)
+        add(n - 4)
+        mix(n - 2)
+        add(n - 3)
+        add(n - 1)
+        add(n - 2)

@@ -27,13 +27,23 @@ UNITS = 2 * NS
 G_UNITS = 3
 G_FIRST = 3
 G_SECOND = 2
-G_LAST = 3
-LATE = 1
-BACK = 3
-G_ADDS = 0
-T_COLS = 256
-T_ODD = 256
+G_THIRD = 3
+G_GROUP = 0
+S_LATE = 0
 G_COLS = 32
+G_MID = 0
+Z_COLS = 0
+MID_FROM = 3
+BACK = 3
+T_COLS = 256
+T_WIDE = 384
+WIDE_FROM = 20
+WIDE_STEP = 1
+SHARE = 1
+PACK = 0
+PLAIN = 0
+SPLIT = 0
+V_BANKS = 4
 SINGLE_STORES = 4
 FLOPS = 2 * TOKENS * NS * H * DS + 2 * TOKENS * D * D
 
@@ -50,7 +60,7 @@ def tile_mopn_layer_pb_t_w4_kernel(tc, hid_bytes, hid_scale, Wd, Wo_words, Wo_sc
         loads = ctx.enter_context(tc.tile_pool(name="loads", bufs=5))
         sb = ctx.enter_context(tc.tile_pool(name="sb", bufs=3))
         ring = ctx.enter_context(tc.tile_pool(name="ring", bufs=1))
-        ps = ctx.enter_context(tc.psum_pool(name="ps", bufs=4))
+        ps = ctx.enter_context(tc.psum_pool(name="ps", bufs=1))
 
         ctx.enter_context(tc.manual_schedule())
 
@@ -64,16 +74,26 @@ def tile_mopn_layer_pb_t_w4_kernel(tc, hid_bytes, hid_scale, Wd, Wo_words, Wo_sc
         wo_words = keep.tile([P, 2 * D], U8, align_bytes=64)
         wo_scales = keep.tile([P, D], U8, align_bytes=64)
 
-        hb_t, x_t, xv_t, xg_t, gs_t, bank_t, q_t, c_t, s_t, jp_t, jb_t, jt_t, jg_t, jc_t, js_t, po_t, o_t, r_t, pt_t, rt_t = ({} for z in range(20))
+        hb_t, x_t, xv_t, xg_t, gs_t, bank_t, room_t, q_t, c_t, s_t = ({} for z in range(10))
+        jp_t, jb_t, jt_t, jg_t, jc_t, js_t, po_t, pt_t, rt_t, o_t = ({} for z in range(10))
+
+        def bank(tag):
+            tile = ps.tile([P, D], F32, name=tag, bufs=V_BANKS if tag == "for_vector" else 8 - V_BANKS)
+            return tile[:]
 
         def g_units(k):
-            return {0: 0, 1: G_FIRST, 2: G_SECOND, PAIRS - 1: G_LAST}.get(k, G_UNITS)
+            return {0: 0, 1: G_FIRST, 2: G_SECOND, 3: G_THIRD}.get(k, G_UNITS)
 
         def v_units(k):
             return UNITS - g_units(k)
 
         def by_bank(lo, hi):
             return [(u, min(u + 2, hi)) for u in range(lo, hi, 2)]
+
+        def t_cols(i):
+            if i % 2 == 0 or i >= TILES - 8:
+                return 0
+            return T_WIDE if i // 2 >= WIDE_FROM and (i // 2 - WIDE_FROM) % WIDE_STEP == 0 else T_COLS
 
         def load_hid(k, lo=0, hi=UNITS):
             if k not in hb_t:
@@ -104,19 +124,25 @@ def tile_mopn_layer_pb_t_w4_kernel(tc, hid_bytes, hid_scale, Wd, Wo_words, Wo_sc
                 op=MULT,
             )
 
-        def turn_v(k, lo, hi):
-            bank_t[k, lo] = ps.tile([P, 2, hi - lo, P], F32, name="for_vector")
+        def turned(k, lo, hi, tag):
+            whole = bank(tag)
+            words = 2 * P * (hi - lo)
+            bank_t[k, lo], room_t[k] = whole[:, :words].rearrange("p (u a r) -> p u a r", u=2, r=P), whole[:, words:]
+            return bank_t[k, lo]
+
+        def turn_v(k, lo, hi, tag="for_vector"):
+            dst = turned(k, lo, hi, tag)
             for a in range(hi - lo):
                 words = xv_t[k, lo + a].bitcast(F32)
                 for u in range(2):
-                    nc.tensor.transpose(bank_t[k, lo][:, u, a, :], words[:, u::2], ident[:])
+                    nc.tensor.transpose(dst[:, u, a, :], words[:, u::2], ident[:])
 
         def turn_g(k, lo, hi):
-            bank_t[k, lo] = ps.tile([P, 2, hi - lo, P], F32, name="for_scalar")
+            dst = turned(k, lo, hi, "for_scalar")
             words = gs_t[k][:].rearrange("r u n p e -> r u n (p e)").bitcast(F32)
             for a in range(hi - lo):
                 for u in range(2):
-                    nc.tensor.transpose(bank_t[k, lo][:, u, a, :], words[:, u, lo - v_units(k) + a, :], ident[:])
+                    nc.tensor.transpose(dst[:, u, a, :], words[:, u, lo - v_units(k) + a, :], ident[:])
 
         def q_cols(k, lo, hi):
             if k == 1 and lo < NS:
@@ -127,43 +153,41 @@ def tile_mopn_layer_pb_t_w4_kernel(tc, hid_bytes, hid_scale, Wd, Wo_words, Wo_sc
                 q_t[k] = sb.tile([P, 2 * ROW], BF16, name="q", bufs=2, align_bytes=64)
             return q_t[k][:, H * lo : H * hi]
 
-        def bank_pairs(k, lo):
-            return bank_t[k, lo][:].rearrange("p u a r -> p (u a r)").bitcast(BF16).rearrange("p (u m e) -> p m u e", u=2, e=2)
-
-        def scale_v(k, lo, hi, skip=0):
-            m = (hi - lo) * P - skip
+        def scale_v(k, lo, hi, less=0):
+            m = (hi - lo) * P - less
+            pairs = bank_t[k, lo].rearrange("p u a r -> p (u a r)").bitcast(BF16).rearrange("p (u m e) -> p m u e", u=2, e=2)
             nc.vector.tensor_tensor(
                 out=q_cols(k, lo, hi).rearrange("p (m u e) -> p m u e", u=2, e=2)[:, :m],
-                in0=bank_pairs(k, lo)[:, :m],
+                in0=pairs[:, :m],
                 in1=scale_p[:].rearrange("p (u e) -> p u e", u=2).unsqueeze(1).to_broadcast([P, m, 2, 2]),
                 op=MULT,
             )
 
-        def scale_s(k, lo, hi, m):
-            dst = q_cols(k, lo, hi).rearrange("p (m t) -> p m t", t=4)
+        def scale_s(k, m):
+            pairs = bank_t[k, NS].rearrange("p u a r -> p (u a r)").bitcast(BF16).rearrange("p (u m e) -> p m u e", u=2, e=2)
+            dst = q_cols(k, NS, NS + 1).rearrange("p (m t) -> p m t", t=4)
             for t in range(4):
-                nc.scalar.activation(out=dst[:, :m, t], in_=bank_pairs(k, lo)[:, :m, t // 2, t % 2], func=COPY, scale=scale_p[:, t : t + 1])
+                nc.scalar.activation(out=dst[:, P - m :, t], in_=pairs[:, P - m :, t // 2, t % 2], func=COPY, scale=scale_p[:, t : t + 1])
 
-        def copy_words(k):
-            words = sb.tile([P, G_COLS + P, 2], F32, name="words", bufs=1, align_bytes=64)
-            if G_COLS:
-                nc.scalar.copy(out=words[:, :G_COLS, :], in_=bank_t[k, 2][:].rearrange("p u a r -> p (a r) u")[:, 2 * P - G_COLS :, :])
-            nc.scalar.copy(out=words[:, G_COLS:, :], in_=bank_t[k, NS][:].rearrange("p u a r -> p (a r) u"))
+        def bank_words(k, lo):
+            return bank_t[k, lo].rearrange("p u a r -> p (a r) u")
+
+        def empty_g(k, lo, hi):
+            nc.scalar.copy(out=q_cols(k, lo, hi).bitcast(F32).rearrange("p (m u) -> p m u", u=2), in_=bank_words(k, lo))
+
+        def copy_words(k, m, tag):
+            words = ring.tile([P, m, 2], F32, name=tag, align_bytes=64)
+            if m > P:
+                nc.scalar.copy(out=words[:, : m - P, :], in_=bank_words(k, 2)[:, 3 * P - m :, :])
+            nc.scalar.copy(out=words[:, max(m - P, 0) :, :], in_=bank_words(k, NS)[:, max(P - m, 0) :, :])
             return words
 
-        def scale_turned(k, words):
-            m = G_COLS + P
+        def scale_turned(k, m, words):
             nc.gpsimd.tensor_tensor(
                 out=q_cols(k, NS - 1, NS + 1)[:, 2 * H - 4 * m :].rearrange("p (m t) -> p m t", t=4),
                 in0=words[:].rearrange("p m u -> p (m u)").bitcast(BF16).rearrange("p (m t) -> p m t", t=4),
                 in1=scale_p[:].unsqueeze(1).to_broadcast([P, m, 4]),
                 op=MULT,
-            )
-
-        def empty_g(k, lo, hi):
-            nc.scalar.copy(
-                out=q_cols(k, lo, hi).bitcast(F32).rearrange("p (m u) -> p m u", u=2),
-                in_=bank_t[k, lo][:].rearrange("p u a r -> p (a r) u"),
             )
 
         def quant(k, lo, hi):
@@ -175,7 +199,7 @@ def tile_mopn_layer_pb_t_w4_kernel(tc, hid_bytes, hid_scale, Wd, Wo_words, Wo_sc
                 c_t[k, u], s_t[k, u] = codes[:, cols], scales[:, cols]
 
         def down(i):
-            jp_t[i] = ps.tile([P, D], F32, name="for_scalar")
+            jp_t[i] = bank("for_scalar")
             for n in range(NS):
                 cols = slice(P * n, P * (n + 1))
                 nc.tensor.matmul_mx(
@@ -190,10 +214,10 @@ def tile_mopn_layer_pb_t_w4_kernel(tc, hid_bytes, hid_scale, Wd, Wo_words, Wo_sc
 
         def round_j(i):
             jb_t[i] = sb.tile([P, 2, P, 2], BF16, name="jb", bufs=4, align_bytes=64)
-            nc.scalar.copy(out=jb_t[i][:], in_=jp_t[i][:].rearrange("r (p u e) -> r u p e", u=2, e=2))
+            nc.scalar.copy(out=jb_t[i][:], in_=jp_t[i].rearrange("r (p u e) -> r u p e", u=2, e=2))
 
         def turn_j(*tiles):
-            jt_t[tiles] = ps.tile([P, 2, len(tiles), P], F32, name="for_scalar")
+            jt_t[tiles] = bank("for_scalar")[:, : 2 * P * len(tiles)].rearrange("p (u i r) -> p u i r", u=2, r=P)
             for z, i in enumerate(tiles):
                 words = jb_t[i][:].rearrange("r u p e -> r (u p e)").bitcast(F32)
                 for u in range(2):
@@ -202,7 +226,7 @@ def tile_mopn_layer_pb_t_w4_kernel(tc, hid_bytes, hid_scale, Wd, Wo_words, Wo_sc
         def empty_j(*tiles):
             tag = "slot%d" % ((tiles[0] // 2 + 1) % 2) if tiles[0] < TILES - 4 else "last%d" % (tiles[0] % 4)
             jg_t[tiles] = ring.tile([P, len(tiles) * P, 2], F32, name=tag, align_bytes=64)
-            nc.scalar.copy(out=jg_t[tiles][:], in_=jt_t[tiles][:].rearrange("p u i r -> p (i r) u"))
+            nc.scalar.copy(out=jg_t[tiles][:], in_=jt_t[tiles].rearrange("p u i r -> p (i r) u"))
 
         def quant_j(*tiles):
             codes = sb.tile([P, len(tiles) * P], U32, name="jcodes", bufs=5, align_bytes=64)
@@ -211,26 +235,22 @@ def tile_mopn_layer_pb_t_w4_kernel(tc, hid_bytes, hid_scale, Wd, Wo_words, Wo_sc
             for z, i in enumerate(tiles):
                 jc_t[i], js_t[i] = codes[:, P * z : P * (z + 1)], scales[:, P * z : P * (z + 1)]
 
-        def t_cols(i):
-            return (T_COLS if i % 4 == 1 else T_ODD) if i % 2 == 1 and i < TILES - 8 else 0
-
-        def mix(i, tag="for_vector"):
+        def mix(i, dst):
             w = D - t_cols(i)
-            po_t[i] = ps.tile([P, w], F32, name=tag)
-            for lo, hi in ((0, w),) if w != 3 * P else ((0, 2 * P), (2 * P, w)):
-                nc.tensor.matmul_mx(
-                    out=po_t[i][:, lo:hi],
-                    lhsT=jc_t[i].bitcast(F8X4),
-                    lhsT_scale=js_t[i],
-                    rhs=wo_words[:, 2 * lo : 2 * hi].bitcast(F4X4),
-                    rhs_scale=wo_scales[:, lo:hi],
-                    start=True,
-                    stop=True,
-                )
+            po_t[i] = dst[:, :w]
+            nc.tensor.matmul_mx(
+                out=po_t[i],
+                lhsT=jc_t[i].bitcast(F8X4),
+                lhsT_scale=js_t[i],
+                rhs=wo_words[:, : 2 * w].bitcast(F4X4),
+                rhs_scale=wo_scales[:, :w],
+                start=True,
+                stop=True,
+            )
 
-        def mix_t(i):
+        def mix_t(i, room=None):
             lo = D - t_cols(i)
-            pt_t[i] = ps.tile([P, t_cols(i)], F32, name="for_scalar")
+            pt_t[i] = (bank("for_scalar") if room is None else room)[:, : t_cols(i)]
             for c in range(0, t_cols(i), P):
                 nc.tensor.matmul_mx(
                     out=pt_t[i][:, c : c + P],
@@ -244,15 +264,15 @@ def tile_mopn_layer_pb_t_w4_kernel(tc, hid_bytes, hid_scale, Wd, Wo_words, Wo_sc
 
         def empty_t(i):
             rt_t[i] = sb.tile([P, t_cols(i)], F32, name="rt", bufs=2, align_bytes=64)
-            nc.scalar.copy(out=rt_t[i][:], in_=pt_t[i][:])
+            nc.scalar.copy(out=rt_t[i][:], in_=pt_t[i])
 
         def sum_t(i):
             w = t_cols(i)
             lo = (i % 2 + 1) * D - w
-            pt_t[i] = ps.tile([P, w], F32, name="for_scalar")
-            nc.tensor.matmul(out=pt_t[i][:], lhsT=ident_bf[:], rhs=x_t[i // 2][:, lo : lo + w], start=True, stop=False)
+            pt_t[i] = bank("for_scalar")[:, :w]
+            nc.tensor.matmul(out=pt_t[i], lhsT=ident_bf[:], rhs=x_t[i // 2][:, lo : lo + w], start=True, stop=False)
             for c in range(0, w, P):
-                nc.tensor.matmul(out=pt_t[i][:, c : c + P], lhsT=rt_t[i][:, c : c + P], rhs=ident[:], is_transpose=True, start=False, stop=c + P == w)
+                nc.tensor.matmul(out=pt_t[i][:, c : c + P], lhsT=rt_t[i][:, c : c + P], rhs=ident[:], is_transpose=not PLAIN, start=False, stop=c + P == w)
 
         def o_tile(k):
             if k not in o_t:
@@ -261,33 +281,21 @@ def tile_mopn_layer_pb_t_w4_kernel(tc, hid_bytes, hid_scale, Wd, Wo_words, Wo_sc
 
         def empty_sum(i):
             lo = (i % 2 + 1) * D - t_cols(i)
-            nc.scalar.copy(out=o_tile(i // 2)[:, lo : lo + t_cols(i)], in_=pt_t[i][:])
+            nc.scalar.copy(out=o_tile(i // 2)[:, lo : lo + t_cols(i)], in_=pt_t[i])
 
-        def empty_o(i):
-            r_t[i] = sb.tile([P, D], F32, name="res", bufs=1, align_bytes=64)
-            nc.scalar.copy(out=r_t[i][:], in_=po_t[i][:])
-
-        def store(i, lo=0, w=D):
+        def add(i, lo=0, w=None):
+            w = D - t_cols(i) if w is None else w
             cols = slice((i % 2) * D + lo, (i % 2) * D + lo + w)
-            nc.sync.dma_start(out=oview[i // 2][:, cols], in_=o_tile(i // 2)[:, cols])
+            nc.vector.tensor_tensor(out=o_tile(i // 2)[:, cols], in0=po_t[i][:, lo : lo + w], in1=x_t[i // 2][:, cols], op=ADD)
 
-        def add_g(i):
-            cols = slice((i % 2) * D, (i % 2 + 1) * D)
-            o = ring.tile([P, D], F32, name="slot0", align_bytes=64)
-            nc.gpsimd.tensor_tensor(out=o[:], in0=r_t[i][:], in1=x_t[i // 2][:, cols], op=ADD)
-            nc.sync.dma_start(out=oview[i // 2][:, cols], in_=o[:])
+        def store(k, lo=0, w=2 * D):
+            nc.sync.dma_start(out=oview[k][:, lo : lo + w], in_=o_tile(k)[:, lo : lo + w])
 
-        def add(i):
-            k = i // 2
-            w = D - t_cols(i)
-            parts = 2 if i == TILES - 2 else 1
-            for lo in range(0, w, w // parts):
-                cols = slice((i % 2) * D + lo, (i % 2) * D + lo + w // parts)
-                nc.vector.tensor_tensor(out=o_tile(k)[:, cols], in0=po_t[i][:, lo : lo + w // parts], in1=x_t[k][:, cols], op=ADD)
-                if k >= PAIRS - SINGLE_STORES:
-                    nc.sync.dma_start(out=oview[k][:, cols], in_=o_t[k][:, cols])
-            if k < PAIRS - SINGLE_STORES and i % 2 == 1:
-                nc.sync.dma_start(out=oview[k], in_=o_t[k][:])
+        def add_store(i, parts=1):
+            w = D // parts
+            for lo in range(0, D, w):
+                add(i, lo, w)
+                store(i // 2, (i % 2) * D + lo, w)
 
         nc.sync.dma_start(out=scale_p[:], in_=srow.rearrange("(p t) -> p t", t=4))
         load_hid(0, 0, 2)
@@ -307,25 +315,26 @@ def tile_mopn_layer_pb_t_w4_kernel(tc, hid_bytes, hid_scale, Wd, Wo_words, Wo_sc
         load_hid(3)
         load_x(0)
 
-        spread = ps.tile([P, 2, 2, P], F32, name="for_scalar")
+        spread = bank("for_scalar").rearrange("r (u e p) -> r u e p", u=2, e=2)
         for t in range(4):
             nc.tensor.transpose(spread[:, t // 2, t % 2, :], scale_p[:, t : t + 1].to_broadcast([P, P]), ident[:])
         widen_v(0, 0, 1, nc.vector.tensor_copy)
         widen_v(0, 1, 2, nc.vector.tensor_copy)
-        nc.vector.tensor_copy(out=scale_row[:], in_=spread[:].rearrange("r u e p -> r u p e"))
-
+        nc.vector.tensor_copy(out=scale_row[:], in_=spread.rearrange("r u e p -> r u p e"))
         widen_v(0, 2, 4)
         widen_g(1)
         scale_g(1)
         widen_v(0, 4, 6)
         widen_v(0, 6, 8)
-        first_banks = [(0, 1), (1, 2)] + by_bank(2, UNITS)
-        for lo, hi in first_banks:
+        for lo, hi in [(0, 1), (1, 2)] + by_bank(2, UNITS):
             turn_v(0, lo, hi)
             scale_v(0, lo, hi)
         widen_v(1, 0, 2)
         w_grp = ring.tile([P, NS, DS, 4], BF16, name="slot1", align_bytes=64)
-        nc.scalar.copy(out=w_grp[:].rearrange("p n (c i) j -> p n c j i", i=4), in_=w_raw[:].rearrange("p n j (c i) -> p n c j i", i=4))
+        nc.scalar.copy(
+            out=w_grp[:].rearrange("p n (c i) j -> p n c j i", i=4),
+            in_=w_raw[:].rearrange("p n j (c i) -> p n c j i", i=4),
+        )
         widen_g(2)
         widen_v(1, 2, v_units(1))
         turn_v(1, 0, 2)
@@ -336,15 +345,17 @@ def tile_mopn_layer_pb_t_w4_kernel(tc, hid_bytes, hid_scale, Wd, Wo_words, Wo_sc
             c, d = 2 * (p - BACK), 2 * (p - BACK) + 1
             last = p == PAIRS - 1
             adds = c >= 0 and not last
+            later = by_bank(NS, v_units(p))
             if p + 3 < PAIRS:
                 load_hid(p + 3)
             load_x(p)
             if not last and p > 1:
                 widen_v(p + 1, 0, v_units(p + 1))
             if last:
-                turn_v(p, NS, v_units(p))
-                words = copy_words(p)
-            for lo, hi in by_bank(v_units(p), UNITS):
+                quant_j(c, d)
+                words = copy_words(p, G_COLS + P, "slot1")
+            both = adds and t_cols(d) <= 2 * P and PACK
+            for lo, hi in by_bank(v_units(p), UNITS)[: 1 if both else 2]:
                 turn_g(p, lo, hi)
                 empty_g(p, lo, hi)
             if p == 1:
@@ -353,9 +364,13 @@ def tile_mopn_layer_pb_t_w4_kernel(tc, hid_bytes, hid_scale, Wd, Wo_words, Wo_sc
                 nc.vector.quantize_mx(out=w_codes[:].bitcast(F8X4), scales=w_scales[:], in_=w_grp[:].rearrange("p n d j -> p (n d j)"))
             if p >= 2:
                 turn_j(a - 2, b - 2)
+            if both:
+                turn_g(p, UNITS - 1, UNITS)
+                spare = room_t[p]
             if not last:
-                turn_v(p, NS, v_units(p))
-            if c >= 0:
+                for lo, hi in later:
+                    turn_v(p, lo, hi)
+            if adds:
                 quant_j(c, d)
             if p == 2:
                 quant(p - 1, 0, NS)
@@ -365,41 +380,62 @@ def tile_mopn_layer_pb_t_w4_kernel(tc, hid_bytes, hid_scale, Wd, Wo_words, Wo_sc
             if not last:
                 scale_g(p + 1)
             else:
-                scale_turned(p, words)
+                scale_turned(p, G_COLS + P, words)
             if p >= 2:
                 empty_j(a - 2, b - 2)
             if adds:
-                mix_t(d)
+                mix_t(d, spare if both else None)
+                if both:
+                    empty_g(p, UNITS - 1, UNITS)
                 empty_t(d)
+                if SHARE:
+                    mix(d, room_t[p])
             if c >= 0:
-                mix(c)
-            if True and p + 2 < PAIRS:
+                mix(c, bank("for_vector"))
+            few = G_MID if MID_FROM <= p < PAIRS - 1 else 0
+            if few:
+                scale_turned(p, few, copy_words(p, few, "few%d" % (p % 2)))
+            if Z_COLS and MID_FROM <= p < PAIRS - 1:
+                few = Z_COLS
+                scale_s(p, few)
+            if p + 2 < PAIRS:
                 widen_g(p + 2)
+            scale_v(p, 0, 2)
+            if adds and p < SPLIT:
+                turn_v(p + 1, 0, 2)
             down(a)
             down(b)
             if last:
-                mix(d, "for_scalar")
-            scale_v(p, 0, 2)
-            if adds:
-                mix(d)
+                mix(d, bank("for_scalar"))
+            if adds and not SHARE and t_cols(d) < D:
+                mix(d, bank("for_vector"))
             round_j(a)
             round_j(b)
             if adds:
                 sum_t(d)
                 empty_sum(d)
             if last:
-                empty_o(d)
-            scale_v(p, 2, 4, G_COLS if last else 0)
-            if not True and p + 2 < PAIRS:
-                widen_g(p + 2)
-            if not last:
+                res = sb.tile([P, D], F32, name="res", bufs=1, align_bytes=64)
+                nc.scalar.copy(out=res[:], in_=po_t[d])
+            if not last and SHARE and p > 1 and not (adds and p < SPLIT):
                 turn_v(p + 1, 0, 2)
+            scale_v(p, 2, 4, G_COLS if last else 0)
             if not last:
-                scale_v(p, NS, v_units(p))
-                turn_v(p + 1, 2, 4)
+                if not SHARE or p == 1:
+                    turn_v(p + 1, 0, 2)
+                if SHARE and p > 1:
+                    turn_v(p + 1, 2, 4)
+                for lo, hi in later:
+                    scale_v(p, lo, hi, few)
+                if not SHARE or p == 1:
+                    turn_v(p + 1, 2, 4)
+            if p == PAIRS - 2:
+                turn_v(p + 1, NS, v_units(p + 1), "for_scalar")
             if adds:
                 add(c)
-                add(d)
+                if t_cols(d) < D:
+                    add(d)
+                store(p - BACK)
 
         turn_j(n - 4, n - 3)
         empty_j(n - 4, n - 3)
@@ -407,27 +443,29 @@ def tile_mopn_layer_pb_t_w4_kernel(tc, hid_bytes, hid_scale, Wd, Wo_words, Wo_sc
         quant_j(n - 6, n - 5)
         quant(PAIRS - 1, 0, NS)
         down(n - 1)
-        mix(n - 6)
+        mix(n - 6, bank("for_vector"))
         down(n - 2)
         round_j(n - 1)
         round_j(n - 2)
-        add(n - 8)
-        add_g(n - 7)
-        mix(n - 5)
-        add(n - 6)
+        add_store(n - 8)
+        sums = ring.tile([P, D], F32, name="slot0", align_bytes=64)
+        nc.gpsimd.tensor_tensor(out=sums[:], in0=res[:], in1=x_t[PAIRS - 4][:, D:], op=ADD)
+        mix(n - 5, bank("for_vector"))
+        add_store(n - 6)
+        nc.sync.dma_start(out=oview[PAIRS - 4][:, D:], in_=sums[:])
         quant_j(n - 4, n - 3)
         turn_j(n - 1)
         empty_j(n - 1)
         turn_j(n - 2)
         empty_j(n - 2)
-        mix(n - 4)
-        mix(n - 3)
-        add(n - 5)
+        mix(n - 4, bank("for_vector"))
+        mix(n - 3, bank("for_vector"))
+        add_store(n - 5)
         quant_j(n - 1)
-        mix(n - 1)
+        mix(n - 1, bank("for_vector"))
         quant_j(n - 2)
-        add(n - 4)
-        mix(n - 2)
-        add(n - 3)
-        add(n - 1)
-        add(n - 2)
+        add_store(n - 4)
+        mix(n - 2, bank("for_vector"))
+        add_store(n - 3)
+        add_store(n - 1)
+        add_store(n - 2, 2)

@@ -1,6 +1,7 @@
+from contextlib import ExitStack
+
 import concourse.mybir as mybir
 from concourse.masks import make_identity
-from contextlib import ExitStack
 
 F32 = mybir.dt.float32
 BF16 = mybir.dt.bfloat16
@@ -12,7 +13,6 @@ F8X4 = mybir.dt.float8_e4m3fn_x4
 F4X4 = mybir.dt.float4_e2m1fn_x4
 MULT = mybir.AluOpType.mult
 ADD = mybir.AluOpType.add
-COPY = mybir.ActivationFunctionType.Copy
 
 P = 128
 TOKENS = 4096
@@ -24,27 +24,8 @@ ROW = NS * H
 TILES = TOKENS // P
 PAIRS = TILES // 2
 UNITS = 2 * NS
-G_UNITS = 3
-G_FIRST = 3
-G_SECOND = 2
-G_THIRD = 3
-G_GROUP = 0
-S_LATE = 0
-G_COLS = 32
-G_MID = 0
-Z_COLS = 0
-MID_FROM = 3
 BACK = 3
-T_COLS = 256
-T_WIDE = 384
-WIDE_FROM = 20
-WIDE_STEP = 1
-SHARE = 1
-PACK = 0
-PLAIN = 0
-SPLIT = 0
-V_BANKS = 4
-SINGLE_STORES = 4
+HALF = 256
 FLOPS = 2 * TOKENS * NS * H * DS + 2 * TOKENS * D * D
 
 
@@ -57,13 +38,12 @@ def tile_mopn_layer_pb_t_w4_kernel(tc, hid_bytes, hid_scale, Wd, Wo_words, Wo_sc
 
     with ExitStack() as ctx:
         keep = ctx.enter_context(tc.tile_pool(name="keep", bufs=1))
-        loads = ctx.enter_context(tc.tile_pool(name="loads", bufs=5))
         sb = ctx.enter_context(tc.tile_pool(name="sb", bufs=3))
         ring = ctx.enter_context(tc.tile_pool(name="ring", bufs=1))
-        ps = ctx.enter_context(tc.psum_pool(name="ps", bufs=1))
-
+        ps = ctx.enter_context(tc.psum_pool(name="ps", bufs=4))
         ctx.enter_context(tc.manual_schedule())
 
+        hb = keep.tile([P, PAIRS * UNITS * H], U8, align_bytes=64)
         scale_p = keep.tile([P, 4], F32, align_bytes=64)
         scale_row = keep.tile([P, 2, P, 2], F32, align_bytes=64)
         ident = keep.tile([P, P], F32, align_bytes=64)
@@ -74,129 +54,83 @@ def tile_mopn_layer_pb_t_w4_kernel(tc, hid_bytes, hid_scale, Wd, Wo_words, Wo_sc
         wo_words = keep.tile([P, 2 * D], U8, align_bytes=64)
         wo_scales = keep.tile([P, D], U8, align_bytes=64)
 
-        hb_t, x_t, xv_t, xg_t, gs_t, bank_t, room_t, q_t, c_t, s_t = ({} for z in range(10))
+        x_t, wide, run_t, done, bank_t, q_t, c_t, s_t = ({} for z in range(8))
         jp_t, jb_t, jt_t, jg_t, jc_t, js_t, po_t, pt_t, rt_t, o_t = ({} for z in range(10))
 
         def bank(tag):
-            tile = ps.tile([P, D], F32, name=tag, bufs=V_BANKS if tag == "for_vector" else 8 - V_BANKS)
+            tile = ps.tile([P, D], F32, name=tag)
             return tile[:]
 
-        def g_units(k):
-            return {0: 0, 1: G_FIRST, 2: G_SECOND, 3: G_THIRD}.get(k, G_UNITS)
+        def load_hid(lo, hi):
+            k = lo // UNITS
+            nc.sync.dma_start(out=hb[:, H * lo : H * hi], in_=hid[k][:, H * (lo - UNITS * k) : H * (hi - UNITS * k)])
 
-        def v_units(k):
-            return UNITS - g_units(k)
-
-        def by_bank(lo, hi):
-            return [(u, min(u + 2, hi)) for u in range(lo, hi, 2)]
-
-        def t_cols(i):
-            if i % 2 == 0 or i >= TILES - 8:
-                return 0
-            return T_WIDE if i // 2 >= WIDE_FROM and (i // 2 - WIDE_FROM) % WIDE_STEP == 0 else T_COLS
-
-        def load_hid(k, lo=0, hi=UNITS):
-            if k not in hb_t:
-                hb_t[k] = loads.tile([P, 2 * ROW], U8, name="hb", align_bytes=64)
-            nc.sync.dma_start(out=hb_t[k][:, H * lo : H * hi], in_=hid[k][:, H * lo : H * hi])
+        def load_pair(k):
+            load_hid(UNITS * k, UNITS * (k + 1))
 
         def load_x(k):
-            x_t[k] = loads.tile([P, 2 * D], BF16, name="x", align_bytes=64)
+            x_t[k] = sb.tile([P, 2 * D], BF16, name="x", bufs=5, align_bytes=64)
             nc.sync.dma_start(out=x_t[k][:], in_=xin[k])
 
-        def widen_v(k, lo, hi, eng=nc.scalar.copy):
-            xv = sb.tile([P, (hi - lo) * H], BF16, name="xv", bufs=6, align_bytes=64)
-            eng(out=xv[:], in_=hb_t[k][:, H * lo : H * hi].bitcast(F8))
+        def widen(lo, hi, tag, bufs, eng=nc.scalar.copy):
+            tile = sb.tile([P, (hi - lo) * H], BF16, name=tag, bufs=bufs, align_bytes=64)
+            eng(out=tile[:], in_=hb[:, H * lo : H * hi].bitcast(F8))
             for u in range(lo, hi):
-                xv_t[k, u] = xv[:, H * (u - lo) : H * (u - lo + 1)]
+                wide[u] = tile[:, H * (u - lo) : H * (u - lo + 1)]
+                run_t[u] = (tile, lo)
 
-        def widen_g(k):
-            xg_t[k] = sb.tile([P, g_units(k) * H], BF16, name="xg", bufs=2, align_bytes=64)
-            nc.scalar.copy(out=xg_t[k][:], in_=hb_t[k][:, H * v_units(k) :].bitcast(F8))
-
-        def scale_g(k):
-            n = g_units(k)
-            gs_t[k] = ring.tile([P, 2, n, P, 2], BF16, name="slot%d" % ((k + 1) % 2), align_bytes=64)
+        def scale_g(lo, hi, slot):
+            n = hi - lo
+            tile, first = run_t[lo]
+            gs = ring.tile([P, 2, n, P, 2], BF16, name=slot, align_bytes=64)
             nc.gpsimd.tensor_tensor(
-                out=gs_t[k][:],
-                in0=xg_t[k][:].rearrange("r (n p u e) -> r u n p e", p=P, u=2, e=2),
+                out=gs[:],
+                in0=tile[:, H * (lo - first) : H * (hi - first)].rearrange("r (n p u e) -> r u n p e", p=P, u=2, e=2),
                 in1=scale_row[:].unsqueeze(2).to_broadcast([P, 2, n, P, 2]),
                 op=MULT,
             )
+            words = gs[:].rearrange("r u n p e -> r u n (p e)").bitcast(F32)
+            for u in range(lo, hi):
+                done[u] = [words[:, h, u - lo, :] for h in range(2)]
 
-        def turned(k, lo, hi, tag):
-            whole = bank(tag)
-            words = 2 * P * (hi - lo)
-            bank_t[k, lo], room_t[k] = whole[:, :words].rearrange("p (u a r) -> p u a r", u=2, r=P), whole[:, words:]
-            return bank_t[k, lo]
-
-        def turn_v(k, lo, hi, tag="for_vector"):
-            dst = turned(k, lo, hi, tag)
+        def turn(lo, hi, tag):
+            dst = bank(tag)[:, : 2 * P * (hi - lo)].rearrange("p (u a r) -> p u a r", u=2, r=P)
+            bank_t[lo] = dst
             for a in range(hi - lo):
-                words = xv_t[k, lo + a].bitcast(F32)
-                for u in range(2):
-                    nc.tensor.transpose(dst[:, u, a, :], words[:, u::2], ident[:])
+                for h in range(2):
+                    src = done[lo + a][h] if lo + a in done else wide[lo + a].bitcast(F32)[:, h::2]
+                    nc.tensor.transpose(dst[:, h, a, :], src, ident[:])
 
-        def turn_g(k, lo, hi):
-            dst = turned(k, lo, hi, "for_scalar")
-            words = gs_t[k][:].rearrange("r u n p e -> r u n (p e)").bitcast(F32)
-            for a in range(hi - lo):
-                for u in range(2):
-                    nc.tensor.transpose(dst[:, u, a, :], words[:, u, lo - v_units(k) + a, :], ident[:])
-
-        def q_cols(k, lo, hi):
-            if k == 1 and lo < NS:
+        def q_cols(lo, hi):
+            k = lo // UNITS
+            if k == 1 and lo < UNITS + NS:
                 if "first" not in q_t:
-                    q_t["first"] = ring.tile([P, ROW], BF16, name="slot0", align_bytes=64)
-                return q_t["first"][:, H * lo : H * hi]
+                    q_t["first"] = ring.tile([P, ROW], BF16, name="slot2", align_bytes=64)
+                return q_t["first"][:, H * (lo - UNITS) : H * (hi - UNITS)]
             if k not in q_t:
-                q_t[k] = sb.tile([P, 2 * ROW], BF16, name="q", bufs=2, align_bytes=64)
-            return q_t[k][:, H * lo : H * hi]
+                q_t[k] = sb.tile([P, 2 * ROW], BF16, name="q", bufs=3, align_bytes=64)
+            return q_t[k][:, H * (lo - UNITS * k) : H * (hi - UNITS * k)]
 
-        def scale_v(k, lo, hi, less=0):
-            m = (hi - lo) * P - less
-            pairs = bank_t[k, lo].rearrange("p u a r -> p (u a r)").bitcast(BF16).rearrange("p (u m e) -> p m u e", u=2, e=2)
+        def scale_v(lo, hi):
+            m = (hi - lo) * P
+            pairs = bank_t[lo].rearrange("p u a r -> p (u a r)").bitcast(BF16).rearrange("p (u m e) -> p m u e", u=2, e=2)
             nc.vector.tensor_tensor(
-                out=q_cols(k, lo, hi).rearrange("p (m u e) -> p m u e", u=2, e=2)[:, :m],
-                in0=pairs[:, :m],
+                out=q_cols(lo, hi).rearrange("p (m u e) -> p m u e", u=2, e=2),
+                in0=pairs,
                 in1=scale_p[:].rearrange("p (u e) -> p u e", u=2).unsqueeze(1).to_broadcast([P, m, 2, 2]),
                 op=MULT,
             )
 
-        def scale_s(k, m):
-            pairs = bank_t[k, NS].rearrange("p u a r -> p (u a r)").bitcast(BF16).rearrange("p (u m e) -> p m u e", u=2, e=2)
-            dst = q_cols(k, NS, NS + 1).rearrange("p (m t) -> p m t", t=4)
-            for t in range(4):
-                nc.scalar.activation(out=dst[:, P - m :, t], in_=pairs[:, P - m :, t // 2, t % 2], func=COPY, scale=scale_p[:, t : t + 1])
+        def empty_g(lo, hi):
+            nc.scalar.copy(out=q_cols(lo, hi).bitcast(F32).rearrange("p (m u) -> p m u", u=2), in_=bank_t[lo].rearrange("p u a r -> p (a r) u"))
 
-        def bank_words(k, lo):
-            return bank_t[k, lo].rearrange("p u a r -> p (a r) u")
-
-        def empty_g(k, lo, hi):
-            nc.scalar.copy(out=q_cols(k, lo, hi).bitcast(F32).rearrange("p (m u) -> p m u", u=2), in_=bank_words(k, lo))
-
-        def copy_words(k, m, tag):
-            words = ring.tile([P, m, 2], F32, name=tag, align_bytes=64)
-            if m > P:
-                nc.scalar.copy(out=words[:, : m - P, :], in_=bank_words(k, 2)[:, 3 * P - m :, :])
-            nc.scalar.copy(out=words[:, max(m - P, 0) :, :], in_=bank_words(k, NS)[:, max(P - m, 0) :, :])
-            return words
-
-        def scale_turned(k, m, words):
-            nc.gpsimd.tensor_tensor(
-                out=q_cols(k, NS - 1, NS + 1)[:, 2 * H - 4 * m :].rearrange("p (m t) -> p m t", t=4),
-                in0=words[:].rearrange("p m u -> p (m u)").bitcast(BF16).rearrange("p (m t) -> p m t", t=4),
-                in1=scale_p[:].unsqueeze(1).to_broadcast([P, m, 4]),
-                op=MULT,
-            )
-
-        def quant(k, lo, hi):
+        def quant(lo, hi):
             codes = sb.tile([P, (hi - lo) * P], U32, name="codes", align_bytes=64)
             scales = sb.tile([P, (hi - lo) * P], U8, name="scales", align_bytes=64)
-            nc.vector.quantize_mx(out=codes[:].bitcast(F8X4), scales=scales[:], in_=q_cols(k, lo, hi))
+            nc.vector.quantize_mx(out=codes[:].bitcast(F8X4), scales=scales[:], in_=q_cols(lo, hi))
             for u in range(lo, hi):
                 cols = slice(P * (u - lo), P * (u - lo + 1))
-                c_t[k, u], s_t[k, u] = codes[:, cols], scales[:, cols]
+                c_t[u], s_t[u] = codes[:, cols], scales[:, cols]
 
         def down(i):
             jp_t[i] = bank("for_scalar")
@@ -204,8 +138,8 @@ def tile_mopn_layer_pb_t_w4_kernel(tc, hid_bytes, hid_scale, Wd, Wo_words, Wo_sc
                 cols = slice(P * n, P * (n + 1))
                 nc.tensor.matmul_mx(
                     out=jp_t[i][:, cols],
-                    lhsT=c_t[i // 2, NS * (i % 2) + n].bitcast(F8X4),
-                    lhsT_scale=s_t[i // 2, NS * (i % 2) + n],
+                    lhsT=c_t[NS * i + n].bitcast(F8X4),
+                    lhsT_scale=s_t[NS * i + n],
                     rhs=w_codes[:, cols].bitcast(F8X4),
                     rhs_scale=w_scales[:, cols],
                     start=True,
@@ -224,7 +158,7 @@ def tile_mopn_layer_pb_t_w4_kernel(tc, hid_bytes, hid_scale, Wd, Wo_words, Wo_sc
                     nc.tensor.transpose(jt_t[tiles][:, u, z, :], words[:, P * u : P * (u + 1)], ident[:])
 
         def empty_j(*tiles):
-            tag = "slot%d" % ((tiles[0] // 2 + 1) % 2) if tiles[0] < TILES - 4 else "last%d" % (tiles[0] % 4)
+            tag = "slot%d" % (tiles[0] // 2 % 3) if len(tiles) == 2 else "last%d" % (tiles[0] % 2)
             jg_t[tiles] = ring.tile([P, len(tiles) * P, 2], F32, name=tag, align_bytes=64)
             nc.scalar.copy(out=jg_t[tiles][:], in_=jt_t[tiles].rearrange("p u i r -> p (i r) u"))
 
@@ -235,27 +169,25 @@ def tile_mopn_layer_pb_t_w4_kernel(tc, hid_bytes, hid_scale, Wd, Wo_words, Wo_sc
             for z, i in enumerate(tiles):
                 jc_t[i], js_t[i] = codes[:, P * z : P * (z + 1)], scales[:, P * z : P * (z + 1)]
 
-        def mix(i, dst):
-            w = D - t_cols(i)
-            po_t[i] = dst[:, :w]
+        def mix(i):
+            po_t[i] = bank("for_vector")
             nc.tensor.matmul_mx(
                 out=po_t[i],
                 lhsT=jc_t[i].bitcast(F8X4),
                 lhsT_scale=js_t[i],
-                rhs=wo_words[:, : 2 * w].bitcast(F4X4),
-                rhs_scale=wo_scales[:, :w],
+                rhs=wo_words[:].bitcast(F4X4),
+                rhs_scale=wo_scales[:],
                 start=True,
                 stop=True,
             )
 
-        def mix_t(i, room=None):
-            lo = D - t_cols(i)
-            pt_t[i] = (bank("for_scalar") if room is None else room)[:, : t_cols(i)]
-            for c in range(0, t_cols(i), P):
+        def mix_t(i):
+            pt_t[i] = bank("for_scalar")
+            for lo in range(0, D, P):
                 nc.tensor.matmul_mx(
-                    out=pt_t[i][:, c : c + P],
-                    lhsT=wo_words[:, 2 * (lo + c) : 2 * (lo + c + P)].bitcast(F4X4),
-                    lhsT_scale=wo_scales[:, lo + c : lo + c + P],
+                    out=pt_t[i][:, lo : lo + P],
+                    lhsT=wo_words[:, 2 * lo : 2 * (lo + P)].bitcast(F4X4),
+                    lhsT_scale=wo_scales[:, lo : lo + P],
                     rhs=jc_t[i].bitcast(F8X4),
                     rhs_scale=js_t[i],
                     start=True,
@@ -263,33 +195,30 @@ def tile_mopn_layer_pb_t_w4_kernel(tc, hid_bytes, hid_scale, Wd, Wo_words, Wo_sc
                 )
 
         def empty_t(i):
-            rt_t[i] = sb.tile([P, t_cols(i)], F32, name="rt", bufs=2, align_bytes=64)
+            rt_t[i] = sb.tile([P, D], F32, name="rt", bufs=2, align_bytes=64)
             nc.scalar.copy(out=rt_t[i][:], in_=pt_t[i])
 
-        def sum_t(i):
-            w = t_cols(i)
-            lo = (i % 2 + 1) * D - w
-            pt_t[i] = bank("for_scalar")[:, :w]
-            nc.tensor.matmul(out=pt_t[i], lhsT=ident_bf[:], rhs=x_t[i // 2][:, lo : lo + w], start=True, stop=False)
-            for c in range(0, w, P):
-                nc.tensor.matmul(out=pt_t[i][:, c : c + P], lhsT=rt_t[i][:, c : c + P], rhs=ident[:], is_transpose=not PLAIN, start=False, stop=c + P == w)
+        def sum_t(i, tag="for_scalar"):
+            rt = rt_t[i]
+            pt_t[i] = bank(tag)
+            nc.tensor.matmul(out=pt_t[i], lhsT=ident_bf[:], rhs=x_t[i // 2][:, (i % 2) * D : (i % 2 + 1) * D], start=True, stop=False)
+            for lo in range(0, D, P):
+                nc.tensor.matmul(out=pt_t[i][:, lo : lo + P], lhsT=rt[:, lo : lo + P], rhs=ident[:], is_transpose=True, start=False, stop=lo + P == D)
 
-        def o_tile(k):
-            if k not in o_t:
-                o_t[k] = sb.tile([P, 2 * D], F32, name="o", bufs=4, align_bytes=64)
-            return o_t[k]
+        def o_cols(i):
+            if i // 2 not in o_t:
+                o_t[i // 2] = sb.tile([P, 2 * D], F32, name="o", bufs=5, align_bytes=64)
+            return o_t[i // 2][:, (i % 2) * D : (i % 2 + 1) * D]
 
         def empty_sum(i):
-            lo = (i % 2 + 1) * D - t_cols(i)
-            nc.scalar.copy(out=o_tile(i // 2)[:, lo : lo + t_cols(i)], in_=pt_t[i])
+            nc.scalar.copy(out=o_cols(i), in_=pt_t[i])
 
-        def add(i, lo=0, w=None):
-            w = D - t_cols(i) if w is None else w
+        def add(i, lo=0, w=D):
             cols = slice((i % 2) * D + lo, (i % 2) * D + lo + w)
-            nc.vector.tensor_tensor(out=o_tile(i // 2)[:, cols], in0=po_t[i][:, lo : lo + w], in1=x_t[i // 2][:, cols], op=ADD)
+            nc.vector.tensor_tensor(out=o_cols(i)[:, lo : lo + w], in0=po_t[i][:, lo : lo + w], in1=x_t[i // 2][:, cols], op=ADD)
 
         def store(k, lo=0, w=2 * D):
-            nc.sync.dma_start(out=oview[k][:, lo : lo + w], in_=o_tile(k)[:, lo : lo + w])
+            nc.sync.dma_start(out=oview[k][:, lo : lo + w], in_=o_t[k][:, lo : lo + w])
 
         def add_store(i, parts=1):
             w = D // parts
@@ -297,175 +226,192 @@ def tile_mopn_layer_pb_t_w4_kernel(tc, hid_bytes, hid_scale, Wd, Wo_words, Wo_sc
                 add(i, lo, w)
                 store(i // 2, (i % 2) * D + lo, w)
 
+        def items(p):
+            u = UNITS * p
+            if p == 1:
+                return [u + 6, u + 8, u + 10]
+            if p % 2 == 0:
+                return [u + 4, u + 12, u + 14]
+            return [u + 8, u + 10]
+
+        def early(p):
+            return 1 if p % 2 == 0 else 2
+
         nc.sync.dma_start(out=scale_p[:], in_=srow.rearrange("(p t) -> p t", t=4))
-        load_hid(0, 0, 2)
-        load_hid(0, 2, 4)
-        load_hid(1, v_units(1), UNITS)
-        load_hid(0, 4, UNITS)
-        load_hid(1, 0, v_units(1))
+        load_hid(0, 2)
+        load_hid(2, 4)
+        load_hid(8, 12)
+        load_hid(4, 8)
+        load_hid(12, 16)
         nc.sync.dma_start(out=w_raw[:].rearrange("p n j d -> p n (j d)"), in_=Wd.rearrange("n (p j) d -> p n (j d)", j=4))
-        load_hid(2)
+        load_pair(2)
         make_identity(nc, ident[:])
         make_identity(nc, ident_bf[:])
         nc.vector.memset(wo_scales[:].bitcast(I32), 0)
+        load_pair(3)
         nc.sync.dma_start(out=wo_words[:], in_=Wo_words[0])
         wos = Wo_scales[0].bitcast(I32)
         for q in range(4):
             nc.sync.dma_start(out=wo_scales[32 * q : 32 * q + 4, :].bitcast(I32), in_=wos[4 * q : 4 * q + 4, :])
-        load_hid(3)
+        load_pair(4)
         load_x(0)
 
         spread = bank("for_scalar").rearrange("r (u e p) -> r u e p", u=2, e=2)
         for t in range(4):
             nc.tensor.transpose(spread[:, t // 2, t % 2, :], scale_p[:, t : t + 1].to_broadcast([P, P]), ident[:])
-        widen_v(0, 0, 1, nc.vector.tensor_copy)
-        widen_v(0, 1, 2, nc.vector.tensor_copy)
+        widen(0, 1, "head", 6, nc.vector.tensor_copy)
+        widen(1, 2, "head", 6, nc.vector.tensor_copy)
         nc.vector.tensor_copy(out=scale_row[:], in_=spread.rearrange("r u e p -> r u p e"))
-        widen_v(0, 2, 4)
-        widen_g(1)
-        scale_g(1)
-        widen_v(0, 4, 6)
-        widen_v(0, 6, 8)
-        for lo, hi in [(0, 1), (1, 2)] + by_bank(2, UNITS):
-            turn_v(0, lo, hi)
-            scale_v(0, lo, hi)
-        widen_v(1, 0, 2)
+        widen(2, 4, "head", 6)
+        widen(8, 12, "for_g", 2)
+        scale_g(8, 12, "slot0")
+        widen(4, 6, "head", 6)
+        widen(6, 8, "head", 6)
+        widen(12, 16, "for_v", 3)
         w_grp = ring.tile([P, NS, DS, 4], BF16, name="slot1", align_bytes=64)
         nc.scalar.copy(
             out=w_grp[:].rearrange("p n (c i) j -> p n c j i", i=4),
             in_=w_raw[:].rearrange("p n j (c i) -> p n c j i", i=4),
         )
-        widen_g(2)
-        widen_v(1, 2, v_units(1))
-        turn_v(1, 0, 2)
+        for lo, hi in [(0, 1), (1, 2), (2, 4), (4, 6), (6, 8), (12, 14)]:
+            turn(lo, hi, "for_vector")
+            scale_v(lo, hi)
+        widen(16, 18, "head", 6)
+        widen(22, 25, "for_g", 2)
+        widen(18, 22, "for_v", 3)
+        for lo in (14, 16):
+            turn(lo, lo + 2, "for_vector")
+        for lo in (8, 10):
+            turn(lo, lo + 2, "for_scalar")
+        turn(18, 20, "for_vector")
+        for lo in (8, 10):
+            empty_g(lo, lo + 2)
+        widen(25, 28, "for_g", 2)
 
-        n = TILES
-        for p in range(1, PAIRS):
+        for p in range(1, PAIRS - 1):
+            u = UNITS * p
             a, b = 2 * p - 2, 2 * p - 1
             c, d = 2 * (p - BACK), 2 * (p - BACK) + 1
-            last = p == PAIRS - 1
-            adds = c >= 0 and not last
-            later = by_bank(NS, v_units(p))
-            if p + 3 < PAIRS:
-                load_hid(p + 3)
+            last = p == PAIRS - 2
+            through = c >= 0 and p % 2 == 0
+            late = items(p)[early(p) :] if p >= 2 else []
+            if p + 4 < PAIRS:
+                load_pair(p + 4)
             load_x(p)
-            if not last and p > 1:
-                widen_v(p + 1, 0, v_units(p + 1))
-            if last:
-                quant_j(c, d)
-                words = copy_words(p, G_COLS + P, "slot1")
-            both = adds and t_cols(d) <= 2 * P and PACK
-            for lo, hi in by_bank(v_units(p), UNITS)[: 1 if both else 2]:
-                turn_g(p, lo, hi)
-                empty_g(p, lo, hi)
-            if p == 1:
-                turn_v(1, 2, 4)
-                widen_v(p + 1, 0, v_units(p + 1))
-                nc.vector.quantize_mx(out=w_codes[:].bitcast(F8X4), scales=w_scales[:], in_=w_grp[:].rearrange("p n d j -> p (n d j)"))
+            for lo in [u + 6] if p % 2 == 0 else [u, u + 2] if p > 1 else []:
+                turn(lo, lo + 2, "for_scalar")
+                empty_g(lo, lo + 2)
+            for lo in late[:1]:
+                turn(lo, lo + 2, "for_vector")
             if p >= 2:
                 turn_j(a - 2, b - 2)
-            if both:
-                turn_g(p, UNITS - 1, UNITS)
-                spare = room_t[p]
-            if not last:
-                for lo, hi in later:
-                    turn_v(p, lo, hi)
-            if adds:
+            if p == 1:
+                nc.vector.quantize_mx(out=w_codes[:].bitcast(F8X4), scales=w_scales[:], in_=w_grp[:].rearrange("p n d j -> p (n d j)"))
+            if c >= 0:
                 quant_j(c, d)
             if p == 2:
-                quant(p - 1, 0, NS)
-                quant(p - 1, NS, UNITS)
+                quant(u - UNITS, u - NS)
+                quant(u - NS, u)
             else:
-                quant(p - 1, 0, UNITS)
-            if not last:
-                scale_g(p + 1)
-            else:
-                scale_turned(p, G_COLS + P, words)
+                quant(u - UNITS, u)
+            first = u + 14 if p % 2 else u + 9
+            scale_g(first, first + 3, "slot%d" % (p % 3))
             if p >= 2:
                 empty_j(a - 2, b - 2)
-            if adds:
-                mix_t(d, spare if both else None)
-                if both:
-                    empty_g(p, UNITS - 1, UNITS)
+            for lo in late[1:]:
+                turn(lo, lo + 2, "for_vector")
+            if last:
+                down(a)
+                down(b)
+                round_j(a)
+                round_j(b)
+            if c > 0 and p % 2 == 1:
+                add(c - 2, HALF, D - HALF)
+                store(p - BACK - 1)
+            for lo in items(p):
+                scale_v(lo, lo + 2)
+            if through:
+                mix_t(d)
                 empty_t(d)
-                if SHARE:
-                    mix(d, room_t[p])
+            if p % 2 == 1:
+                widen(u + 20, u + 24, "for_v", 3)
+            elif not last:
+                widen(u + 22, u + 28, "for_g", 2)
             if c >= 0:
-                mix(c, bank("for_vector"))
-            few = G_MID if MID_FROM <= p < PAIRS - 1 else 0
-            if few:
-                scale_turned(p, few, copy_words(p, few, "few%d" % (p % 2)))
-            if Z_COLS and MID_FROM <= p < PAIRS - 1:
-                few = Z_COLS
-                scale_s(p, few)
-            if p + 2 < PAIRS:
-                widen_g(p + 2)
-            scale_v(p, 0, 2)
-            if adds and p < SPLIT:
-                turn_v(p + 1, 0, 2)
+                mix(c)
+            if last:
+                break
+            if c >= 0 and not through:
+                mix(d)
             down(a)
             down(b)
-            if last:
-                mix(d, bank("for_scalar"))
-            if adds and not SHARE and t_cols(d) < D:
-                mix(d, bank("for_vector"))
             round_j(a)
             round_j(b)
-            if adds:
+            if p % 2 == 1 and p + 3 < PAIRS:
+                widen(u + 24, u + 30, "for_v", 3)
+            if through:
                 sum_t(d)
                 empty_sum(d)
-            if last:
-                res = sb.tile([P, D], F32, name="res", bufs=1, align_bytes=64)
-                nc.scalar.copy(out=res[:], in_=po_t[d])
-            if not last and SHARE and p > 1 and not (adds and p < SPLIT):
-                turn_v(p + 1, 0, 2)
-            scale_v(p, 2, 4, G_COLS if last else 0)
-            if not last:
-                if not SHARE or p == 1:
-                    turn_v(p + 1, 0, 2)
-                if SHARE and p > 1:
-                    turn_v(p + 1, 2, 4)
-                for lo, hi in later:
-                    scale_v(p, lo, hi, few)
-                if not SHARE or p == 1:
-                    turn_v(p + 1, 2, 4)
-            if p == PAIRS - 2:
-                turn_v(p + 1, NS, v_units(p + 1), "for_scalar")
-            if adds:
-                add(c)
-                if t_cols(d) < D:
-                    add(d)
+            for lo in items(p + 1)[: early(p + 1)]:
+                turn(lo, lo + 2, "for_vector")
+            if c >= 0:
+                add(c, 0, HALF if through else D)
+            if c >= 0 and not through:
+                add(d)
                 store(p - BACK)
 
-        turn_j(n - 4, n - 3)
-        empty_j(n - 4, n - 3)
-        quant(PAIRS - 1, NS, UNITS)
+        n = TILES
+        u = UNITS * (PAIRS - 1)
+        load_x(PAIRS - 1)
+        turn_j(n - 6, n - 5)
+        empty_j(n - 6, n - 5)
+        sum_t(n - 9)
+        empty_sum(n - 9)
+        add(n - 10)
+        store(PAIRS - 5)
+        quant(u - UNITS, u - NS)
+        quant_j(n - 8, n - 7)
+        quant(u - NS, u)
+        for lo in (u, u + 2):
+            turn(lo, lo + 2, "for_scalar")
+            empty_g(lo, lo + 2)
+        quant(u + NS, u + UNITS)
         quant_j(n - 6, n - 5)
-        quant(PAIRS - 1, 0, NS)
+        quant(u, u + NS)
+        down(n - 4)
+        mix(n - 8)
+        down(n - 3)
+        mix(n - 7)
+        round_j(n - 4)
+        pt_t[n - 8] = po_t[n - 8]
+        empty_t(n - 8)
+        round_j(n - 3)
         down(n - 1)
-        mix(n - 6, bank("for_vector"))
+        mix(n - 6)
+        sums = ring.tile([P, D], F32, name="slot%d" % ((PAIRS - 3) % 3), align_bytes=64)
+        nc.gpsimd.tensor_tensor(out=sums[:], in0=rt_t[n - 8][:], in1=x_t[PAIRS - 4][:, :D], op=ADD)
+        turn_j(n - 4, n - 3)
         down(n - 2)
+        mix(n - 5)
         round_j(n - 1)
+        empty_j(n - 4, n - 3)
         round_j(n - 2)
-        add_store(n - 8)
-        sums = ring.tile([P, D], F32, name="slot0", align_bytes=64)
-        nc.gpsimd.tensor_tensor(out=sums[:], in0=res[:], in1=x_t[PAIRS - 4][:, D:], op=ADD)
-        mix(n - 5, bank("for_vector"))
+        add_store(n - 7)
         add_store(n - 6)
-        nc.sync.dma_start(out=oview[PAIRS - 4][:, D:], in_=sums[:])
+        nc.sync.dma_start(out=oview[PAIRS - 4][:, :D], in_=sums[:])
         quant_j(n - 4, n - 3)
         turn_j(n - 1)
         empty_j(n - 1)
+        mix(n - 4)
         turn_j(n - 2)
         empty_j(n - 2)
-        mix(n - 4, bank("for_vector"))
-        mix(n - 3, bank("for_vector"))
+        mix(n - 3)
         add_store(n - 5)
         quant_j(n - 1)
-        mix(n - 1, bank("for_vector"))
-        quant_j(n - 2)
         add_store(n - 4)
-        mix(n - 2, bank("for_vector"))
+        mix(n - 1)
+        quant_j(n - 2)
         add_store(n - 3)
+        mix(n - 2)
         add_store(n - 1)
         add_store(n - 2, 2)

@@ -24,8 +24,10 @@ ROW = NS * H
 TILES = TOKENS // P
 PAIRS = TILES // 2
 UNITS = 2 * NS
-BACK = 3
-HALF = 256
+QUAD = 2 * UNITS
+QUADS = PAIRS // 2
+G_UNITS = 6
+G_LAST = 3
 FLOPS = 2 * TOKENS * NS * H * DS + 2 * TOKENS * D * D
 
 
@@ -43,7 +45,6 @@ def tile_mopn_layer_pb_t_w4_kernel(tc, hid_bytes, hid_scale, Wd, Wo_words, Wo_sc
         ps = ctx.enter_context(tc.psum_pool(name="ps", bufs=4))
         ctx.enter_context(tc.manual_schedule())
 
-        hb = keep.tile([P, PAIRS * UNITS * H], U8, align_bytes=64)
         scale_p = keep.tile([P, 4], F32, align_bytes=64)
         scale_row = keep.tile([P, 2, P, 2], F32, align_bytes=64)
         ident = keep.tile([P, P], F32, align_bytes=64)
@@ -54,7 +55,7 @@ def tile_mopn_layer_pb_t_w4_kernel(tc, hid_bytes, hid_scale, Wd, Wo_words, Wo_sc
         wo_words = keep.tile([P, 2 * D], U8, align_bytes=64)
         wo_scales = keep.tile([P, D], U8, align_bytes=64)
 
-        x_t, wide, run_t, done, bank_t, q_t, c_t, s_t = ({} for z in range(8))
+        hb_t, x_t, wide, run_t, done, bank_t, q_t, c_t, s_t = ({} for z in range(9))
         jp_t, jb_t, jt_t, jg_t, jc_t, js_t, po_t, pt_t, rt_t, o_t = ({} for z in range(10))
 
         def bank(tag):
@@ -62,19 +63,21 @@ def tile_mopn_layer_pb_t_w4_kernel(tc, hid_bytes, hid_scale, Wd, Wo_words, Wo_sc
             return tile[:]
 
         def load_hid(lo, hi):
-            k = lo // UNITS
-            nc.sync.dma_start(out=hb[:, H * lo : H * hi], in_=hid[k][:, H * (lo - UNITS * k) : H * (hi - UNITS * k)])
+            m, k = lo // QUAD, lo // UNITS
+            if m not in hb_t:
+                hb_t[m] = sb.tile([P, QUAD * H], U8, name="hb", bufs=4, align_bytes=64)
+            nc.sync.dma_start(out=hb_t[m][:, H * (lo - QUAD * m) : H * (hi - QUAD * m)], in_=hid[k][:, H * (lo - UNITS * k) : H * (hi - UNITS * k)])
 
         def load_pair(k):
             load_hid(UNITS * k, UNITS * (k + 1))
 
         def load_x(k):
-            x_t[k] = sb.tile([P, 2 * D], BF16, name="x", bufs=5, align_bytes=64)
+            x_t[k] = sb.tile([P, 2 * D], BF16, name="x", bufs=6, align_bytes=64)
             nc.sync.dma_start(out=x_t[k][:], in_=xin[k])
 
         def widen(lo, hi, tag, bufs, eng=nc.scalar.copy):
             tile = sb.tile([P, (hi - lo) * H], BF16, name=tag, bufs=bufs, align_bytes=64)
-            eng(out=tile[:], in_=hb[:, H * lo : H * hi].bitcast(F8))
+            eng(out=tile[:], in_=hb_t[lo // QUAD][:, H * (lo % QUAD) : H * (lo % QUAD + hi - lo)].bitcast(F8))
             for u in range(lo, hi):
                 wide[u] = tile[:, H * (u - lo) : H * (u - lo + 1)]
                 run_t[u] = (tile, lo)
@@ -103,12 +106,8 @@ def tile_mopn_layer_pb_t_w4_kernel(tc, hid_bytes, hid_scale, Wd, Wo_words, Wo_sc
 
         def q_cols(lo, hi):
             k = lo // UNITS
-            if k == 1 and lo < UNITS + NS:
-                if "first" not in q_t:
-                    q_t["first"] = ring.tile([P, ROW], BF16, name="slot2", align_bytes=64)
-                return q_t["first"][:, H * (lo - UNITS) : H * (hi - UNITS)]
             if k not in q_t:
-                q_t[k] = sb.tile([P, 2 * ROW], BF16, name="q", bufs=3, align_bytes=64)
+                q_t[k] = sb.tile([P, 2 * ROW], BF16, name="q", bufs=5, align_bytes=64)
             return q_t[k][:, H * (lo - UNITS * k) : H * (hi - UNITS * k)]
 
         def scale_v(lo, hi):
@@ -157,14 +156,15 @@ def tile_mopn_layer_pb_t_w4_kernel(tc, hid_bytes, hid_scale, Wd, Wo_words, Wo_sc
                 for u in range(2):
                     nc.tensor.transpose(jt_t[tiles][:, u, z, :], words[:, P * u : P * (u + 1)], ident[:])
 
-        def empty_j(*tiles):
-            tag = "slot%d" % (tiles[0] // 2 % 3) if len(tiles) == 2 else "last%d" % (tiles[0] % 2)
-            jg_t[tiles] = ring.tile([P, len(tiles) * P, 2], F32, name=tag, align_bytes=64)
-            nc.scalar.copy(out=jg_t[tiles][:], in_=jt_t[tiles].rearrange("p u i r -> p (i r) u"))
+        def empty_j(tiles, group, tag):
+            if group not in jg_t:
+                jg_t[group] = ring.tile([P, len(group) * P, 2], F32, name=tag, align_bytes=64)
+            lo = P * group.index(tiles[0])
+            nc.scalar.copy(out=jg_t[group][:, lo : lo + P * len(tiles), :], in_=jt_t[tiles].rearrange("p u i r -> p (i r) u"))
 
         def quant_j(*tiles):
-            codes = sb.tile([P, len(tiles) * P], U32, name="jcodes", bufs=5, align_bytes=64)
-            scales = sb.tile([P, len(tiles) * P], U8, name="jscales", bufs=5, align_bytes=64)
+            codes = sb.tile([P, len(tiles) * P], U32, name="jcodes", bufs=4, align_bytes=64)
+            scales = sb.tile([P, len(tiles) * P], U8, name="jscales", bufs=4, align_bytes=64)
             nc.vector.quantize_mx(out=codes[:].bitcast(F8X4), scales=scales[:], in_=jg_t[tiles][:].rearrange("p r u -> p (r u)").bitcast(BF16))
             for z, i in enumerate(tiles):
                 jc_t[i], js_t[i] = codes[:, P * z : P * (z + 1)], scales[:, P * z : P * (z + 1)]
@@ -217,6 +217,19 @@ def tile_mopn_layer_pb_t_w4_kernel(tc, hid_bytes, hid_scale, Wd, Wo_words, Wo_sc
             cols = slice((i % 2) * D + lo, (i % 2) * D + lo + w)
             nc.vector.tensor_tensor(out=o_cols(i)[:, lo : lo + w], in0=po_t[i][:, lo : lo + w], in1=x_t[i // 2][:, cols], op=ADD)
 
+        def copy_aside(i):
+            res = sb.tile([P, D], F32, name="rt", bufs=2, align_bytes=64)
+            nc.scalar.copy(out=res[:], in_=po_t[i])
+            return res
+
+        def add_aside(i, res, tag):
+            sums = ring.tile([P, D], F32, name=tag, align_bytes=64)
+            nc.gpsimd.tensor_tensor(out=sums[:], in0=res[:], in1=x_t[i // 2][:, (i % 2) * D : (i % 2 + 1) * D], op=ADD)
+            return sums
+
+        def store_aside(i, sums):
+            nc.sync.dma_start(out=oview[i // 2][:, (i % 2) * D : (i % 2 + 1) * D], in_=sums[:])
+
         def store(k, lo=0, w=2 * D):
             nc.sync.dma_start(out=oview[k][:, lo : lo + w], in_=o_t[k][:, lo : lo + w])
 
@@ -226,192 +239,217 @@ def tile_mopn_layer_pb_t_w4_kernel(tc, hid_bytes, hid_scale, Wd, Wo_words, Wo_sc
                 add(i, lo, w)
                 store(i // 2, (i % 2) * D + lo, w)
 
-        def items(p):
-            u = UNITS * p
-            if p == 1:
-                return [u + 6, u + 8, u + 10]
-            if p % 2 == 0:
-                return [u + 4, u + 12, u + 14]
-            return [u + 8, u + 10]
+        def turn_v(lo, hi=None):
+            turn(lo, hi or lo + 2, "for_vector")
 
-        def early(p):
-            return 1 if p % 2 == 0 else 2
+        def turn_g(lo, hi=None):
+            turn(lo, hi or lo + 2, "for_scalar")
+            empty_g(lo, hi or lo + 2)
+
+        def joined(i, group, tag):
+            turn_j(i, i + 1)
+            empty_j((i, i + 1), group, tag)
 
         nc.sync.dma_start(out=scale_p[:], in_=srow.rearrange("(p t) -> p t", t=4))
         load_hid(0, 2)
         load_hid(2, 4)
-        load_hid(8, 12)
+        load_hid(QUAD, QUAD + 3)
         load_hid(4, 8)
-        load_hid(12, 16)
+        load_hid(QUAD + 3, QUAD + UNITS)
+        load_pair(1)
         nc.sync.dma_start(out=w_raw[:].rearrange("p n j d -> p n (j d)"), in_=Wd.rearrange("n (p j) d -> p n (j d)", j=4))
-        load_pair(2)
         make_identity(nc, ident[:])
-        make_identity(nc, ident_bf[:])
+        nc.scalar.copy(out=ident_bf[:], in_=ident[:])
         nc.vector.memset(wo_scales[:].bitcast(I32), 0)
         load_pair(3)
+        load_pair(4)
         nc.sync.dma_start(out=wo_words[:], in_=Wo_words[0])
         wos = Wo_scales[0].bitcast(I32)
         for q in range(4):
             nc.sync.dma_start(out=wo_scales[32 * q : 32 * q + 4, :].bitcast(I32), in_=wos[4 * q : 4 * q + 4, :])
-        load_pair(4)
-        load_x(0)
+        load_pair(5)
 
         spread = bank("for_scalar").rearrange("r (u e p) -> r u e p", u=2, e=2)
         for t in range(4):
             nc.tensor.transpose(spread[:, t // 2, t % 2, :], scale_p[:, t : t + 1].to_broadcast([P, P]), ident[:])
-        widen(0, 1, "head", 6, nc.vector.tensor_copy)
-        widen(1, 2, "head", 6, nc.vector.tensor_copy)
+        widen(0, 1, "head", 4, nc.vector.tensor_copy)
+        widen(1, 2, "head", 4, nc.vector.tensor_copy)
         nc.vector.tensor_copy(out=scale_row[:], in_=spread.rearrange("r u e p -> r u p e"))
-        widen(2, 4, "head", 6)
-        widen(8, 12, "for_g", 2)
-        scale_g(8, 12, "slot0")
-        widen(4, 6, "head", 6)
-        widen(6, 8, "head", 6)
-        widen(12, 16, "for_v", 3)
+        widen(2, 4, "head", 4)
+        widen(QUAD, QUAD + 3, "for_g", 3)
+        scale_g(QUAD, QUAD + 3, "slot0")
+        widen(4, 6, "head", 4)
+        for lo, hi in [(0, 1), (1, 2), (2, 4)]:
+            turn_v(lo, hi)
+            scale_v(lo, hi)
+        widen(6, 8, "head", 4)
+        widen(QUAD + 3, QUAD + G_UNITS, "for_g", 3)
+        scale_g(QUAD + 3, QUAD + G_UNITS, "late0")
+        widen(8, 10, "head", 4)
+        widen(10, QUAD, "for_v", 2)
         w_grp = ring.tile([P, NS, DS, 4], BF16, name="slot1", align_bytes=64)
         nc.scalar.copy(
             out=w_grp[:].rearrange("p n (c i) j -> p n c j i", i=4),
             in_=w_raw[:].rearrange("p n j (c i) -> p n c j i", i=4),
         )
-        for lo, hi in [(0, 1), (1, 2), (2, 4), (4, 6), (6, 8), (12, 14)]:
-            turn(lo, hi, "for_vector")
-            scale_v(lo, hi)
-        widen(16, 18, "head", 6)
-        widen(22, 25, "for_g", 2)
-        widen(18, 22, "for_v", 3)
-        for lo in (14, 16):
-            turn(lo, lo + 2, "for_vector")
-        for lo in (8, 10):
-            turn(lo, lo + 2, "for_scalar")
-        turn(18, 20, "for_vector")
-        for lo in (8, 10):
-            empty_g(lo, lo + 2)
-        widen(25, 28, "for_g", 2)
+        for lo in range(4, QUAD, 2):
+            turn_v(lo)
+            scale_v(lo, lo + 2)
+        widen(QUAD + G_UNITS, QUAD + 10, "head", 4)
+        widen(2 * QUAD, 2 * QUAD + G_UNITS, "for_g", 3)
+        widen(QUAD + 10, 2 * QUAD, "for_v", 2)
+        turn_v(QUAD + 6)
 
-        for p in range(1, PAIRS - 1):
-            u = UNITS * p
-            a, b = 2 * p - 2, 2 * p - 1
-            c, d = 2 * (p - BACK), 2 * (p - BACK) + 1
-            last = p == PAIRS - 2
-            through = c >= 0 and p % 2 == 0
-            late = items(p)[early(p) :] if p >= 2 else []
-            if p + 4 < PAIRS:
-                load_pair(p + 4)
-            load_x(p)
-            for lo in [u + 6] if p % 2 == 0 else [u, u + 2] if p > 1 else []:
-                turn(lo, lo + 2, "for_scalar")
-                empty_g(lo, lo + 2)
-            for lo in late[:1]:
-                turn(lo, lo + 2, "for_vector")
-            if p >= 2:
-                turn_j(a - 2, b - 2)
-            if p == 1:
+        for m in range(1, QUADS - 1):
+            u = QUAD * m
+            a = 4 * (m - 1)
+            c = 4 * (m - 2)
+            old, new = tuple(range(c, c + 4)), tuple(range(a, a + 4))
+            slot = "slot%d" % ((m + 1) % 2)
+            todo = [u + 6, u + 8, u + 10, u + 12, u + 14, u + QUAD + 6] if m == 1 else [u + 8, u + 10, u + 12, u + 14, u + QUAD + 6]
+            if m + 2 < QUADS:
+                load_pair(2 * m + 4)
+                load_pair(2 * m + 5)
+            load_x(2 * m - 2)
+            load_x(2 * m - 1)
+            quant(u - QUAD, u - UNITS)
+            if m == 1:
                 nc.vector.quantize_mx(out=w_codes[:].bitcast(F8X4), scales=w_scales[:], in_=w_grp[:].rearrange("p n d j -> p (n d j)"))
-            if c >= 0:
-                quant_j(c, d)
-            if p == 2:
-                quant(u - UNITS, u - NS)
-                quant(u - NS, u)
             else:
-                quant(u - UNITS, u)
-            first = u + 14 if p % 2 else u + 9
-            scale_g(first, first + 3, "slot%d" % (p % 3))
-            if p >= 2:
-                empty_j(a - 2, b - 2)
-            for lo in late[1:]:
-                turn(lo, lo + 2, "for_vector")
-            if last:
-                down(a)
-                down(b)
-                round_j(a)
-                round_j(b)
-            if c > 0 and p % 2 == 1:
-                add(c - 2, HALF, D - HALF)
-                store(p - BACK - 1)
-            for lo in items(p):
-                scale_v(lo, lo + 2)
-            if through:
-                mix_t(d)
-                empty_t(d)
-            if p % 2 == 1:
-                widen(u + 20, u + 24, "for_v", 3)
-            elif not last:
-                widen(u + 22, u + 28, "for_g", 2)
-            if c >= 0:
-                mix(c)
-            if last:
-                break
-            if c >= 0 and not through:
-                mix(d)
+                quant_j(*old)
+            quant(u - UNITS, u)
+            scale_g(u + QUAD, u + QUAD + G_UNITS, "slot%d" % (m % 2))
+            for lo in (u, u + 2, u + 4):
+                turn_g(lo)
+            turn_v(todo[1])
             down(a)
-            down(b)
+            down(a + 1)
             round_j(a)
-            round_j(b)
-            if p % 2 == 1 and p + 3 < PAIRS:
-                widen(u + 24, u + 30, "for_v", 3)
-            if through:
-                sum_t(d)
-                empty_sum(d)
-            for lo in items(p + 1)[: early(p + 1)]:
-                turn(lo, lo + 2, "for_vector")
-            if c >= 0:
-                add(c, 0, HALF if through else D)
-            if c >= 0 and not through:
-                add(d)
-                store(p - BACK)
+            round_j(a + 1)
+            if m > 1:
+                mix_t(c + 3)
+                empty_t(c + 3)
+            down(a + 2)
+            down(a + 3)
+            round_j(a + 2)
+            round_j(a + 3)
+            if m > 1:
+                mix(c)
+            cut = u + QUAD + (10 if m + 2 < QUADS else 8)
+            widen(u + QUAD + G_UNITS, cut, "head", 4)
+            turn_v(todo[2])
+            scale_v(todo[0], todo[0] + 2)
+            turn_v(todo[3])
+            scale_v(todo[1], todo[1] + 2)
+            joined(a, new, slot)
+            widen(cut if m + 2 < QUADS else cut + G_LAST, u + 2 * QUAD, "for_v", 2)
+            if m > 1:
+                mix(c + 1)
+                add(c)
+            else:
+                turn_v(todo[4])
+            scale_v(todo[2], todo[2] + 2)
+            turn_v(todo[-1])
+            joined(a + 2, new, slot)
+            scale_v(todo[3], todo[3] + 2)
+            if m > 1:
+                add(c + 1)
+                store(c // 2)
+            else:
+                scale_v(todo[4], todo[4] + 2)
+            if m > 1:
+                mix(c + 2)
+                sum_t(c + 3)
+            if m + 1 < QUADS - 1:
+                turn_v(u + QUAD + 8)
+            else:
+                turn_v(u + QUAD + 11, u + QUAD + 12)
+            if m + 2 < QUADS:
+                widen(u + 2 * QUAD, u + 2 * QUAD + G_UNITS, "for_g", 3)
+            else:
+                widen(cut, cut + G_LAST, "for_g", 3)
+            scale_v(todo[-1], todo[-1] + 2)
+            if m > 1:
+                empty_sum(c + 3)
+                add(c + 2)
+                store(c // 2 + 1)
 
         n = TILES
-        u = UNITS * (PAIRS - 1)
-        load_x(PAIRS - 1)
-        turn_j(n - 6, n - 5)
-        empty_j(n - 6, n - 5)
-        sum_t(n - 9)
-        empty_sum(n - 9)
-        add(n - 10)
-        store(PAIRS - 5)
-        quant(u - UNITS, u - NS)
-        quant_j(n - 8, n - 7)
-        quant(u - NS, u)
-        for lo in (u, u + 2):
-            turn(lo, lo + 2, "for_scalar")
-            empty_g(lo, lo + 2)
-        quant(u + NS, u + UNITS)
-        quant_j(n - 6, n - 5)
+        u = QUAD * (QUADS - 1)
+        for k in range(PAIRS - 4, PAIRS):
+            load_x(k)
+        quant(u - QUAD, u - UNITS)
+        quant_j(*range(n - 12, n - 8))
+        quant(u - UNITS, u)
+        scale_g(u + 8, u + 11, "slot1")
+        turn_v(u + 12)
+        for lo in (u, u + 2, u + 4):
+            turn_g(lo)
+        turn_v(u + 14)
+        down(n - 8)
+        down(n - 7)
+        mix(n - 12)
+        round_j(n - 8)
+        round_j(n - 7)
+        down(n - 6)
+        down(n - 5)
+        scale_v(u + 11, u + 12)
+        mix(n - 11)
+        round_j(n - 6)
+        round_j(n - 5)
+        joined(n - 8, (n - 8, n - 7), "late0")
+        joined(n - 6, (n - 6, n - 5), "late1")
+        scale_v(u + 12, u + 14)
+        scale_v(u + 14, u + 16)
+        mix(n - 10)
+        mix(n - 9)
+        first = copy_aside(n - 10)
+        add(n - 12)
+        add(n - 11)
+        store(PAIRS - 6)
         quant(u, u + NS)
+        quant_j(n - 8, n - 7)
+        quant(u + NS, u + UNITS)
+        turn_g(u + 8)
+        turn_g(u + 10, u + 11)
+        quant(u + 12, u + 16)
+        quant_j(n - 6, n - 5)
+        quant(u + 8, u + 12)
+        first = add_aside(n - 10, first, "late1")
         down(n - 4)
         mix(n - 8)
         down(n - 3)
-        mix(n - 7)
         round_j(n - 4)
-        pt_t[n - 8] = po_t[n - 8]
-        empty_t(n - 8)
+        second = copy_aside(n - 9)
         round_j(n - 3)
+        mix(n - 7)
         down(n - 1)
-        mix(n - 6)
-        sums = ring.tile([P, D], F32, name="slot%d" % ((PAIRS - 3) % 3), align_bytes=64)
-        nc.gpsimd.tensor_tensor(out=sums[:], in0=rt_t[n - 8][:], in1=x_t[PAIRS - 4][:, :D], op=ADD)
         turn_j(n - 4, n - 3)
         down(n - 2)
+        mix(n - 6)
         mix(n - 5)
         round_j(n - 1)
-        empty_j(n - 4, n - 3)
+        empty_j((n - 4, n - 3), (n - 4, n - 3), "late0")
         round_j(n - 2)
+        add_store(n - 8)
         add_store(n - 7)
-        add_store(n - 6)
-        nc.sync.dma_start(out=oview[PAIRS - 4][:, :D], in_=sums[:])
+        store_aside(n - 10, first)
         quant_j(n - 4, n - 3)
         turn_j(n - 1)
-        empty_j(n - 1)
+        empty_j((n - 1,), (n - 1,), "last1")
         mix(n - 4)
         turn_j(n - 2)
-        empty_j(n - 2)
+        empty_j((n - 2,), (n - 2,), "last0")
         mix(n - 3)
-        add_store(n - 5)
+        add_store(n - 6)
         quant_j(n - 1)
-        add_store(n - 4)
-        mix(n - 1)
+        add_store(n - 5)
         quant_j(n - 2)
-        add_store(n - 3)
+        second = add_aside(n - 9, second, "last0")
+        mix(n - 1)
+        add_store(n - 4)
         mix(n - 2)
+        add_store(n - 3)
+        store_aside(n - 9, second)
         add_store(n - 1)
         add_store(n - 2, 2)

@@ -72,7 +72,7 @@ def tile_mopn_layer_pb_t_w4_kernel(tc, hid_bytes, hid_scale, Wd, Wo_words, Wo_sc
             load_hid(UNITS * k, UNITS * (k + 1))
 
         def load_x(k):
-            x_t[k] = sb.tile([P, 2 * D], BF16, name="x", bufs=6, align_bytes=64)
+            x_t[k] = sb.tile([P, 2 * D], BF16, name="x", bufs=8, align_bytes=64)
             nc.sync.dma_start(out=x_t[k][:], in_=xin[k])
 
         def widen(lo, hi, tag, bufs, eng=nc.scalar.copy):
@@ -107,7 +107,7 @@ def tile_mopn_layer_pb_t_w4_kernel(tc, hid_bytes, hid_scale, Wd, Wo_words, Wo_sc
         def q_cols(lo, hi):
             k = lo // UNITS
             if k not in q_t:
-                q_t[k] = sb.tile([P, 2 * ROW], BF16, name="q", bufs=5, align_bytes=64)
+                q_t[k] = sb.tile([P, 2 * ROW], BF16, name="q", bufs=6, align_bytes=64)
             return q_t[k][:, H * (lo - UNITS * k) : H * (hi - UNITS * k)]
 
         def scale_v(lo, hi):
@@ -145,9 +145,9 @@ def tile_mopn_layer_pb_t_w4_kernel(tc, hid_bytes, hid_scale, Wd, Wo_words, Wo_sc
                     stop=True,
                 )
 
-        def round_j(i):
+        def round_j(i, eng=nc.scalar.copy):
             jb_t[i] = sb.tile([P, 2, P, 2], BF16, name="jb", bufs=4, align_bytes=64)
-            nc.scalar.copy(out=jb_t[i][:], in_=jp_t[i].rearrange("r (p u e) -> r u p e", u=2, e=2))
+            eng(out=jb_t[i][:], in_=jp_t[i].rearrange("r (p u e) -> r u p e", u=2, e=2))
 
         def turn_j(*tiles):
             jt_t[tiles] = bank("for_scalar")[:, : 2 * P * len(tiles)].rearrange("p (u i r) -> p u i r", u=2, r=P)
@@ -207,7 +207,7 @@ def tile_mopn_layer_pb_t_w4_kernel(tc, hid_bytes, hid_scale, Wd, Wo_words, Wo_sc
 
         def o_cols(i):
             if i // 2 not in o_t:
-                o_t[i // 2] = sb.tile([P, 2 * D], F32, name="o", bufs=5, align_bytes=64)
+                o_t[i // 2] = sb.tile([P, 2 * D], F32, name="o", bufs=6, align_bytes=64)
             return o_t[i // 2][:, (i % 2) * D : (i % 2 + 1) * D]
 
         def empty_sum(i):
@@ -306,8 +306,11 @@ def tile_mopn_layer_pb_t_w4_kernel(tc, hid_bytes, hid_scale, Wd, Wo_words, Wo_sc
             c = 4 * (m - 2)
             old, new = tuple(range(c, c + 4)), tuple(range(a, a + 4))
             slot = "slot%d" % ((m + 1) % 2)
-            todo = [u + 6, u + 8, u + 10, u + 12, u + 14, u + QUAD + 6] if m == 1 else [u + 8, u + 10, u + 12, u + 14, u + QUAD + 6]
-            if m + 2 < QUADS:
+            last = m == QUADS - 2
+            v = u + QUAD
+            todo = list(range(u + (6, 8, 10)[min(m, 3) - 1], v, 2)) + [v + 6] + [v + (12 if last else 8)] * (m > 1)
+            ahead = [v + 14] if last else [v + 8, v + 10] if m == 1 else [v + 10, v + 12]
+            if not last:
                 load_pair(2 * m + 4)
                 load_pair(2 * m + 5)
             load_x(2 * m - 2)
@@ -321,7 +324,12 @@ def tile_mopn_layer_pb_t_w4_kernel(tc, hid_bytes, hid_scale, Wd, Wo_words, Wo_sc
             scale_g(u + QUAD, u + QUAD + G_UNITS, "slot%d" % (m % 2))
             for lo in (u, u + 2, u + 4):
                 turn_g(lo)
-            turn_v(todo[1])
+            if m == 1:
+                turn_v(todo[1])
+            if m <= 2:
+                turn_v(todo[2])
+            if m > 2:
+                mix(c - 3)
             down(a)
             down(a + 1)
             round_j(a)
@@ -329,50 +337,61 @@ def tile_mopn_layer_pb_t_w4_kernel(tc, hid_bytes, hid_scale, Wd, Wo_words, Wo_sc
             if m > 1:
                 mix_t(c + 3)
                 empty_t(c + 3)
+            if m > 2:
+                mix(c - 2)
             down(a + 2)
             down(a + 3)
             round_j(a + 2)
-            round_j(a + 3)
-            if m > 1:
-                mix(c)
-            cut = u + QUAD + (10 if m + 2 < QUADS else 8)
-            widen(u + QUAD + G_UNITS, cut, "head", 4)
-            turn_v(todo[2])
             scale_v(todo[0], todo[0] + 2)
-            turn_v(todo[3])
-            scale_v(todo[1], todo[1] + 2)
-            joined(a, new, slot)
-            widen(cut if m + 2 < QUADS else cut + G_LAST, u + 2 * QUAD, "for_v", 2)
             if m > 1:
-                mix(c + 1)
-                add(c)
-            else:
-                turn_v(todo[4])
-            scale_v(todo[2], todo[2] + 2)
-            turn_v(todo[-1])
-            joined(a + 2, new, slot)
-            scale_v(todo[3], todo[3] + 2)
-            if m > 1:
-                add(c + 1)
-                store(c // 2)
-            else:
-                scale_v(todo[4], todo[4] + 2)
-            if m > 1:
-                mix(c + 2)
+                round_j(a + 3)
+                mix(c)
                 sum_t(c + 3)
-            if m + 1 < QUADS - 1:
-                turn_v(u + QUAD + 8)
+            scale_v(todo[1], todo[1] + 2)
+            if m > 2:
+                turn_v(todo[2])
+            if last:
+                widen(v + 6, v + 8, "head", 4)
+                widen(v + 11, v + QUAD, "for_v", 2)
             else:
-                turn_v(u + QUAD + 11, u + QUAD + 12)
-            if m + 2 < QUADS:
-                widen(u + 2 * QUAD, u + 2 * QUAD + G_UNITS, "for_g", 3)
-            else:
-                widen(cut, cut + G_LAST, "for_g", 3)
-            scale_v(todo[-1], todo[-1] + 2)
+                widen(v + 6, v + 10, "head", 4)
+                widen(v + 10, v + QUAD, "for_v", 2)
+            joined(a, new, slot)
             if m > 1:
                 empty_sum(c + 3)
-                add(c + 2)
-                store(c // 2 + 1)
+            if m > 2:
+                add(c - 3)
+                store(c // 2 - 2)
+            turn_v(todo[3])
+            if m == 1:
+                scale_v(todo[2], todo[2] + 2)
+                round_j(a + 3, nc.vector.tensor_copy)
+            joined(a + 2, new, slot)
+            if m > 2:
+                add(c - 2)
+                store(c // 2 - 1)
+            if m != 2:
+                turn_v(todo[4])
+            if m > 1:
+                add(c)
+            if m == 2:
+                turn_v(todo[4])
+            if m > 1:
+                scale_v(todo[2], todo[2] + 2)
+            later = todo[5:] + ahead
+            turn_v(later[0])
+            scale_v(todo[3], todo[3] + 2)
+            for lo in later[1:2]:
+                turn_v(lo)
+            if last:
+                widen(v + 8, v + 8 + G_LAST, "for_g", 3)
+            else:
+                widen(v + QUAD, v + QUAD + G_UNITS, "for_g", 3)
+            scale_v(todo[4], todo[4] + 2)
+            for lo in later[2:]:
+                turn_v(lo)
+            for lo in todo[5:]:
+                scale_v(lo, lo + 2)
 
         n = TILES
         u = QUAD * (QUADS - 1)
@@ -382,28 +401,36 @@ def tile_mopn_layer_pb_t_w4_kernel(tc, hid_bytes, hid_scale, Wd, Wo_words, Wo_sc
         quant_j(*range(n - 12, n - 8))
         quant(u - UNITS, u)
         scale_g(u + 8, u + 11, "slot1")
-        turn_v(u + 12)
+        turn_v(u + 11, u + 12)
         for lo in (u, u + 2, u + 4):
             turn_g(lo)
-        turn_v(u + 14)
+        mix(n - 15)
         down(n - 8)
         down(n - 7)
-        mix(n - 12)
         round_j(n - 8)
+        mix_t(n - 9)
         round_j(n - 7)
+        empty_t(n - 9)
+        mix(n - 14)
         down(n - 6)
         down(n - 5)
-        scale_v(u + 11, u + 12)
-        mix(n - 11)
         round_j(n - 6)
         round_j(n - 5)
+        scale_v(u + 14, u + 16)
+        mix(n - 12)
+        scale_v(u + 11, u + 12)
+        mix(n - 11)
         joined(n - 8, (n - 8, n - 7), "late0")
         joined(n - 6, (n - 6, n - 5), "late1")
-        scale_v(u + 12, u + 14)
-        scale_v(u + 14, u + 16)
+        add(n - 15)
+        store(PAIRS - 8)
         mix(n - 10)
-        mix(n - 9)
+        sum_t(n - 9)
         first = copy_aside(n - 10)
+        empty_sum(n - 9)
+        store(PAIRS - 5, D, D)
+        add(n - 14)
+        store(PAIRS - 7)
         add(n - 12)
         add(n - 11)
         store(PAIRS - 6)
@@ -415,41 +442,38 @@ def tile_mopn_layer_pb_t_w4_kernel(tc, hid_bytes, hid_scale, Wd, Wo_words, Wo_sc
         quant(u + 12, u + 16)
         quant_j(n - 6, n - 5)
         quant(u + 8, u + 12)
-        first = add_aside(n - 10, first, "late1")
         down(n - 4)
         mix(n - 8)
         down(n - 3)
         round_j(n - 4)
-        second = copy_aside(n - 9)
+        first = add_aside(n - 10, first, "late1")
         round_j(n - 3)
         mix(n - 7)
         down(n - 1)
+        mix(n - 6)
         turn_j(n - 4, n - 3)
         down(n - 2)
-        mix(n - 6)
-        mix(n - 5)
         round_j(n - 1)
         empty_j((n - 4, n - 3), (n - 4, n - 3), "late0")
         round_j(n - 2)
+        mix(n - 5)
         add_store(n - 8)
         add_store(n - 7)
         store_aside(n - 10, first)
         quant_j(n - 4, n - 3)
         turn_j(n - 1)
         empty_j((n - 1,), (n - 1,), "last1")
-        mix(n - 4)
         turn_j(n - 2)
         empty_j((n - 2,), (n - 2,), "last0")
+        mix(n - 4)
         mix(n - 3)
         add_store(n - 6)
         quant_j(n - 1)
         add_store(n - 5)
         quant_j(n - 2)
-        second = add_aside(n - 9, second, "last0")
         mix(n - 1)
         add_store(n - 4)
         mix(n - 2)
         add_store(n - 3)
-        store_aside(n - 9, second)
         add_store(n - 1)
         add_store(n - 2, 2)

@@ -428,12 +428,11 @@ def tile_mopn_layer_pb_t_w4_kernel(tc, hid_bytes, hid_scale, Wd, Wo_words, Wo_sc
         sum_t(n - 9)
         first = copy_aside(n - 10)
         empty_sum(n - 9)
-        store(PAIRS - 5, D, D)
         add(n - 14)
         store(PAIRS - 7)
-        add(n - 12)
-        add(n - 11)
-        store(PAIRS - 6)
+        add_store(n - 12)
+        add_store(n - 11)
+        store(PAIRS - 5, D, D)
         quant(u, u + NS)
         quant_j(n - 8, n - 7)
         quant(u + NS, u + UNITS)

@@ -13,6 +13,7 @@ F8X4 = mybir.dt.float8_e4m3fn_x4
 F4X4 = mybir.dt.float4_e2m1fn_x4
 MULT = mybir.AluOpType.mult
 ADD = mybir.AluOpType.add
+COPY = mybir.ActivationFunctionType.Copy
 
 P = 128
 TOKENS = 4096
@@ -122,6 +123,13 @@ def tile_mopn_layer_pb_t_w4_kernel(tc, hid_bytes, hid_scale, Wd, Wo_words, Wo_sc
 
         def empty_g(lo, hi):
             nc.scalar.copy(out=q_cols(lo, hi).bitcast(F32).rearrange("p (m u) -> p m u", u=2), in_=bank_t[lo].rearrange("p u a r -> p (a r) u"))
+
+        def scale_s(lo):
+            planes = sb.tile([P, 4, P], BF16, name="planes", bufs=1, align_bytes=64)
+            values = bank_t[lo].rearrange("p u a r -> p (u a r)").bitcast(BF16).rearrange("p (u m e) -> p u e m", u=2, e=2)
+            for t in range(4):
+                nc.scalar.activation(out=planes[:, t, :], in_=values[:, t // 2, t % 2, :], func=COPY, scale=scale_p[:, t : t + 1])
+            nc.scalar.copy(out=q_cols(lo, lo + 1).rearrange("p (m t) -> p m t", t=4), in_=planes[:].rearrange("p t m -> p m t"))
 
         def quant(lo, hi):
             codes = sb.tile([P, (hi - lo) * P], U32, name="codes", align_bytes=64)
@@ -259,7 +267,7 @@ def tile_mopn_layer_pb_t_w4_kernel(tc, hid_bytes, hid_scale, Wd, Wo_words, Wo_sc
         load_pair(1)
         nc.sync.dma_start(out=w_raw[:].rearrange("p n j d -> p n (j d)"), in_=Wd.rearrange("n (p j) d -> p n (j d)", j=4))
         make_identity(nc, ident[:])
-        nc.scalar.copy(out=ident_bf[:], in_=ident[:])
+        nc.scalar.activation(out=ident_bf[:], in_=ident[:], func=COPY)
         nc.vector.memset(wo_scales[:].bitcast(I32), 0)
         load_pair(3)
         load_pair(4)
@@ -330,6 +338,7 @@ def tile_mopn_layer_pb_t_w4_kernel(tc, hid_bytes, hid_scale, Wd, Wo_words, Wo_sc
                 turn_v(todo[2])
             if m > 2:
                 mix(c - 3)
+            widen(v + 6, v + (8 if last else 10), "head", 4)
             down(a)
             down(a + 1)
             round_j(a)
@@ -350,36 +359,38 @@ def tile_mopn_layer_pb_t_w4_kernel(tc, hid_bytes, hid_scale, Wd, Wo_words, Wo_sc
             scale_v(todo[1], todo[1] + 2)
             if m > 2:
                 turn_v(todo[2])
-            if last:
-                widen(v + 6, v + 8, "head", 4)
-                widen(v + 11, v + QUAD, "for_v", 2)
-            else:
-                widen(v + 6, v + 10, "head", 4)
-                widen(v + 10, v + QUAD, "for_v", 2)
+            widen(v + (11 if last else 10), v + QUAD, "for_v", 2)
+            if m == 1:
+                turn_v(todo[3])
+                turn_v(todo[4])
             joined(a, new, slot)
             if m > 1:
                 empty_sum(c + 3)
             if m > 2:
                 add(c - 3)
                 store(c // 2 - 2)
-            turn_v(todo[3])
-            if m == 1:
+            if m > 1:
+                turn_v(todo[3])
+            else:
                 scale_v(todo[2], todo[2] + 2)
+                turn_v(todo[5])
                 round_j(a + 3, nc.vector.tensor_copy)
             joined(a + 2, new, slot)
             if m > 2:
                 add(c - 2)
                 store(c // 2 - 1)
-            if m != 2:
+            if m > 2:
+                turn_v(todo[4])
+            if m == 2:
+                scale_v(todo[2], todo[2] + 2)
                 turn_v(todo[4])
             if m > 1:
                 add(c)
-            if m == 2:
-                turn_v(todo[4])
-            if m > 1:
+            if m > 2:
                 scale_v(todo[2], todo[2] + 2)
             later = todo[5:] + ahead
-            turn_v(later[0])
+            if m > 1:
+                turn_v(later[0])
             scale_v(todo[3], todo[3] + 2)
             for lo in later[1:2]:
                 turn_v(lo)
@@ -401,7 +412,8 @@ def tile_mopn_layer_pb_t_w4_kernel(tc, hid_bytes, hid_scale, Wd, Wo_words, Wo_sc
         quant_j(*range(n - 12, n - 8))
         quant(u - UNITS, u)
         scale_g(u + 8, u + 11, "slot1")
-        turn_v(u + 11, u + 12)
+        turn(u + 11, u + 12, "for_scalar")
+        scale_s(u + 11)
         for lo in (u, u + 2, u + 4):
             turn_g(lo)
         mix(n - 15)
@@ -418,7 +430,6 @@ def tile_mopn_layer_pb_t_w4_kernel(tc, hid_bytes, hid_scale, Wd, Wo_words, Wo_sc
         round_j(n - 5)
         scale_v(u + 14, u + 16)
         mix(n - 12)
-        scale_v(u + 11, u + 12)
         mix(n - 11)
         joined(n - 8, (n - 8, n - 7), "late0")
         joined(n - 6, (n - 6, n - 5), "late1")

@@ -21,7 +21,6 @@ NS = 4
 H = 512
 DS = 128
 D = NS * DS
-ROW = NS * H
 TILES = TOKENS // P
 PAIRS = TILES // 2
 UNITS = 2 * NS
@@ -29,6 +28,7 @@ QUAD = 2 * UNITS
 QUADS = PAIRS // 2
 G_UNITS = 6
 G_LAST = 3
+LEAD = 4
 FLOPS = 2 * TOKENS * NS * H * DS + 2 * TOKENS * D * D
 
 
@@ -108,7 +108,7 @@ def tile_mopn_layer_pb_t_w4_kernel(tc, hid_bytes, hid_scale, Wd, Wo_words, Wo_sc
         def q_cols(lo, hi):
             k = lo // UNITS
             if k not in q_t:
-                q_t[k] = sb.tile([P, 2 * ROW], BF16, name="q", bufs=6, align_bytes=64)
+                q_t[k] = sb.tile([P, UNITS * H], BF16, name="q", bufs=6, align_bytes=64)
             return q_t[k][:, H * (lo - UNITS * k) : H * (hi - UNITS * k)]
 
         def scale_v(lo, hi):
@@ -206,12 +206,11 @@ def tile_mopn_layer_pb_t_w4_kernel(tc, hid_bytes, hid_scale, Wd, Wo_words, Wo_sc
             rt_t[i] = sb.tile([P, D], F32, name="rt", bufs=2, align_bytes=64)
             nc.scalar.copy(out=rt_t[i][:], in_=pt_t[i])
 
-        def sum_t(i, tag="for_scalar"):
-            rt = rt_t[i]
-            pt_t[i] = bank(tag)
+        def sum_t(i):
+            pt_t[i] = bank("for_scalar")
             nc.tensor.matmul(out=pt_t[i], lhsT=ident_bf[:], rhs=x_t[i // 2][:, (i % 2) * D : (i % 2 + 1) * D], start=True, stop=False)
             for lo in range(0, D, P):
-                nc.tensor.matmul(out=pt_t[i][:, lo : lo + P], lhsT=rt[:, lo : lo + P], rhs=ident[:], is_transpose=True, start=False, stop=lo + P == D)
+                nc.tensor.matmul(out=pt_t[i][:, lo : lo + P], lhsT=rt_t[i][:, lo : lo + P], rhs=ident[:], is_transpose=True, start=False, stop=lo + P == D)
 
         def o_cols(i):
             if i // 2 not in o_t:
@@ -247,6 +246,9 @@ def tile_mopn_layer_pb_t_w4_kernel(tc, hid_bytes, hid_scale, Wd, Wo_words, Wo_sc
                 add(i, lo, w)
                 store(i // 2, (i % 2) * D + lo, w)
 
+        def scale_bank(lo):
+            scale_v(lo, lo + 2)
+
         def turn_v(lo, hi=None):
             turn(lo, hi or lo + 2, "for_vector")
 
@@ -258,12 +260,42 @@ def tile_mopn_layer_pb_t_w4_kernel(tc, hid_bytes, hid_scale, Wd, Wo_words, Wo_sc
             turn_j(i, i + 1)
             empty_j((i, i + 1), group, tag)
 
+        def widen_few(lo, hi, eng=nc.scalar.copy):
+            widen(lo, hi, "few", 4, eng)
+
+        def widen_v(lo, hi):
+            widen(lo, hi, "for_v", 2)
+
+        def widen_g(lo, hi):
+            widen(lo, hi, "for_g", 3)
+
+        def open_period(m):
+            u = QUAD * m
+            if m + 2 < QUADS:
+                load_pair(2 * m + 4)
+                load_pair(2 * m + 5)
+            load_x(2 * m - 2)
+            load_x(2 * m - 1)
+            quant(u - QUAD, u - UNITS)
+            if m == 1:
+                nc.vector.quantize_mx(out=w_codes[:].bitcast(F8X4), scales=w_scales[:], in_=w_grp[:].rearrange("p n d j -> p (n d j)"))
+            else:
+                quant_j(*quad_tiles(m - 2))
+            quant(u - UNITS, u)
+            scale_g(u + QUAD, u + QUAD + G_UNITS, "slot%d" % (m % 2))
+            for lo in range(u, u + G_UNITS, 2):
+                turn_g(lo)
+
+        def quad_tiles(m):
+            return tuple(range(4 * m, 4 * m + 4))
+
+        half = QUAD + G_UNITS // 2
         nc.sync.dma_start(out=scale_p[:], in_=srow.rearrange("(p t) -> p t", t=4))
         load_hid(0, 2)
-        load_hid(2, 4)
-        load_hid(QUAD, QUAD + 3)
-        load_hid(4, 8)
-        load_hid(QUAD + 3, QUAD + UNITS)
+        load_hid(2, NS)
+        load_hid(QUAD, half)
+        load_hid(NS, UNITS)
+        load_hid(half, QUAD + UNITS)
         load_pair(1)
         nc.sync.dma_start(out=w_raw[:].rearrange("p n j d -> p n (j d)"), in_=Wd.rearrange("n (p j) d -> p n (j d)", j=4))
         make_identity(nc, ident[:])
@@ -280,21 +312,21 @@ def tile_mopn_layer_pb_t_w4_kernel(tc, hid_bytes, hid_scale, Wd, Wo_words, Wo_sc
         spread = bank("for_scalar").rearrange("r (u e p) -> r u e p", u=2, e=2)
         for t in range(4):
             nc.tensor.transpose(spread[:, t // 2, t % 2, :], scale_p[:, t : t + 1].to_broadcast([P, P]), ident[:])
-        widen(0, 1, "head", 4, nc.vector.tensor_copy)
-        widen(1, 2, "head", 4, nc.vector.tensor_copy)
+        widen_few(0, 1, nc.vector.tensor_copy)
+        widen_few(1, 2, nc.vector.tensor_copy)
         nc.vector.tensor_copy(out=scale_row[:], in_=spread.rearrange("r u e p -> r u p e"))
-        widen(2, 4, "head", 4)
-        widen(QUAD, QUAD + 3, "for_g", 3)
-        scale_g(QUAD, QUAD + 3, "slot0")
-        widen(4, 6, "head", 4)
+        widen_few(2, 4)
+        widen_g(QUAD, half)
+        scale_g(QUAD, half, "slot0")
+        widen_few(4, 6)
         for lo, hi in [(0, 1), (1, 2), (2, 4)]:
             turn_v(lo, hi)
             scale_v(lo, hi)
-        widen(6, 8, "head", 4)
-        widen(QUAD + 3, QUAD + G_UNITS, "for_g", 3)
-        scale_g(QUAD + 3, QUAD + G_UNITS, "late0")
-        widen(8, 10, "head", 4)
-        widen(10, QUAD, "for_v", 2)
+        widen_few(6, 8)
+        widen_g(half, QUAD + G_UNITS)
+        scale_g(half, QUAD + G_UNITS, "late0")
+        widen_few(8, 10)
+        widen_v(10, QUAD)
         w_grp = ring.tile([P, NS, DS, 4], BF16, name="slot1", align_bytes=64)
         nc.scalar.copy(
             out=w_grp[:].rearrange("p n (c i) j -> p n c j i", i=4),
@@ -302,119 +334,138 @@ def tile_mopn_layer_pb_t_w4_kernel(tc, hid_bytes, hid_scale, Wd, Wo_words, Wo_sc
         )
         for lo in range(4, QUAD, 2):
             turn_v(lo)
-            scale_v(lo, lo + 2)
-        widen(QUAD + G_UNITS, QUAD + 10, "head", 4)
-        widen(2 * QUAD, 2 * QUAD + G_UNITS, "for_g", 3)
-        widen(QUAD + 10, 2 * QUAD, "for_v", 2)
-        turn_v(QUAD + 6)
+            scale_bank(lo)
+        mine = QUAD + G_UNITS
+        widen_few(mine, mine + LEAD)
+        widen_g(2 * QUAD, 2 * QUAD + G_UNITS)
+        widen_v(mine + LEAD, 2 * QUAD)
+        turn_v(mine)
 
-        for m in range(1, QUADS - 1):
-            u = QUAD * m
-            a = 4 * (m - 1)
-            c = 4 * (m - 2)
-            old, new = tuple(range(c, c + 4)), tuple(range(a, a + 4))
-            slot = "slot%d" % ((m + 1) % 2)
+        nxt = mine + QUAD
+        banks = list(range(mine, 2 * QUAD, 2)) + [nxt]
+        open_period(1)
+        turn_v(banks[1])
+        turn_v(banks[2])
+        widen_few(nxt, nxt + LEAD)
+        down(0)
+        down(1)
+        round_j(0)
+        round_j(1)
+        down(2)
+        down(3)
+        round_j(2)
+        scale_bank(banks[0])
+        scale_bank(banks[1])
+        widen_v(nxt + LEAD, 3 * QUAD)
+        turn_v(banks[3])
+        turn_v(banks[4])
+        joined(0, quad_tiles(0), "slot0")
+        scale_bank(banks[2])
+        turn_v(banks[5])
+        round_j(3, nc.vector.tensor_copy)
+        joined(2, quad_tiles(0), "slot0")
+        scale_bank(banks[3])
+        turn_v(nxt + 2)
+        widen_g(3 * QUAD, 3 * QUAD + G_UNITS)
+        scale_bank(banks[4])
+        turn_v(nxt + 4)
+        scale_bank(banks[5])
+
+        mine, nxt = nxt, nxt + QUAD
+        banks = list(range(mine + 2, 3 * QUAD, 2)) + [nxt, nxt + 2]
+        open_period(2)
+        turn_v(banks[2])
+        widen_few(nxt, nxt + LEAD)
+        down(4)
+        down(5)
+        round_j(4)
+        round_j(5)
+        mix_t(3)
+        empty_t(3)
+        down(6)
+        down(7)
+        round_j(6)
+        scale_bank(banks[0])
+        round_j(7)
+        mix(0)
+        sum_t(3)
+        scale_bank(banks[1])
+        widen_v(nxt + LEAD, 4 * QUAD)
+        turn_v(banks[3])
+        turn_v(banks[4])
+        joined(4, quad_tiles(1), "slot1")
+        empty_sum(3)
+        joined(6, quad_tiles(1), "slot1")
+        scale_bank(banks[2])
+        add(0)
+        turn_v(banks[5])
+        scale_bank(banks[3])
+        turn_v(nxt + LEAD)
+        widen_g(4 * QUAD, 4 * QUAD + G_UNITS)
+        scale_bank(banks[4])
+        turn_v(nxt + LEAD + 2)
+        scale_bank(banks[5])
+
+        tail = QUAD * (QUADS - 1) + UNITS
+        alone = tail + G_LAST
+        for m in range(3, QUADS - 1):
+            a, c = 4 * (m - 1), 4 * (m - 2)
             last = m == QUADS - 2
-            v = u + QUAD
-            todo = list(range(u + (6, 8, 10)[min(m, 3) - 1], v, 2)) + [v + 6] + [v + (12 if last else 8)] * (m > 1)
-            ahead = [v + 14] if last else [v + 8, v + 10] if m == 1 else [v + 10, v + 12]
-            if not last:
-                load_pair(2 * m + 4)
-                load_pair(2 * m + 5)
-            load_x(2 * m - 2)
-            load_x(2 * m - 1)
-            quant(u - QUAD, u - UNITS)
-            if m == 1:
-                nc.vector.quantize_mx(out=w_codes[:].bitcast(F8X4), scales=w_scales[:], in_=w_grp[:].rearrange("p n d j -> p (n d j)"))
-            else:
-                quant_j(*old)
-            quant(u - UNITS, u)
-            scale_g(u + QUAD, u + QUAD + G_UNITS, "slot%d" % (m % 2))
-            for lo in (u, u + 2, u + 4):
-                turn_g(lo)
-            if m == 1:
-                turn_v(todo[1])
-            if m <= 2:
-                turn_v(todo[2])
-            if m > 2:
-                mix(c - 3)
-            widen(v + 6, v + (8 if last else 10), "head", 4)
+            slot = "slot%d" % ((m + 1) % 2)
+            end = QUAD * (m + 1)
+            nxt = end + G_UNITS
+            banks = list(range(nxt - QUAD + LEAD, end, 2)) + [nxt, alone + 1 if last else nxt + 2]
+            open_period(m)
+            mix(c - 3)
+            widen_few(nxt, tail if last else nxt + LEAD)
             down(a)
             down(a + 1)
             round_j(a)
             round_j(a + 1)
-            if m > 1:
-                mix_t(c + 3)
-                empty_t(c + 3)
-            if m > 2:
-                mix(c - 2)
+            mix_t(c + 3)
+            empty_t(c + 3)
+            mix(c - 2)
             down(a + 2)
             down(a + 3)
             round_j(a + 2)
-            scale_v(todo[0], todo[0] + 2)
-            if m > 1:
-                round_j(a + 3)
-                mix(c)
-                sum_t(c + 3)
-            scale_v(todo[1], todo[1] + 2)
-            if m > 2:
-                turn_v(todo[2])
-            widen(v + (11 if last else 10), v + QUAD, "for_v", 2)
-            if m == 1:
-                turn_v(todo[3])
-                turn_v(todo[4])
-            joined(a, new, slot)
-            if m > 1:
-                empty_sum(c + 3)
-            if m > 2:
-                add(c - 3)
-                store(c // 2 - 2)
-            if m > 1:
-                turn_v(todo[3])
-            else:
-                scale_v(todo[2], todo[2] + 2)
-                turn_v(todo[5])
-                round_j(a + 3, nc.vector.tensor_copy)
-            joined(a + 2, new, slot)
-            if m > 2:
-                add(c - 2)
-                store(c // 2 - 1)
-            if m > 2:
-                turn_v(todo[4])
-            if m == 2:
-                scale_v(todo[2], todo[2] + 2)
-                turn_v(todo[4])
-            if m > 1:
-                add(c)
-            if m > 2:
-                scale_v(todo[2], todo[2] + 2)
-            later = todo[5:] + ahead
-            if m > 1:
-                turn_v(later[0])
-            scale_v(todo[3], todo[3] + 2)
-            for lo in later[1:2]:
-                turn_v(lo)
+            scale_bank(banks[0])
+            round_j(a + 3)
+            mix(c)
+            sum_t(c + 3)
+            scale_bank(banks[1])
+            turn_v(banks[2])
+            widen_v(alone if last else nxt + LEAD, end + QUAD)
+            joined(a, quad_tiles(m - 1), slot)
+            empty_sum(c + 3)
+            add(c - 3)
+            store(c // 2 - 2)
+            turn_v(banks[3])
+            joined(a + 2, quad_tiles(m - 1), slot)
+            add(c - 2)
+            store(c // 2 - 1)
+            turn_v(banks[4])
+            add(c)
+            scale_bank(banks[2])
+            turn_v(banks[4] + 2)
+            scale_bank(banks[3])
             if last:
-                widen(v + 8, v + 8 + G_LAST, "for_g", 3)
+                widen_g(tail, alone)
             else:
-                widen(v + QUAD, v + QUAD + G_UNITS, "for_g", 3)
-            scale_v(todo[4], todo[4] + 2)
-            for lo in later[2:]:
-                turn_v(lo)
-            for lo in todo[5:]:
-                scale_v(lo, lo + 2)
+                turn_v(banks[4] + 4)
+                widen_g(end + QUAD, end + QUAD + G_UNITS)
+            scale_bank(banks[4])
 
         n = TILES
-        u = QUAD * (QUADS - 1)
+        u = tail - UNITS
         for k in range(PAIRS - 4, PAIRS):
             load_x(k)
         quant(u - QUAD, u - UNITS)
-        quant_j(*range(n - 12, n - 8))
+        quant_j(*quad_tiles(QUADS - 3))
         quant(u - UNITS, u)
-        scale_g(u + 8, u + 11, "slot1")
-        turn(u + 11, u + 12, "for_scalar")
-        scale_s(u + 11)
-        for lo in (u, u + 2, u + 4):
+        scale_g(tail, alone, "slot1")
+        turn(alone, alone + 1, "for_scalar")
+        scale_s(alone)
+        for lo in range(u, u + G_UNITS, 2):
             turn_g(lo)
         mix(n - 15)
         down(n - 8)
@@ -428,7 +479,7 @@ def tile_mopn_layer_pb_t_w4_kernel(tc, hid_bytes, hid_scale, Wd, Wo_words, Wo_sc
         down(n - 5)
         round_j(n - 6)
         round_j(n - 5)
-        scale_v(u + 14, u + 16)
+        scale_bank(alone + 3)
         mix(n - 12)
         mix(n - 11)
         joined(n - 8, (n - 8, n - 7), "late0")
@@ -437,26 +488,27 @@ def tile_mopn_layer_pb_t_w4_kernel(tc, hid_bytes, hid_scale, Wd, Wo_words, Wo_sc
         store(PAIRS - 8)
         mix(n - 10)
         sum_t(n - 9)
-        first = copy_aside(n - 10)
+        aside = copy_aside(n - 10)
         empty_sum(n - 9)
         add(n - 14)
         store(PAIRS - 7)
         add_store(n - 12)
         add_store(n - 11)
         store(PAIRS - 5, D, D)
+
         quant(u, u + NS)
         quant_j(n - 8, n - 7)
-        quant(u + NS, u + UNITS)
-        turn_g(u + 8)
-        turn_g(u + 10, u + 11)
-        quant(u + 12, u + 16)
+        quant(u + NS, tail)
+        turn_g(tail)
+        turn_g(tail + 2, alone)
+        quant(tail + NS, tail + UNITS)
         quant_j(n - 6, n - 5)
-        quant(u + 8, u + 12)
+        quant(tail, tail + NS)
         down(n - 4)
         mix(n - 8)
         down(n - 3)
         round_j(n - 4)
-        first = add_aside(n - 10, first, "late1")
+        aside = add_aside(n - 10, aside, "late1")
         round_j(n - 3)
         mix(n - 7)
         down(n - 1)
@@ -469,7 +521,8 @@ def tile_mopn_layer_pb_t_w4_kernel(tc, hid_bytes, hid_scale, Wd, Wo_words, Wo_sc
         mix(n - 5)
         add_store(n - 8)
         add_store(n - 7)
-        store_aside(n - 10, first)
+        store_aside(n - 10, aside)
+        add_store(n - 6)
         quant_j(n - 4, n - 3)
         turn_j(n - 1)
         empty_j((n - 1,), (n - 1,), "last1")
@@ -477,9 +530,8 @@ def tile_mopn_layer_pb_t_w4_kernel(tc, hid_bytes, hid_scale, Wd, Wo_words, Wo_sc
         empty_j((n - 2,), (n - 2,), "last0")
         mix(n - 4)
         mix(n - 3)
-        add_store(n - 6)
-        quant_j(n - 1)
         add_store(n - 5)
+        quant_j(n - 1)
         quant_j(n - 2)
         mix(n - 1)
         add_store(n - 4)

@@ -83,6 +83,15 @@ def tile_mopn_layer_pb_t_w4_kernel(tc, hid_bytes, hid_scale, Wd, Wo_words, Wo_sc
                 wide[u] = tile[:, H * (u - lo) : H * (u - lo + 1)]
                 run_t[u] = (tile, lo)
 
+        def widen_words(lo, hi, tag, bufs):
+            n = hi - lo
+            tile = sb.tile([P, 2, n * P, 2], BF16, name=tag, bufs=bufs, align_bytes=64)
+            src = hb_t[lo // QUAD][:, H * (lo % QUAD) : H * (lo % QUAD + n)].bitcast(F8)
+            nc.scalar.copy(out=tile[:], in_=src.rearrange("r (m u e) -> r u m e", u=2, e=2))
+            words = tile[:].rearrange("r u m e -> r u (m e)").bitcast(F32)
+            for u in range(lo, hi):
+                done[u] = [words[:, h, P * (u - lo) : P * (u - lo + 1)] for h in range(2)]
+
         def scale_g(lo, hi, slot):
             n = hi - lo
             tile, first = run_t[lo]
@@ -260,11 +269,11 @@ def tile_mopn_layer_pb_t_w4_kernel(tc, hid_bytes, hid_scale, Wd, Wo_words, Wo_sc
             turn_j(i, i + 1)
             empty_j((i, i + 1), group, tag)
 
-        def widen_few(lo, hi, eng=nc.scalar.copy):
-            widen(lo, hi, "few", 4, eng)
+        def widen_few(lo, hi):
+            widen_words(lo, hi, "few", 4)
 
         def widen_v(lo, hi):
-            widen(lo, hi, "for_v", 2)
+            widen_words(lo, hi, "for_v", 2)
 
         def widen_g(lo, hi):
             widen(lo, hi, "for_g", 3)
@@ -312,8 +321,8 @@ def tile_mopn_layer_pb_t_w4_kernel(tc, hid_bytes, hid_scale, Wd, Wo_words, Wo_sc
         spread = bank("for_scalar").rearrange("r (u e p) -> r u e p", u=2, e=2)
         for t in range(4):
             nc.tensor.transpose(spread[:, t // 2, t % 2, :], scale_p[:, t : t + 1].to_broadcast([P, P]), ident[:])
-        widen_few(0, 1, nc.vector.tensor_copy)
-        widen_few(1, 2, nc.vector.tensor_copy)
+        widen(0, 1, "few", 4, nc.vector.tensor_copy)
+        widen(1, 2, "few", 4, nc.vector.tensor_copy)
         nc.vector.tensor_copy(out=scale_row[:], in_=spread.rearrange("r u e p -> r u p e"))
         widen_few(2, 4)
         widen_g(QUAD, half)

@@ -299,9 +299,9 @@ def tile_mopn_layer_pb_t_w4_kernel(tc, hid_bytes, hid_scale, Wd, Wo_words, Wo_sc
             return tuple(range(4 * m, 4 * m + 4))
 
         half = QUAD + G_UNITS // 2
+        load_hid(0, 1)
         nc.sync.dma_start(out=scale_p[:], in_=srow.rearrange("(p t) -> p t", t=4))
-        load_hid(0, 2)
-        load_hid(2, NS)
+        load_hid(1, NS)
         load_hid(QUAD, half)
         load_hid(NS, UNITS)
         load_hid(half, QUAD + UNITS)

from contextlib import ExitStack

import concourse.mybir as mybir
from concourse.masks import make_identity

F32 = mybir.dt.float32
BF16 = mybir.dt.bfloat16
U32 = mybir.dt.uint32
I32 = mybir.dt.int32
U8 = mybir.dt.uint8
F8 = mybir.dt.float8_e4m3fn
F8X4 = mybir.dt.float8_e4m3fn_x4
F4X4 = mybir.dt.float4_e2m1fn_x4
MULT = mybir.AluOpType.mult
ADD = mybir.AluOpType.add
COPY = mybir.ActivationFunctionType.Copy

P = 128
TOKENS = 4096
NS = 4
H = 512
DS = 128
D = NS * DS
TILES = TOKENS // P
PAIRS = TILES // 2
UNITS = 2 * NS
QUAD = 2 * UNITS
QUADS = PAIRS // 2
G_UNITS = 6
G_LAST = 3
LEAD = 4
FLOPS = 2 * TOKENS * NS * H * DS + 2 * TOKENS * D * D


def tile_mopn_layer_pb_t_w4_kernel(tc, hid_bytes, hid_scale, Wd, Wo_words, Wo_scales, x, out):
    nc = tc.nc
    hid = hid_bytes.rearrange("b s n k -> (b s) (n k)").rearrange("(j p i) c -> j p (i c)", p=P, i=2)
    xin = x.rearrange("b s d -> (b s) d").rearrange("(j p i) c -> j p (i c)", p=P, i=2)
    oview = out.rearrange("b s d -> (b s) d").rearrange("(j p i) c -> j p (i c)", p=P, i=2)
    srow = hid_scale.rearrange("a b c k -> (a b c k)")

    with ExitStack() as ctx:
        keep = ctx.enter_context(tc.tile_pool(name="keep", bufs=1))
        sb = ctx.enter_context(tc.tile_pool(name="sb", bufs=3))
        ring = ctx.enter_context(tc.tile_pool(name="ring", bufs=1))
        ps = ctx.enter_context(tc.psum_pool(name="ps", bufs=4))
        ctx.enter_context(tc.manual_schedule())

        scale_p = keep.tile([P, 4], F32, align_bytes=64)
        scale_row = keep.tile([P, 2, P, 2], F32, align_bytes=64)
        ident = keep.tile([P, P], F32, align_bytes=64)
        ident_bf = keep.tile([P, P], BF16, align_bytes=64)
        w_raw = keep.tile([P, NS, 4, DS], BF16, align_bytes=64)
        w_codes = keep.tile([P, D], U32, align_bytes=64)
        w_scales = keep.tile([P, D], U8, align_bytes=64)
        wo_words = keep.tile([P, 2 * D], U8, align_bytes=64)
        wo_scales = keep.tile([P, D], U8, align_bytes=64)

        hb_t, x_t, wide, run_t, done, bank_t, q_t, c_t, s_t = ({} for z in range(9))
        jp_t, jb_t, jt_t, jg_t, jc_t, js_t, po_t, pt_t, rt_t, o_t = ({} for z in range(10))

        def bank(tag):
            tile = ps.tile([P, D], F32, name=tag)
            return tile[:]

        def load_hid(lo, hi):
            m, k = lo // QUAD, lo // UNITS
            if m not in hb_t:
                hb_t[m] = sb.tile([P, QUAD * H], U8, name="hb", bufs=4, align_bytes=64)
            nc.sync.dma_start(out=hb_t[m][:, H * (lo - QUAD * m) : H * (hi - QUAD * m)], in_=hid[k][:, H * (lo - UNITS * k) : H * (hi - UNITS * k)])

        def load_pair(k):
            load_hid(UNITS * k, UNITS * (k + 1))

        def load_x(k):
            x_t[k] = sb.tile([P, 2 * D], BF16, name="x", bufs=8, align_bytes=64)
            nc.sync.dma_start(out=x_t[k][:], in_=xin[k])

        def widen(lo, hi, tag, bufs, eng=nc.scalar.copy):
            tile = sb.tile([P, (hi - lo) * H], BF16, name=tag, bufs=bufs, align_bytes=64)
            eng(out=tile[:], in_=hb_t[lo // QUAD][:, H * (lo % QUAD) : H * (lo % QUAD + hi - lo)].bitcast(F8))
            for u in range(lo, hi):
                wide[u] = tile[:, H * (u - lo) : H * (u - lo + 1)]
                run_t[u] = (tile, lo)

        def widen_words(lo, hi, tag, bufs):
            n = hi - lo
            tile = sb.tile([P, 2, n * P, 2], BF16, name=tag, bufs=bufs, align_bytes=64)
            src = hb_t[lo // QUAD][:, H * (lo % QUAD) : H * (lo % QUAD + n)].bitcast(F8)
            nc.scalar.copy(out=tile[:], in_=src.rearrange("r (m u e) -> r u m e", u=2, e=2))
            words = tile[:].rearrange("r u m e -> r u (m e)").bitcast(F32)
            for u in range(lo, hi):
                done[u] = [words[:, h, P * (u - lo) : P * (u - lo + 1)] for h in range(2)]

        def scale_g(lo, hi, slot):
            n = hi - lo
            tile, first = run_t[lo]
            gs = ring.tile([P, 2, n, P, 2], BF16, name=slot, align_bytes=64)
            nc.gpsimd.tensor_tensor(
                out=gs[:],
                in0=tile[:, H * (lo - first) : H * (hi - first)].rearrange("r (n p u e) -> r u n p e", p=P, u=2, e=2),
                in1=scale_row[:].unsqueeze(2).to_broadcast([P, 2, n, P, 2]),
                op=MULT,
            )
            words = gs[:].rearrange("r u n p e -> r u n (p e)").bitcast(F32)
            for u in range(lo, hi):
                done[u] = [words[:, h, u - lo, :] for h in range(2)]

        def turn(lo, hi, tag):
            dst = bank(tag)[:, : 2 * P * (hi - lo)].rearrange("p (u a r) -> p u a r", u=2, r=P)
            bank_t[lo] = dst
            for a in range(hi - lo):
                for h in range(2):
                    src = done[lo + a][h] if lo + a in done else wide[lo + a].bitcast(F32)[:, h::2]
                    nc.tensor.transpose(dst[:, h, a, :], src, ident[:])

        def q_cols(lo, hi):
            k = lo // UNITS
            if k not in q_t:
                q_t[k] = sb.tile([P, UNITS * H], BF16, name="q", bufs=6, align_bytes=64)
            return q_t[k][:, H * (lo - UNITS * k) : H * (hi - UNITS * k)]

        def scale_v(lo, hi):
            m = (hi - lo) * P
            pairs = bank_t[lo].rearrange("p u a r -> p (u a r)").bitcast(BF16).rearrange("p (u m e) -> p m u e", u=2, e=2)
            nc.vector.tensor_tensor(
                out=q_cols(lo, hi).rearrange("p (m u e) -> p m u e", u=2, e=2),
                in0=pairs,
                in1=scale_p[:].rearrange("p (u e) -> p u e", u=2).unsqueeze(1).to_broadcast([P, m, 2, 2]),
                op=MULT,
            )

        def empty_g(lo, hi):
            nc.scalar.copy(out=q_cols(lo, hi).bitcast(F32).rearrange("p (m u) -> p m u", u=2), in_=bank_t[lo].rearrange("p u a r -> p (a r) u"))

        def scale_s(lo):
            planes = sb.tile([P, 4, P], BF16, name="planes", bufs=1, align_bytes=64)
            values = bank_t[lo].rearrange("p u a r -> p (u a r)").bitcast(BF16).rearrange("p (u m e) -> p u e m", u=2, e=2)
            for t in range(4):
                nc.scalar.activation(out=planes[:, t, :], in_=values[:, t // 2, t % 2, :], func=COPY, scale=scale_p[:, t : t + 1])
            nc.scalar.copy(out=q_cols(lo, lo + 1).rearrange("p (m t) -> p m t", t=4), in_=planes[:].rearrange("p t m -> p m t"))

        def quant(lo, hi):
            codes = sb.tile([P, (hi - lo) * P], U32, name="codes", align_bytes=64)
            scales = sb.tile([P, (hi - lo) * P], U8, name="scales", align_bytes=64)
            nc.vector.quantize_mx(out=codes[:].bitcast(F8X4), scales=scales[:], in_=q_cols(lo, hi))
            for u in range(lo, hi):
                cols = slice(P * (u - lo), P * (u - lo + 1))
                c_t[u], s_t[u] = codes[:, cols], scales[:, cols]

        def down(i):
            jp_t[i] = bank("for_scalar")
            for n in range(NS):
                cols = slice(P * n, P * (n + 1))
                nc.tensor.matmul_mx(
                    out=jp_t[i][:, cols],
                    lhsT=c_t[NS * i + n].bitcast(F8X4),
                    lhsT_scale=s_t[NS * i + n],
                    rhs=w_codes[:, cols].bitcast(F8X4),
                    rhs_scale=w_scales[:, cols],
                    start=True,
                    stop=True,
                )

        def round_j(i, eng=nc.scalar.copy):
            jb_t[i] = sb.tile([P, 2, P, 2], BF16, name="jb", bufs=4, align_bytes=64)
            eng(out=jb_t[i][:], in_=jp_t[i].rearrange("r (p u e) -> r u p e", u=2, e=2))

        def turn_j(*tiles):
            jt_t[tiles] = bank("for_scalar")[:, : 2 * P * len(tiles)].rearrange("p (u i r) -> p u i r", u=2, r=P)
            for z, i in enumerate(tiles):
                words = jb_t[i][:].rearrange("r u p e -> r (u p e)").bitcast(F32)
                for u in range(2):
                    nc.tensor.transpose(jt_t[tiles][:, u, z, :], words[:, P * u : P * (u + 1)], ident[:])

        def empty_j(tiles, group, tag):
            if group not in jg_t:
                jg_t[group] = ring.tile([P, len(group) * P, 2], F32, name=tag, align_bytes=64)
            lo = P * group.index(tiles[0])
            nc.scalar.copy(out=jg_t[group][:, lo : lo + P * len(tiles), :], in_=jt_t[tiles].rearrange("p u i r -> p (i r) u"))

        def quant_j(*tiles):
            codes = sb.tile([P, len(tiles) * P], U32, name="jcodes", bufs=4, align_bytes=64)
            scales = sb.tile([P, len(tiles) * P], U8, name="jscales", bufs=4, align_bytes=64)
            nc.vector.quantize_mx(out=codes[:].bitcast(F8X4), scales=scales[:], in_=jg_t[tiles][:].rearrange("p r u -> p (r u)").bitcast(BF16))
            for z, i in enumerate(tiles):
                jc_t[i], js_t[i] = codes[:, P * z : P * (z + 1)], scales[:, P * z : P * (z + 1)]

        def mix(i):
            po_t[i] = bank("for_vector")
            nc.tensor.matmul_mx(
                out=po_t[i],
                lhsT=jc_t[i].bitcast(F8X4),
                lhsT_scale=js_t[i],
                rhs=wo_words[:].bitcast(F4X4),
                rhs_scale=wo_scales[:],
                start=True,
                stop=True,
            )

        def mix_t(i):
            pt_t[i] = bank("for_scalar")
            for lo in range(0, D, P):
                nc.tensor.matmul_mx(
                    out=pt_t[i][:, lo : lo + P],
                    lhsT=wo_words[:, 2 * lo : 2 * (lo + P)].bitcast(F4X4),
                    lhsT_scale=wo_scales[:, lo : lo + P],
                    rhs=jc_t[i].bitcast(F8X4),
                    rhs_scale=js_t[i],
                    start=True,
                    stop=True,
                )

        def empty_t(i):
            rt_t[i] = sb.tile([P, D], F32, name="rt", bufs=2, align_bytes=64)
            nc.scalar.copy(out=rt_t[i][:], in_=pt_t[i])

        def sum_t(i):
            pt_t[i] = bank("for_scalar")
            nc.tensor.matmul(out=pt_t[i], lhsT=ident_bf[:], rhs=x_t[i // 2][:, (i % 2) * D : (i % 2 + 1) * D], start=True, stop=False)
            for lo in range(0, D, P):
                nc.tensor.matmul(out=pt_t[i][:, lo : lo + P], lhsT=rt_t[i][:, lo : lo + P], rhs=ident[:], is_transpose=True, start=False, stop=lo + P == D)

        def o_cols(i):
            if i // 2 not in o_t:
                o_t[i // 2] = sb.tile([P, 2 * D], F32, name="o", bufs=6, align_bytes=64)
            return o_t[i // 2][:, (i % 2) * D : (i % 2 + 1) * D]

        def empty_sum(i):
            nc.scalar.copy(out=o_cols(i), in_=pt_t[i])

        def add(i, lo=0, w=D):
            cols = slice((i % 2) * D + lo, (i % 2) * D + lo + w)
            nc.vector.tensor_tensor(out=o_cols(i)[:, lo : lo + w], in0=po_t[i][:, lo : lo + w], in1=x_t[i // 2][:, cols], op=ADD)

        def copy_aside(i):
            res = sb.tile([P, D], F32, name="rt", bufs=2, align_bytes=64)
            nc.scalar.copy(out=res[:], in_=po_t[i])
            return res

        def add_aside(i, res, tag):
            sums = ring.tile([P, D], F32, name=tag, align_bytes=64)
            nc.gpsimd.tensor_tensor(out=sums[:], in0=res[:], in1=x_t[i // 2][:, (i % 2) * D : (i % 2 + 1) * D], op=ADD)
            return sums

        def store_aside(i, sums):
            nc.sync.dma_start(out=oview[i // 2][:, (i % 2) * D : (i % 2 + 1) * D], in_=sums[:])

        def store(k, lo=0, w=2 * D):
            nc.sync.dma_start(out=oview[k][:, lo : lo + w], in_=o_t[k][:, lo : lo + w])

        def add_store(i, parts=1):
            w = D // parts
            for lo in range(0, D, w):
                add(i, lo, w)
                store(i // 2, (i % 2) * D + lo, w)

        def scale_bank(lo):
            scale_v(lo, lo + 2)

        def turn_v(lo, hi=None):
            turn(lo, hi or lo + 2, "for_vector")

        def turn_g(lo, hi=None):
            turn(lo, hi or lo + 2, "for_scalar")
            empty_g(lo, hi or lo + 2)

        def joined(i, group, tag):
            turn_j(i, i + 1)
            empty_j((i, i + 1), group, tag)

        def widen_few(lo, hi):
            widen_words(lo, hi, "few", 4)

        def widen_v(lo, hi):
            widen_words(lo, hi, "for_v", 2)

        def widen_g(lo, hi):
            widen(lo, hi, "for_g", 3)

        def open_period(m):
            u = QUAD * m
            if m + 2 < QUADS:
                load_pair(2 * m + 4)
                load_pair(2 * m + 5)
            load_x(2 * m - 2)
            load_x(2 * m - 1)
            quant(u - QUAD, u - UNITS)
            if m == 1:
                nc.vector.quantize_mx(out=w_codes[:].bitcast(F8X4), scales=w_scales[:], in_=w_grp[:].rearrange("p n d j -> p (n d j)"))
            else:
                quant_j(*quad_tiles(m - 2))
            quant(u - UNITS, u)
            scale_g(u + QUAD, u + QUAD + G_UNITS, "slot%d" % (m % 2))
            for lo in range(u, u + G_UNITS, 2):
                turn_g(lo)

        def quad_tiles(m):
            return tuple(range(4 * m, 4 * m + 4))

        half = QUAD + G_UNITS // 2
        load_hid(0, 1)
        nc.sync.dma_start(out=scale_p[:], in_=srow.rearrange("(p t) -> p t", t=4))
        load_hid(1, NS)
        load_hid(QUAD, half)
        load_hid(NS, UNITS)
        load_hid(half, QUAD + UNITS)
        load_pair(1)
        nc.sync.dma_start(out=w_raw[:].rearrange("p n j d -> p n (j d)"), in_=Wd.rearrange("n (p j) d -> p n (j d)", j=4))
        make_identity(nc, ident[:])
        nc.scalar.activation(out=ident_bf[:], in_=ident[:], func=COPY)
        nc.vector.memset(wo_scales[:].bitcast(I32), 0)
        load_pair(3)
        load_pair(4)
        nc.sync.dma_start(out=wo_words[:], in_=Wo_words[0])
        wos = Wo_scales[0].bitcast(I32)
        for q in range(4):
            nc.sync.dma_start(out=wo_scales[32 * q : 32 * q + 4, :].bitcast(I32), in_=wos[4 * q : 4 * q + 4, :])
        load_pair(5)

        spread = bank("for_scalar").rearrange("r (u e p) -> r u e p", u=2, e=2)
        for t in range(4):
            nc.tensor.transpose(spread[:, t // 2, t % 2, :], scale_p[:, t : t + 1].to_broadcast([P, P]), ident[:])
        widen(0, 1, "few", 4, nc.vector.tensor_copy)
        widen(1, 2, "few", 4, nc.vector.tensor_copy)
        nc.vector.tensor_copy(out=scale_row[:], in_=spread.rearrange("r u e p -> r u p e"))
        widen_few(2, 4)
        widen_g(QUAD, half)
        scale_g(QUAD, half, "slot0")
        widen_few(4, 6)
        for lo, hi in [(0, 1), (1, 2), (2, 4)]:
            turn_v(lo, hi)
            scale_v(lo, hi)
        widen_few(6, 8)
        widen_g(half, QUAD + G_UNITS)
        scale_g(half, QUAD + G_UNITS, "late0")
        widen_few(8, 10)
        widen_v(10, QUAD)
        w_grp = ring.tile([P, NS, DS, 4], BF16, name="slot1", align_bytes=64)
        nc.scalar.copy(
            out=w_grp[:].rearrange("p n (c i) j -> p n c j i", i=4),
            in_=w_raw[:].rearrange("p n j (c i) -> p n c j i", i=4),
        )
        for lo in range(4, QUAD, 2):
            turn_v(lo)
            scale_bank(lo)
        mine = QUAD + G_UNITS
        widen_few(mine, mine + LEAD)
        widen_g(2 * QUAD, 2 * QUAD + G_UNITS)
        widen_v(mine + LEAD, 2 * QUAD)
        turn_v(mine)

        nxt = mine + QUAD
        banks = list(range(mine, 2 * QUAD, 2)) + [nxt]
        open_period(1)
        turn_v(banks[1])
        turn_v(banks[2])
        widen_few(nxt, nxt + LEAD)
        down(0)
        down(1)
        round_j(0)
        round_j(1)
        down(2)
        down(3)
        round_j(2)
        scale_bank(banks[0])
        scale_bank(banks[1])
        widen_v(nxt + LEAD, 3 * QUAD)
        turn_v(banks[3])
        turn_v(banks[4])
        joined(0, quad_tiles(0), "slot0")
        scale_bank(banks[2])
        turn_v(banks[5])
        round_j(3, nc.vector.tensor_copy)
        joined(2, quad_tiles(0), "slot0")
        scale_bank(banks[3])
        turn_v(nxt + 2)
        widen_g(3 * QUAD, 3 * QUAD + G_UNITS)
        scale_bank(banks[4])
        turn_v(nxt + 4)
        scale_bank(banks[5])

        mine, nxt = nxt, nxt + QUAD
        banks = list(range(mine + 2, 3 * QUAD, 2)) + [nxt, nxt + 2]
        open_period(2)
        turn_v(banks[2])
        widen_few(nxt, nxt + LEAD)
        down(4)
        down(5)
        round_j(4)
        round_j(5)
        mix_t(3)
        empty_t(3)
        down(6)
        down(7)
        round_j(6)
        scale_bank(banks[0])
        round_j(7)
        mix(0)
        sum_t(3)
        scale_bank(banks[1])
        widen_v(nxt + LEAD, 4 * QUAD)
        turn_v(banks[3])
        turn_v(banks[4])
        joined(4, quad_tiles(1), "slot1")
        empty_sum(3)
        joined(6, quad_tiles(1), "slot1")
        scale_bank(banks[2])
        add(0)
        turn_v(banks[5])
        scale_bank(banks[3])
        turn_v(nxt + LEAD)
        widen_g(4 * QUAD, 4 * QUAD + G_UNITS)
        scale_bank(banks[4])
        turn_v(nxt + LEAD + 2)
        scale_bank(banks[5])

        tail = QUAD * (QUADS - 1) + UNITS
        alone = tail + G_LAST
        for m in range(3, QUADS - 1):
            a, c = 4 * (m - 1), 4 * (m - 2)
            last = m == QUADS - 2
            slot = "slot%d" % ((m + 1) % 2)
            end = QUAD * (m + 1)
            nxt = end + G_UNITS
            banks = list(range(nxt - QUAD + LEAD, end, 2)) + [nxt, alone + 1 if last else nxt + 2]
            open_period(m)
            mix(c - 3)
            widen_few(nxt, tail if last else nxt + LEAD)
            down(a)
            down(a + 1)
            round_j(a)
            round_j(a + 1)
            mix_t(c + 3)
            empty_t(c + 3)
            mix(c - 2)
            down(a + 2)
            down(a + 3)
            round_j(a + 2)
            scale_bank(banks[0])
            round_j(a + 3)
            mix(c)
            sum_t(c + 3)
            scale_bank(banks[1])
            turn_v(banks[2])
            widen_v(alone if last else nxt + LEAD, end + QUAD)
            joined(a, quad_tiles(m - 1), slot)
            empty_sum(c + 3)
            add(c - 3)
            store(c // 2 - 2)
            turn_v(banks[3])
            joined(a + 2, quad_tiles(m - 1), slot)
            add(c - 2)
            store(c // 2 - 1)
            turn_v(banks[4])
            add(c)
            scale_bank(banks[2])
            turn_v(banks[4] + 2)
            scale_bank(banks[3])
            if last:
                widen_g(tail, alone)
            else:
                turn_v(banks[4] + 4)
                widen_g(end + QUAD, end + QUAD + G_UNITS)
            scale_bank(banks[4])

        n = TILES
        u = tail - UNITS
        for k in range(PAIRS - 4, PAIRS):
            load_x(k)
        quant(u - QUAD, u - UNITS)
        quant_j(*quad_tiles(QUADS - 3))
        quant(u - UNITS, u)
        scale_g(tail, alone, "slot1")
        turn(alone, alone + 1, "for_scalar")
        scale_s(alone)
        for lo in range(u, u + G_UNITS, 2):
            turn_g(lo)
        mix(n - 15)
        down(n - 8)
        down(n - 7)
        round_j(n - 8)
        mix_t(n - 9)
        round_j(n - 7)
        empty_t(n - 9)
        mix(n - 14)
        down(n - 6)
        down(n - 5)
        round_j(n - 6)
        round_j(n - 5)
        scale_bank(alone + 3)
        mix(n - 12)
        mix(n - 11)
        joined(n - 8, (n - 8, n - 7), "late0")
        joined(n - 6, (n - 6, n - 5), "late1")
        add(n - 15)
        store(PAIRS - 8)
        mix(n - 10)
        sum_t(n - 9)
        aside = copy_aside(n - 10)
        empty_sum(n - 9)
        add(n - 14)
        store(PAIRS - 7)
        add_store(n - 12)
        add_store(n - 11)
        store(PAIRS - 5, D, D)

        quant(u, u + NS)
        quant_j(n - 8, n - 7)
        quant(u + NS, tail)
        turn_g(tail)
        turn_g(tail + 2, alone)
        quant(tail + NS, tail + UNITS)
        quant_j(n - 6, n - 5)
        quant(tail, tail + NS)
        down(n - 4)
        mix(n - 8)
        down(n - 3)
        round_j(n - 4)
        aside = add_aside(n - 10, aside, "late1")
        round_j(n - 3)
        mix(n - 7)
        down(n - 1)
        mix(n - 6)
        turn_j(n - 4, n - 3)
        down(n - 2)
        round_j(n - 1)
        empty_j((n - 4, n - 3), (n - 4, n - 3), "late0")
        round_j(n - 2)
        mix(n - 5)
        add_store(n - 8)
        add_store(n - 7)
        store_aside(n - 10, aside)
        add_store(n - 6)
        quant_j(n - 4, n - 3)
        turn_j(n - 1)
        empty_j((n - 1,), (n - 1,), "last1")
        turn_j(n - 2)
        empty_j((n - 2,), (n - 2,), "last0")
        mix(n - 4)
        mix(n - 3)
        add_store(n - 5)
        quant_j(n - 1)
        quant_j(n - 2)
        mix(n - 1)
        add_store(n - 4)
        mix(n - 2)
        add_store(n - 3)
        add_store(n - 1)
        add_store(n - 2, 2)
